import numpy as np
import ml_dtypes


def mxq(x, axis, fmt="e4m3"):
    dtype, down = {"e4m3": (ml_dtypes.float8_e4m3fn, 7), "e5m2": (ml_dtypes.float8_e5m2, 14)}[fmt]
    v = np.moveaxis(np.asarray(x, np.float32).astype(ml_dtypes.bfloat16).astype(np.float64), axis, -1)
    blocks = v.reshape(v.shape[:-1] + (-1, 32))
    amax = np.abs(blocks).max(-1, keepdims=True)
    byte = np.maximum(np.where(amax > 0, np.frexp(amax)[1] - 1 + 127, 0) - down, 1)
    scale = np.exp2(byte - 127.0)
    codes = (blocks / scale).astype(np.float32).astype(dtype).astype(np.float64)
    return np.moveaxis((codes * scale).reshape(v.shape), -1, axis)


WIDE = False


def mx_kscale(k):
    if not WIDE:
        return np.ones(k)
    levels = np.array([18, -18])
    if k % 512:
        return np.exp2(np.random.permutation(np.resize(levels, k // 32))).repeat(32)
    a = np.empty((k // 512, 16))
    for p in range(k // 512):
        a[p, :8] = np.random.permutation(np.resize(levels, 8))
        for g in range(8):
            far = levels[np.abs(levels - a[p, g]) >= 10]
            a[p, g + 8] = far[np.random.randint(len(far))]
    return np.exp2(a.ravel()).repeat(32)


BF16 = ml_dtypes.bfloat16


def bf(x):
    return np.asarray(x, np.float32).astype(BF16)


def f64(x):
    return np.asarray(x).astype(np.float64)


N, IN, HID, OUT, NB = 1536, 512, 1024, 256, 64
EPS = 1e-8


def draw_adj():
    r = np.exp(0.5 * np.random.standard_normal(N))
    u = np.random.uniform(size=(N, N)) * (np.random.uniform(size=(N, N)) < NB / N)
    return u * r[:, None] * r[None, :]


def setup_inputs():
    s = mx_kscale(N)[:, None]
    u = mx_kscale(HID)
    v = mx_kscale(IN)
    x0 = bf(np.random.standard_normal((N, IN)) * 0.25 * np.sqrt(NB))
    adj0 = bf(draw_adj())
    W1_0 = bf(np.random.standard_normal((HID, IN)) * 3.0 / np.sqrt(IN))
    b1 = bf(np.random.standard_normal(HID) * 0.3)
    g = bf(4.0 * np.random.standard_normal((N, HID)) * np.exp2(np.random.randint(-6, 1, (N, 1))) / s * u[None, :])
    a = f64(adj0)
    rdeg = 1.0 / np.sqrt(a.sum(axis=1) + EPS)
    agg = (rdeg[:, None] * a * rdeg[None, :]) @ f64(x0)
    z = agg @ f64(W1_0).T + f64(b1)
    return {"x": bf(f64(x0) / v[None, :]),
            "adj": bf(f64(adj0) * s),
            "W1": bf(f64(W1_0) * v[None, :] / u[:, None]),
            "b1": b1,
            "z": np.asarray(z, np.float32),
            "rdeg": np.asarray(rdeg, np.float32),
            "grad_out": g}


def reference(x, adj, W1, b1, z, rdeg, grad_out):
    a = f64(adj)
    d = f64(rdeg)
    dz2 = f64(grad_out) * (f64(z) > 0.0)
    dagg = mxq(dz2, 1, "e5m2") @ mxq(f64(W1), 0, "e4m3")
    dz1 = dagg * d[:, None]
    dx = d[:, None] * (mxq(a, 0, "e4m3").T @ mxq(dz1, 0, "e5m2"))
    P = mxq(dz1, 1, "e5m2") @ mxq(f64(x), 1, "e4m3").T
    t = a * P
    rows = (t * d[None, :]).sum(axis=1)
    cols = t.sum(axis=0)
    q = -0.5 * d ** 2 * rows - 0.5 * d ** 3 * cols
    dadj = P * d[None, :] + q[:, None]
    return dx, dadj

@@ -1,0 +1,468 @@
+from contextlib import ExitStack
+
+import concourse.mybir as mybir
+from concourse.masks import make_identity
+
+N, IN, HID = 1536, 512, 1024
+P = 128
+G = 3
+S = 4
+B = 6
+E = 2
+W = 512
+
+FLOPS = 2 * N * HID * IN + 2 * 2 * N * N * IN
+BYTES = 2 * (N * IN + N * N + HID * IN + N * HID) + 4 * (N * HID + N) + 4 * (N * IN + N * N)
+
+F32 = mybir.dt.float32
+BF16 = mybir.dt.bfloat16
+U32 = mybir.dt.uint32
+U8 = mybir.dt.uint8
+E4M3 = mybir.dt.float8_e4m3fn_x4
+E5M2 = mybir.dt.float8_e5m2_x4
+ALU = mybir.AluOpType
+ACT = mybir.ActivationFunctionType
+AX = mybir.AxisListType
+
+
+PRM = {"m": [4.83, 6.1, 7.23, 8.61, 12.77, 14.02, 15.25, 16.36, 18.71, 22.13, 23.11, 25.37], "u0": 22.4, "du0": 1.11, "du1": 0.27, "hsw": 18, "x": 8.2, "xt": 11.51, "dx": 1.37, "adj": [16.83, 21.39, 17.93], "nc": [26.19, 28.97, 33.34], "lag": {"tr2": 0.93, "cp2": 1.39, "qz2": 2.11, "mxd": 2.78, "cpd": 3.21, "tr1": 3.68, "cp1": 4.23, "qz1": 6.53, "adj": 1.5, "mx": 1.62, "act": 1.21}}
+
+
+def valid(p):
+    m, L = p["m"], p["lag"]
+    u = []
+    t = p["u0"]
+    for h in range(18):
+        u.append(t)
+        t += p["du0"] if h < p["hsw"] else p["du1"]
+    o = []
+    for n in range(12):
+        ch = [0, L["tr2"], L["cp2"], L["qz2"], L["mxd"], L["cpd"], L["tr1"], L["cp1"]]
+        o += [a < b for a, b in zip(ch, ch[1:])]
+        if n + 1 < 12:
+            o.append(m[n] + L["cp2"] < m[n + 1] + L["tr2"])
+            o.append(m[n] + L["cpd"] < m[n + 1] + L["mxd"])
+        if n + 2 < 12:
+            o.append(m[n] + L["tr2"] < m[n + 2])
+            o.append(m[n] + L["qz2"] < m[n + 2] + L["cp2"])
+            o.append(m[n] + L["mxd"] < m[n + 2] + L["qz2"])
+            o.append(m[n] + L["cp1"] < m[n + 2] + L["tr1"])
+    o.append(L["qz1"] > L["cp1"])
+    o.append(m[11] + L["qz1"] > u[5] - L["mx"])
+    for g in range(3):
+        f = m[4 * g + 3] + L["qz1"]
+        if g < 2:
+            o.append(f < m[4 * g + 4] + L["cp1"])
+        o.append(f < u[6 * g] - L["mx"])
+        o.append(p["adj"][g] < u[6 * g] - L["adj"])
+        if g < 2:
+            o.append(m[4 * g + 3] + L["cpd"] < p["nc"][g] < 45 and p["nc"][g] > 6)
+    xe = p["xt"] + 5 * p["dx"] + 1.2
+    o.append(xe < u[0] - L["mx"] and xe < u[0] - L["adj"])
+    o.append(p["x"] + 0.3 < p["xt"] and p["dx"] > 0.35)
+    for h in range(18):
+        if h >= 2:
+            o.append(u[h - 2] + 0 < u[h] - L["mx"])
+        if h >= 11 or h < 11:
+            if h >= 1 and (h < 11 or h >= 15):
+                o.append(u[h - 1] - L["act"] + 0.45 < u[h] - L["mx"])
+        if h >= 3:
+            o.append(u[h - 3] + 0.5 < u[h] - L["adj"])
+        o.append(L["mx"] > L["act"] > 0.5)
+    o.append(m[11] + L["cp1"] < u[11] - L["mx"] and m[11] + L["cp1"] < u[7])
+    return all(o)
+
+
+def tile_simplegcn_pa_v_kernel(tc, x, adj, W1, b1, z, rdeg, grad_out, out_0, out_1):
+    nc = tc.nc
+    x_v = x.rearrange("(b p e) f -> p b e f", b=B, e=E)
+    adj_v = adj.rearrange("(g p s) w -> p g s w", g=G, s=S)
+    w1_v = W1.rearrange("(c p j) f -> p c j f", c=2, j=4)
+    z_v = z.rearrange("(g p s) k -> p g s k", g=G, s=S)
+    go_v = grad_out.rearrange("(g p s) k -> p g s k", g=G, s=S)
+    d_v = rdeg.rearrange("(g p s) -> p g s", g=G, s=S)
+    d2_v = rdeg.rearrange("(b p e) -> p b e", b=B, e=E)
+    o0_v = out_0.rearrange("(g p s) f -> p g s f", g=G, s=S)
+    o1_v = out_1.rearrange("(g p s) w -> p g s w", g=G, s=S)
+    NZ = 3
+    W_CUT = (IN, IN // 4)
+    NS = G * S
+    NF = G * B
+    GADD = NF - 4
+    V0 = 26
+    MX0 = 5
+    FREE = 11
+
+    with ExitStack() as ctx:
+        keep = ctx.enter_context(tc.tile_pool(name="keep", bufs=1))
+        over = ctx.enter_context(tc.tile_pool(name="over", bufs=1))
+        psum = ctx.enter_context(tc.psum_pool(name="psum", bufs=1))
+        ctx.enter_context(tc.manual_schedule())
+
+        def sb(name, cols, dtype, offset=None):
+            if offset is None:
+                return keep.tile([P] + cols, dtype, name=name, align_bytes=64)
+            return over.tile([P] + cols, dtype, name=name, align_bytes=64, offset=offset)
+
+        ident = sb("ident", [P], F32)
+        perm = sb("perm", [2, 2, P], F32)
+        d_sb = sb("d_sb", [NS], F32)
+        d2_sb = sb("d2_sb", [B * E], F32)
+        mh = sb("mh", [NS], F32)
+        csum = sb("csum", [2, G * E], F32)
+        cacc = sb("cacc", [2, G, E, G], F32)
+        rsum = sb("rsum", [NS], F32)
+        junk = sb("junk", [P], F32)
+        q_sb = sb("q_sb", [NS], F32)
+        adj_sb = sb("adj_sb", [G, S, N], BF16)
+        st = [[sb(f"st{g}{b}", [E, W], F32) for b in range(B)] for g in range(G)]
+        dz1 = [sb(f"dz1_{g}", [S, IN], BF16) for g in range(G)]
+        w_codes = sb("w_codes", [2 * IN], U32)
+        w_scales = sb("w_scales", [2 * IN], U8)
+        x_codes = [sb(f"x_codes{i}", [W], U32) for i in range(3)]
+        x_scales = [sb(f"x_scales{i}", [W], U8) for i in range(3)]
+        f_codes = [sb(f"f_codes{i}", [W], U32) for i in range(2)]
+        f_scales = [sb(f"f_scales{i}", [W], U8) for i in range(2)]
+        buf4 = [sb(f"buf4_{i}", [HID], F32) for i in range(NZ)]
+        d1t = sb("d1t", [S * IN], BF16)
+
+        wil = [sb(f"wil{i}", [4 * IN], BF16, 4096 * i) for i in range(2)]
+        RX = 8192
+        xraw = sb("xraw", [B, E, IN], BF16, RX)
+        wraw = sb("wraw", [2, 4, IN], BF16, RX + 12288)
+        xt = [sb(f"xt{i}", [4 * IN], BF16, RX + 20480 + 4096 * i) for i in range(2)]
+        nq = [sb(f"nq{g}", [W], U32, RX + 12288 + 2048 * g) for g in range(G)]
+        nqs = [sb(f"nqs{g}", [W], U8, RX + 18432 + 512 * g) for g in range(G)]
+        aq = [[sb(f"aq{g}{h}", [W], U32, RX + 2048 * (3 * g + h) + (8192 if 3 * g + h >= 6 else 0)) for h in range(G)] for g in range(G)]
+        aqs = [[sb(f"aqs{g}{h}", [W], U8, RX + 26624 + 512 * (3 * g + h)) for h in range(G)] for g in range(G)]
+        RB = RX + 31232
+        T2A = 9
+        T2N = 12
+        t2 = [sb(f"t2_{i}", [W], F32, RB + 2048 * i) for i in range(T2N)]
+        ot = [sb(f"ot{i}", [N], F32, RB + 6144 * i) for i in range(4)]
+        RC = RB + 2048 * T2N
+        gt = [sb(f"gt{i}", [HID], BF16, RC + 2048 * i) for i in range(NZ)]
+        dz2 = [sb(f"dz2_{i}", [2, HID // 2], BF16, RC + 6144 + 2048 * i) for i in range(2)]
+        d2t = [sb(f"d2t{i}", [HID], BF16, RC + 10240 + 2048 * i) for i in range(2)]
+        d2q = [sb(f"d2q{i}", [2 * P], U32, RC + 14336 + 1024 * i) for i in range(2)]
+        d2s = [sb(f"d2s{i}", [2 * P], U8, RC + 16384 + 256 * i) for i in range(2)]
+        o0 = [sb(f"o0_{i}", [S, IN], F32, RC + 8192 * i) for i in range(2)]
+
+        bank = [psum.tile([P, W], F32, name=f"bank{i}") for i in range(8)]
+        TPB, DAB, T1B, XB = bank[0], bank[1], bank[4], [bank[5], bank[6], bank[7], bank[2], bank[3]]
+        RB4 = [bank[0], bank[1], bank[4], bank[7]]
+        LAST = NF - 3
+
+        def pt_of(i):
+            return bank[0:2] if (i % 2 and FREE <= i < LAST) else bank[2:4]
+
+        def at_of(i):
+            return bank[5 + i % 3] if i < LAST else bank[5 + i % 2]
+
+        def load_slot(n):
+            nc.sync.dma_start(out=buf4[n % NZ][:], in_=z_v[:, n // S, n % S, :])
+            nc.sync.dma_start(out=gt[n % NZ][:], in_=go_v[:, n // S, n % S, :])
+
+        def load_adj(g):
+            for s in range(S):
+                nc.sync.dma_start(out=adj_sb[:, g, s, :], in_=adj_v[:, g, s, :])
+
+        def load_x(i):
+            nc.sync.dma_start(out=xraw[:, 2 * i:2 * i + 2, :, :], in_=x_v[:, 2 * i:2 * i + 2, :, :])
+
+        def w_copy(c):
+            for lo, hi, eng in ((0, W_CUT[c], nc.vector.tensor_copy), (W_CUT[c], IN, nc.scalar.copy)):
+                if lo < hi:
+                    eng(out=wil[c][:, 4 * lo:4 * hi].rearrange("p (f j) -> p f j", j=4), in_=wraw[:, c, :, lo:hi].rearrange("p j f -> p f j"))
+
+        def w_quant(c):
+            nc.vector.quantize_mx(out=w_codes[:, c * IN:(c + 1) * IN].bitcast(E4M3), scales=w_scales[:, c * IN:(c + 1) * IN], in_=wil[c][:])
+
+        def x_half(b):
+            bk = XB[b % 5]
+            ps = bk[:].rearrange("p (e u t) -> p e u t", e=2, u=2)
+            for e in range(2):
+                words = xraw[:, b, e, :].bitcast(F32)
+                for u in range(2):
+                    nc.tensor.transpose(ps[:, e, u, :], words[:, u::2], ident[:])
+
+        def x_copy(b):
+            ps = XB[b % 5][:].rearrange("p (e u t) -> p e u t", e=2, u=2)
+            dst = xt[b // 2 % 2][:, (b % 2) * 1024:(b % 2 + 1) * 1024].bitcast(F32).rearrange("p (e t u) -> p e t u", e=2, u=2)
+            nc.scalar.copy(out=dst, in_=ps.rearrange("p e u t -> p e t u"))
+
+        def x_quant(i):
+            nc.vector.quantize_mx(out=x_codes[i][:].bitcast(E4M3), scales=x_scales[i][:], in_=xt[i % 2][:])
+
+        def mask(n):
+            if not 0 <= n < NS:
+                return
+            zt, g_, o = buf4[n % NZ], gt[n % NZ], dz2[n % 2]
+            for u in range(2):
+                nc.vector.scalar_tensor_tensor(
+                    out=o[:, u, :].rearrange("p (q e) -> p q e", e=2),
+                    in0=zt[:].rearrange("p (q u e) -> p u q e", u=2, e=2)[:, u, :, :],
+                    scalar=0.0,
+                    in1=g_[:].rearrange("p (q u e) -> p u q e", u=2, e=2)[:, u, :, :],
+                    op0=ALU.is_gt, op1=ALU.mult)
+
+        def tr2(n):
+            if not 0 <= n < NS:
+                return
+            words = dz2[n % 2][:].rearrange("p u k -> p (u k)").bitcast(F32)
+            ps = TPB[:].rearrange("p (c u t) -> p c u t", c=2, u=2)
+            for c in range(2):
+                for u in range(2):
+                    nc.tensor.transpose(ps[:, c, u, :], words[:, u * 256 + c * P:u * 256 + (c + 1) * P], ident[:])
+
+        def cp2(n):
+            ps = TPB[:].rearrange("p (c u t) -> p c u t", c=2, u=2)
+            nc.scalar.copy(out=d2t[n % 2][:].bitcast(F32).rearrange("p (c t u) -> p c t u", c=2, u=2), in_=ps.rearrange("p c u t -> p c t u"))
+
+        def qz2(n):
+            if not 0 <= n < NS:
+                return
+            nc.vector.quantize_mx(out=d2q[n % 2][:].bitcast(E5M2), scales=d2s[n % 2][:], in_=d2t[n % 2][:])
+
+        def mxd(n):
+            if not 0 <= n < NS:
+                return
+            for c in range(2):
+                nc.tensor.matmul_mx(out=DAB[:], lhsT=d2q[n % 2][:, c * P:(c + 1) * P].bitcast(E5M2), lhsT_scale=d2s[n % 2][:, c * P:(c + 1) * P],
+                                    rhs=w_codes[:, c * IN:(c + 1) * IN].bitcast(E4M3), rhs_scale=w_scales[:, c * IN:(c + 1) * IN],
+                                    start=(c == 0), stop=(c == 1))
+
+        def cpd(n):
+            nc.scalar.activation(out=dz1[n // S][:, n % S, :].rearrange("p (u q e) -> p u q e", u=2, e=2),
+                                 in_=DAB[:].rearrange("p (q u e) -> p u q e", u=2, e=2), func=ACT.Copy, scale=d_sb[:, n:n + 1])
+
+        def tr1(n):
+            if not 0 <= n < NS:
+                return
+            words = dz1[n // S][:, n % S, :].bitcast(F32)
+            ps = T1B[:, (n % 2) * 256:(n % 2 + 1) * 256].rearrange("p (u t) -> p u t", u=2)
+            for u in range(2):
+                nc.tensor.transpose(ps[:, u, :], words[:, u * P:(u + 1) * P], ident[:])
+
+        def cp1(n):
+            ps = T1B[:, (n % 2) * 256:(n % 2 + 1) * 256].rearrange("p (u t) -> p u t", u=2)
+            dst = d1t[:, (n % S) * IN:(n % S + 1) * IN].bitcast(F32).rearrange("p (t u) -> p t u", u=2)
+            nc.scalar.copy(out=dst, in_=ps.rearrange("p u t -> p t u"))
+
+        def qz1(g):
+            nc.vector.quantize_mx(out=f_codes[g % 2][:].bitcast(E5M2), scales=f_scales[g % 2][:], in_=d1t[:])
+
+        def front(i):
+            if not 0 <= i < NF:
+                return
+            g, b = i // B, i % B
+            for e in range(E):
+                c0 = ((b % 2) * E + e) * P
+                nc.tensor.matmul_mx(out=pt_of(i)[e][:], lhsT=x_codes[b // 2][:, c0:c0 + P].bitcast(E4M3), lhsT_scale=x_scales[b // 2][:, c0:c0 + P],
+                                    rhs=f_codes[g % 2][:].bitcast(E5M2), rhs_scale=f_scales[g % 2][:], start=True, stop=True)
+
+        def act(i, e):
+            g, b = i // B, i % B
+            if True:
+                nc.scalar.activation(out=st[g][b][:, e, :], in_=pt_of(i)[e][:], func=ACT.Copy, scale=d2_sb[:, b * E + e:b * E + e + 1])
+
+        def adj_t(i):
+            if not 0 <= i < NF:
+                return
+            g, b = i // B, i % B
+            for s in range(S):
+                words = adj_sb[:, g, s, b * 256:(b + 1) * 256].bitcast(F32)
+                nc.tensor.transpose(at_of(i)[:, s * P:(s + 1) * P], words, ident[:])
+
+
+        def t2_of(i, e):
+            return (t2[i % T2A] if e == 0 else t2[T2A + i % (T2N - T2A)])[:]
+
+        def stt(i, e):
+            g, b = i // B, i % B
+            at = at_of(i)[:].bitcast(BF16).rearrange("p (t e) -> p e t", e=E)
+            nc.vector.scalar_tensor_tensor(out=t2_of(i, e), in0=at[:, e, :], scalar=1.0, in1=st[g][b][:, e, :],
+                                           op0=ALU.mult, op1=ALU.mult, accum_out=cacc[:, b % 2, b // 2, e, g:g + 1])
+
+        def gadd(i):
+            nc.gpsimd.tensor_tensor(out=t2_of(i, 0), in0=t2_of(i, 0), in1=t2_of(i, 1), op=ALU.add)
+
+        pend = {i: [t2_of(i, 0)] if i < GADD else [t2_of(i, 0), t2_of(i, 1)] for i in range(NF)}
+
+        def row_half(g, r):
+            bk = bank[4]
+            tiles = [t for i in range(g * B, (g + 1) * B) for t in pend[i]]
+            for s in (2 * r, 2 * r + 1):
+                for j, t in enumerate(tiles):
+                    nc.tensor.matmul(out=bk[:, s * P:(s + 1) * P], lhsT=t[:, s * P:(s + 1) * P], rhs=ident[:], start=(j == 0), stop=(j == len(tiles) - 1), is_transpose=True)
+
+        def row_red(g):
+            for s in range(S):
+                nc.scalar.activation(out=junk[:], in_=bank[4][:, s * P:(s + 1) * P], func=ACT.Copy, accum_out=rsum[:, g * S + s:g * S + s + 1])
+
+        def row_last(i):
+            for j, t in enumerate(pend[i]):
+                for s in range(S):
+                    nc.tensor.matmul(out=RB4[s][:, :P], lhsT=t[:, s * P:(s + 1) * P], rhs=ident[:], start=(i % B == 0 and j == 0), stop=(i == NF - 1 and j == len(pend[i]) - 1), is_transpose=True)
+
+        def n_prep_copy(g):
+            o, i = wil[g % 2][:].rearrange("p (f s) -> p f s", s=S), dz1[g][:].rearrange("p s f -> p f s")
+            if g < 2:
+                nc.gpsimd.tensor_scalar(out=o, in0=i, scalar1=1.0, scalar2=1.0, op0=ALU.mult, op1=ALU.mult)
+            else:
+                nc.vector.tensor_copy(out=o, in_=i)
+
+        def n_prep_quant(g):
+            t = wil[g % 2][:]
+            nc.vector.quantize_mx(out=nq[g][:].bitcast(E5M2), scales=nqs[g][:], in_=t)
+
+        def a_buf(i):
+            return buf4[i % NZ][:].bitcast(BF16)
+
+        def a_prep_copy(i):
+            g, h = i % G, i // G
+            nc.vector.tensor_copy(out=a_buf(i).rearrange("p (a b s) -> p a b s", a=S, s=S), in_=adj_sb[:, g, :, h * W:(h + 1) * W].rearrange("p s (b a) -> p a b s", a=S))
+
+        def a_prep_quant(i):
+            g, h = i % G, i // G
+            nc.vector.quantize_mx(out=aq[g][h][:].bitcast(E4M3), scales=aqs[g][h][:], in_=a_buf(i))
+
+        def mxo(h, s):
+            bk = bank[s % 3]
+            for g in range(G):
+                nc.tensor.matmul_mx(out=bk[:], lhsT=aq[g][h][:, s * P:(s + 1) * P].bitcast(E4M3), lhsT_scale=aqs[g][h][:, s * P:(s + 1) * P],
+                                    rhs=nq[g][:].bitcast(E5M2), rhs_scale=nqs[g][:], start=(g == 0), stop=(g == G - 1))
+            o = o0[h % 2][:, s, :].rearrange("p (q u e) -> p q u e", u=2, e=2)
+            i = bk[:].rearrange("p (u q e) -> p q u e", u=2, e=2)
+            sc = d_sb[:, S * h + s:S * h + s + 1]
+            if not (h == 2 and s % 2):
+                nc.scalar.activation(out=o, in_=i, func=ACT.Copy, scale=sc)
+            else:
+                nc.vector.tensor_scalar(out=o, in0=i, scalar1=sc, scalar2=None, op0=ALU.mult)
+            if s == S - 1:
+                nc.sync.dma_start(out=o0_v[:, h, :, :], in_=o0[h % 2][:])
+
+        ob = [0]
+
+        def o1row(n):
+            g, s = n // S, n % S
+            t = ot[n % 4]
+            for h in range(G):
+                bk = bank[3 + ob[0] % 5]
+                for k in range(4):
+                    nc.tensor.transpose(bk[:, k * P:(k + 1) * P], st[g][2 * h + k // 2][:, k % 2, s * P:(s + 1) * P], ident[:])
+                o = t[:, h * W:(h + 1) * W].rearrange("p (c b a) -> p c b a", c=2, a=2)
+                i = bk[:].rearrange("p (c a b) -> p c b a", c=2, a=2)
+                if not ((ob[0] >= V0 and ob[0] % 2) or ob[0] == 1):
+                    nc.scalar.activation(out=o, in_=i, func=ACT.Identity, bias=q_sb[:, n:n + 1])
+                else:
+                    nc.vector.tensor_scalar(out=o, in0=i, scalar1=q_sb[:, n:n + 1], scalar2=None, op0=ALU.add)
+                ob[0] += 1
+                if n == 0:
+                    nc.sync.dma_start(out=o1_v[:, g, s, h * W:(h + 1) * W], in_=t[:, h * W:(h + 1) * W])
+            if n:
+                nc.sync.dma_start(out=o1_v[:, g, s, :], in_=t[:])
+
+        def mh_step():
+            nc.vector.scalar_tensor_tensor(out=mh[:], in0=d_sb[:], scalar=-0.5, in1=d_sb[:], op0=ALU.mult, op1=ALU.mult)
+
+        for c in range(2):
+            nc.sync.dma_start(out=wraw[:, c, :, :], in_=w1_v[:, c, :, :])
+        load_slot(0)
+        nc.scalar.dma_start(out=d_sb[:].rearrange("p (g s) -> p g s", g=G), in_=d_v)
+        nc.scalar.dma_start(out=d2_sb[:].rearrange("p (b e) -> p b e", b=B), in_=d2_v)
+        load_slot(1)
+        make_identity(nc, ident[:])
+        nc.gpsimd.memset(perm[:], 0.0)
+        for c in range(2):
+            for r in range(2):
+                nc.gpsimd.tensor_copy(out=perm[:, c, r, 64 * c:64 * c + 64], in_=ident[:, r::2])
+
+        plan = []
+
+        def at(t, fn, *args):
+            plan.append((t, len(plan), fn, args))
+
+        m = PRM["m"]
+        u = []
+        t = PRM["u0"]
+        for h in range(NF):
+            u.append(t)
+            t += PRM["du0"] if h < PRM["hsw"] else PRM["du1"]
+        L = PRM["lag"]
+        at(2.4, w_copy, 0)
+        at(3.5, w_quant, 0)
+        at(3.6, w_copy, 1)
+        at(5.6, w_quant, 1)
+        for i in range(3):
+            at(PRM["x"] + 0.1 * i, load_x, i)
+        for n in range(NS):
+            if n >= 2:
+                at(m[n - NZ] + 0.95 if n >= NZ else 1.0 + n, load_slot, n)
+            at(m[n], mask, n)
+            at(m[n] + L["tr2"], tr2, n)
+            at(m[n] + L["cp2"], cp2, n)
+            at(m[n] + L["qz2"], qz2, n)
+            at(m[n] + L["mxd"], mxd, n)
+            at(m[n] + L["cpd"], cpd, n)
+            at(m[n] + L["tr1"], tr1, n)
+            at(m[n] + L["cp1"], cp1, n)
+        for g in range(G):
+            at(m[S * g + 3] + L["qz1"], qz1, g)
+        for b in range(B):
+            tx = PRM["xt"] + PRM["dx"] * b
+            at(tx, x_half, b)
+            at(tx + 0.5, x_copy, b)
+            if b % 2:
+                at(tx + 1.2, x_quant, b // 2)
+        at(8.5, mh_step)
+        for g in range(G):
+            at(PRM["adj"][g], load_adj, g)
+        for h in range(NF):
+            at(u[h] - L["adj"] if h < LAST else u[h] - 0.4, adj_t, h)
+            at(u[h] - L["mx"], front, h)
+            at(u[h] - L["act"], act, h, 0)
+            at(u[h] - L["act"] + 0.45, act, h, 1)
+            at(u[h], stt, h, 0)
+            at(u[h] + 0.5, stt, h, 1)
+            if h < GADD:
+                at(u[h] + 1.0, gadd, h)
+        for g in range(G - 1):
+            for r in range(2):
+                at(u[(g + 1) * B + 1 + r] + 0.1, row_half, g, r)
+            at(u[(g + 1) * B + 3] + 0.6, row_red, g)
+        for k, h in enumerate(range((G - 1) * B, NF)):
+            at(max(u[h] + 1.2, u[NF - 2] + 0.1 * k), row_last, h)
+        for g in range(2):
+            at(PRM["nc"][g], n_prep_copy, g)
+            at(u[NF - 1] + 0.51 + 0.1 * g, n_prep_quant, g)
+        for t, i, fn, args in sorted(plan, key=lambda step: step[:2]):
+            fn(*args)
+        nc.vector.reduce_sum(out=csum[:].rearrange("p c k -> p (c k)"), in_=cacc[:].rearrange("p c b e g -> p (c b e) g"), axis=AX.X)
+        cps = bank[2]
+        for r in range(2):
+            for c in range(2):
+                nc.tensor.matmul(out=cps[:, r * 6:(r + 1) * 6], lhsT=perm[:, c, r, :], rhs=csum[:, c, :], start=(c == 0), stop=(c == 1))
+        for s in range(S):
+            o = rsum[:, (G - 1) * S + s:(G - 1) * S + s + 1]
+            if s % 2:
+                nc.scalar.activation(out=junk[:], in_=RB4[s][:, :P], func=ACT.Copy, accum_out=o)
+            else:
+                nc.vector.reduce_sum(out=o, in_=RB4[s][:, :P], axis=AX.X)
+        nc.vector.tensor_tensor(out=q_sb[:].rearrange("p (g r e) -> p g r e", g=G, r=2), in0=cps[:, 0:12].rearrange("p (r g e) -> p g r e", r=2, g=G),
+                                in1=rsum[:].rearrange("p (g r e) -> p g r e", g=G, r=2), op=ALU.add)
+        nc.vector.tensor_tensor(out=q_sb[:], in0=q_sb[:], in1=mh[:], op=ALU.mult)
+
+        copies = [lambda: n_prep_copy(2)] + [lambda i=i: a_prep_copy(i) for i in range(9)]
+        quants = [lambda: n_prep_quant(2)] + [lambda i=i: a_prep_quant(i) for i in range(9)]
+        o1row(0)
+        copies[0]()
+        for k in range(10):
+            if k < 9:
+                copies[k + 1]()
+            quants[k]()
+        for n in range(1, NS):
+            o1row(n)
+            if n >= MX0:
+                for j in range((n - MX0) * 12 // (NS - MX0), (n - MX0 + 1) * 12 // (NS - MX0)):
+                    mxo(j // S, j % S)

@@ -25,52 +25,428 @@ ACT = mybir.ActivationFunctionType
 AX = mybir.AxisListType
 
 
-PRM = {"m": [4.83, 6.1, 7.23, 8.61, 12.77, 14.02, 15.25, 16.36, 18.71, 22.13, 23.11, 25.37], "u0": 22.4, "du0": 1.11, "du1": 0.27, "hsw": 18, "x": 8.2, "xt": 11.51, "dx": 1.37, "adj": [16.83, 21.39, 17.93], "nc": [26.19, 28.97, 33.34], "lag": {"tr2": 0.93, "cp2": 1.39, "qz2": 2.11, "mxd": 2.78, "cpd": 3.21, "tr1": 3.68, "cp1": 4.23, "qz1": 6.53, "adj": 1.5, "mx": 1.62, "act": 1.21}}
-
-
-def valid(p):
-    m, L = p["m"], p["lag"]
-    u = []
-    t = p["u0"]
-    for h in range(18):
-        u.append(t)
-        t += p["du0"] if h < p["hsw"] else p["du1"]
-    o = []
-    for n in range(12):
-        ch = [0, L["tr2"], L["cp2"], L["qz2"], L["mxd"], L["cpd"], L["tr1"], L["cp1"]]
-        o += [a < b for a, b in zip(ch, ch[1:])]
-        if n + 1 < 12:
-            o.append(m[n] + L["cp2"] < m[n + 1] + L["tr2"])
-            o.append(m[n] + L["cpd"] < m[n + 1] + L["mxd"])
-        if n + 2 < 12:
-            o.append(m[n] + L["tr2"] < m[n + 2])
-            o.append(m[n] + L["qz2"] < m[n + 2] + L["cp2"])
-            o.append(m[n] + L["mxd"] < m[n + 2] + L["qz2"])
-            o.append(m[n] + L["cp1"] < m[n + 2] + L["tr1"])
-    o.append(L["qz1"] > L["cp1"])
-    o.append(m[11] + L["qz1"] > u[5] - L["mx"])
-    for g in range(3):
-        f = m[4 * g + 3] + L["qz1"]
-        if g < 2:
-            o.append(f < m[4 * g + 4] + L["cp1"])
-        o.append(f < u[6 * g] - L["mx"])
-        o.append(p["adj"][g] < u[6 * g] - L["adj"])
-        if g < 2:
-            o.append(m[4 * g + 3] + L["cpd"] < p["nc"][g] < 45 and p["nc"][g] > 6)
-    xe = p["xt"] + 5 * p["dx"] + 1.2
-    o.append(xe < u[0] - L["mx"] and xe < u[0] - L["adj"])
-    o.append(p["x"] + 0.3 < p["xt"] and p["dx"] > 0.35)
-    for h in range(18):
-        if h >= 2:
-            o.append(u[h - 2] + 0 < u[h] - L["mx"])
-        if h >= 11 or h < 11:
-            if h >= 1 and (h < 11 or h >= 15):
-                o.append(u[h - 1] - L["act"] + 0.45 < u[h] - L["mx"])
-        if h >= 3:
-            o.append(u[h - 3] + 0.5 < u[h] - L["adj"])
-        o.append(L["mx"] > L["act"] > 0.5)
-    o.append(m[11] + L["cp1"] < u[11] - L["mx"] and m[11] + L["cp1"] < u[7])
-    return all(o)
+GADD = (6, 7, 8, 9, 10, 11, 12, 13)
+VEC = {"cp2": ((5,),), "cpd": ((4,),), "cp1": ((1,), (3,), (11,),), "x_copy": ((1,),), "act": ((1, 1), (3, 0), (8, 0), (12, 0),), "o1_c": ((1, 0), (1, 1), (2, 1), (4, 0), (6, 0), (6, 2), (7, 0), (7, 2), (10, 2), (10, 1), (11, 1),), "mxo_c": ((0, 0), (0, 3), (0, 1), (2, 1), (2, 0), (2, 3),)}
+SCA = {"n_prep_copy": ((0,), (2,),), "a_prep_copy": ((0,), (5,), (8,),)}
+ORDER = [
+    ("load_w", (1,)),
+    ("w_copy", (1,)),
+    ("load_w", (0,)),
+    ("w_copy", (0,)),
+    ("load_g", (0,)),
+    ("load_slot", (0,)),
+    ("load_slot", (1,)),
+    ("mask", (0,)),
+    ("load_g", (2,)),
+    ("load_slot", (2,)),
+    ("w_quant", (0,)),
+    ("mask", (1,)),
+    ("load_slot", (3,)),
+    ("tr2", (0,)),
+    ("load_g", (4,)),
+    ("cp2", (0,)),
+    ("tr2", (1,)),
+    ("qz2", (0,)),
+    ("load_slot", (4,)),
+    ("w_quant", (1,)),
+    ("cp2", (1,)),
+    ("mask", (2,)),
+    ("mh_step", ()),
+    ("load_x", (0,)),
+    ("load_slot", (5,)),
+    ("mxd", (0,)),
+    ("tr2", (2,)),
+    ("cpd", (0,)),
+    ("tr1", (0,)),
+    ("cp2", (2,)),
+    ("qz2", (1,)),
+    ("mask", (3,)),
+    ("qz2", (2,)),
+    ("load_x", (1,)),
+    ("mxd", (1,)),
+    ("cpd", (1,)),
+    ("mask", (4,)),
+    ("tr2", (3,)),
+    ("mxd", (2,)),
+    ("tr1", (1,)),
+    ("x_half", (1,)),
+    ("cp2", (3,)),
+    ("cpd", (2,)),
+    ("x_half", (0,)),
+    ("x_copy", (0,)),
+    ("tr2", (4,)),
+    ("qz2", (3,)),
+    ("cp1", (1,)),
+    ("x_copy", (1,)),
+    ("cp2", (4,)),
+    ("mxd", (3,)),
+    ("tr1", (2,)),
+    ("load_g", (6,)),
+    ("x_half", (3,)),
+    ("mask", (5,)),
+    ("qz2", (4,)),
+    ("load_x", (2,)),
+    ("x_quant", (0,)),
+    ("tr2", (5,)),
+    ("cpd", (3,)),
+    ("tr1", (3,)),
+    ("cp2", (5,)),
+    ("mxd", (4,)),
+    ("x_copy", (3,)),
+    ("x_half", (4,)),
+    ("x_half", (2,)),
+    ("cp1", (3,)),
+    ("n_prep_copy", (0,)),
+    ("qz2", (5,)),
+    ("qz1", (0,)),
+    ("load_slot", (6,)),
+    ("load_slot", (7,)),
+    ("x_half", (5,)),
+    ("x_copy", (4,)),
+    ("cpd", (4,)),
+    ("x_copy", (2,)),
+    ("load_slot", (8,)),
+    ("mask", (6,)),
+    ("front", (0,)),
+    ("n_prep_quant", (0,)),
+    ("load_g", (8,)),
+    ("tr2", (6,)),
+    ("act", (0, 0)),
+    ("x_quant", (1,)),
+    ("load_slot", (9,)),
+    ("act", (0, 1)),
+    ("cp2", (6,)),
+    ("front", (1,)),
+    ("mask", (7,)),
+    ("x_copy", (5,)),
+    ("mxd", (5,)),
+    ("tr1", (4,)),
+    ("load_adj", (0,)),
+    ("act", (1, 0)),
+    ("act", (1, 1)),
+    ("tr2", (7,)),
+    ("mask", (8,)),
+    ("qz2", (6,)),
+    ("front", (2,)),
+    ("cpd", (5,)),
+    ("tr1", (5,)),
+    ("cp2", (7,)),
+    ("act", (2, 0)),
+    ("tr2", (8,)),
+    ("load_slot", (11,)),
+    ("mask", (9,)),
+    ("act", (2, 1)),
+    ("qz2", (7,)),
+    ("cp2", (8,)),
+    ("mxd", (6,)),
+    ("x_quant", (2,)),
+    ("front", (3,)),
+    ("tr2", (9,)),
+    ("adj_t", (1,)),
+    ("cpd", (6,)),
+    ("adj_t", (2,)),
+    ("qz2", (8,)),
+    ("act", (3, 1)),
+    ("cp2", (9,)),
+    ("adj_t", (0,)),
+    ("act", (3, 0)),
+    ("cp1", (5,)),
+    ("load_slot", (10,)),
+    ("front", (4,)),
+    ("stt", (1, 1)),
+    ("act", (4, 0)),
+    ("load_g", (10,)),
+    ("stt", (0, 0)),
+    ("act", (4, 1)),
+    ("mxd", (7,)),
+    ("tr1", (6,)),
+    ("stt", (1, 0)),
+    ("front", (5,)),
+    ("stt", (0, 1)),
+    ("stt", (2, 0)),
+    ("adj_t", (4,)),
+    ("cpd", (7,)),
+    ("load_adj", (1,)),
+    ("act", (5, 0)),
+    ("mask", (10,)),
+    ("tr1", (7,)),
+    ("mxd", (8,)),
+    ("cp1", (7,)),
+    ("cpd", (8,)),
+    ("qz2", (9,)),
+    ("adj_t", (3,)),
+    ("act", (5, 1)),
+    ("tr2", (10,)),
+    ("qz1", (1,)),
+    ("tr1", (8,)),
+    ("front", (6,)),
+    ("mask", (11,)),
+    ("mxd", (9,)),
+    ("cp2", (10,)),
+    ("act", (6, 0)),
+    ("act", (6, 1)),
+    ("qz2", (10,)),
+    ("tr2", (11,)),
+    ("stt", (4, 0)),
+    ("stt", (2, 1)),
+    ("front", (7,)),
+    ("cpd", (9,)),
+    ("act", (7, 0)),
+    ("mxd", (10,)),
+    ("tr1", (9,)),
+    ("act", (7, 1)),
+    ("adj_t", (5,)),
+    ("stt", (3, 1)),
+    ("cp2", (11,)),
+    ("front", (8,)),
+    ("stt", (4, 1)),
+    ("stt", (3, 0)),
+    ("stt", (5, 0)),
+    ("adj_t", (7,)),
+    ("perm_step", ()),
+    ("stt", (5, 1)),
+    ("adj_t", (6,)),
+    ("stt", (7, 0)),
+    ("row_q", (0, 0)),
+    ("qz2", (11,)),
+    ("row_q", (0, 1)),
+    ("adj_t", (8,)),
+    ("cpd", (10,)),
+    ("act", (8, 1)),
+    ("act", (8, 0)),
+    ("stt", (6, 1)),
+    ("stt", (6, 0)),
+    ("mxd", (11,)),
+    ("a_prep_copy", (0,)),
+    ("cpd", (11,)),
+    ("load_adj", (2,)),
+    ("cp1", (9,)),
+    ("front", (9,)),
+    ("stt", (7, 1)),
+    ("row_q", (0, 2)),
+    ("gadd", (6,)),
+    ("row_q", (0, 3)),
+    ("act", (9, 1)),
+    ("adj_t", (9,)),
+    ("stt", (8, 0)),
+    ("adj_t", (10,)),
+    ("tr1", (10,)),
+    ("stt", (8, 1)),
+    ("tr1", (11,)),
+    ("act", (9, 0)),
+    ("gadd", (7,)),
+    ("row_red", (0,)),
+    ("stt", (9, 0)),
+    ("front", (10,)),
+    ("act", (10, 1)),
+    ("cp1", (11,)),
+    ("act", (10, 0)),
+    ("stt", (9, 1)),
+    ("adj_t", (11,)),
+    ("qz1", (2,)),
+    ("gadd", (8,)),
+    ("front", (11,)),
+    ("stt", (10, 1)),
+    ("act", (11, 0)),
+    ("front", (12,)),
+    ("act", (12, 1)),
+    ("act", (12, 0)),
+    ("adj_t", (12,)),
+    ("front", (14,)),
+    ("stt", (10, 0)),
+    ("adj_t", (13,)),
+    ("gadd", (9,)),
+    ("act", (11, 1)),
+    ("act", (14, 0)),
+    ("act", (14, 1)),
+    ("front", (13,)),
+    ("stt", (11, 0)),
+    ("stt", (11, 1)),
+    ("stt", (12, 1)),
+    ("stt", (12, 0)),
+    ("act", (13, 0)),
+    ("front", (15,)),
+    ("act", (15, 0)),
+    ("gadd", (10,)),
+    ("gadd", (11,)),
+    ("adj_t", (14,)),
+    ("act", (15, 1)),
+    ("stt", (14, 1)),
+    ("row_q", (1, 0)),
+    ("row_q", (1, 1)),
+    ("front", (16,)),
+    ("gadd", (12,)),
+    ("act", (13, 1)),
+    ("row_q", (1, 2)),
+    ("act", (16, 0)),
+    ("row_q", (1, 3)),
+    ("stt", (13, 0)),
+    ("act", (16, 1)),
+    ("stt", (13, 1)),
+    ("adj_t", (15,)),
+    ("stt", (14, 0)),
+    ("row_red", (1,)),
+    ("front", (17,)),
+    ("adj_t", (16,)),
+    ("stt", (15, 1)),
+    ("stt", (15, 0)),
+    ("gadd", (13,)),
+    ("act", (17, 1)),
+    ("adj_t", (17,)),
+    ("row_last", (12,)),
+    ("stt", (16, 0)),
+    ("stt", (16, 1)),
+    ("act", (17, 0)),
+    ("n_prep_copy", (2,)),
+    ("stt", (17, 1)),
+    ("stt", (17, 0)),
+    ("row_last", (13,)),
+    ("row_last", (14,)),
+    ("row_last", (15,)),
+    ("row_last", (16,)),
+    ("col_red", ()),
+    ("n_prep_copy", (1,)),
+    ("row_last", (17,)),
+    ("last_red", (0,)),
+    ("last_red", (1,)),
+    ("o1_t", (0, 2)),
+    ("last_red", (2,)),
+    ("col_mm", ()),
+    ("o1_t", (1, 0)),
+    ("o1_t", (0, 0)),
+    ("last_red", (3,)),
+    ("q_add", ()),
+    ("o1_t", (0, 1)),
+    ("q_mul", ()),
+    ("o1_c", (0, 2)),
+    ("o1_c", (1, 0)),
+    ("o1_c", (0, 0)),
+    ("o1_t", (1, 1)),
+    ("o1_t", (2, 1)),
+    ("o1_t", (1, 2)),
+    ("o1_c", (0, 1)),
+    ("o1_t", (2, 0)),
+    ("n_prep_quant", (1,)),
+    ("o1_c", (1, 2)),
+    ("o1_t", (2, 2)),
+    ("o1_store", (0, 2)),
+    ("a_prep_quant", (0,)),
+    ("o1_c", (1, 1)),
+    ("o1_store", (0, 0)),
+    ("o1_store", (0, 1)),
+    ("o1_t", (3, 0)),
+    ("o1_t", (3, 1)),
+    ("o1_c", (2, 0)),
+    ("o1_store", (1,)),
+    ("o1_c", (2, 2)),
+    ("o1_t", (3, 2)),
+    ("o1_c", (3, 0)),
+    ("o1_c", (3, 2)),
+    ("o1_c", (2, 1)),
+    ("o1_t", (4, 0)),
+    ("a_prep_copy", (1,)),
+    ("o1_t", (4, 2)),
+    ("o1_c", (3, 1)),
+    ("o1_store", (2,)),
+    ("o1_c", (4, 2)),
+    ("o1_t", (4, 1)),
+    ("o1_c", (4, 1)),
+    ("o1_c", (4, 0)),
+    ("o1_t", (5, 2)),
+    ("o1_t", (5, 0)),
+    ("o1_t", (5, 1)),
+    ("a_prep_copy", (2,)),
+    ("o1_t", (6, 1)),
+    ("o1_c", (5, 0)),
+    ("o1_t", (6, 0)),
+    ("n_prep_quant", (2,)),
+    ("a_prep_quant", (1,)),
+    ("o1_t", (6, 2)),
+    ("a_prep_quant", (2,)),
+    ("o1_store", (3,)),
+    ("mxo_mm", (0, 0)),
+    ("o1_c", (6, 0)),
+    ("o1_c", (5, 1)),
+    ("o1_t", (7, 0)),
+    ("o1_c", (6, 2)),
+    ("o1_c", (6, 1)),
+    ("mxo_c", (0, 0)),
+    ("o1_t", (7, 2)),
+    ("o1_c", (5, 2)),
+    ("o1_t", (8, 0)),
+    ("o1_t", (7, 1)),
+    ("o1_c", (7, 0)),
+    ("a_prep_copy", (5,)),
+    ("o1_t", (8, 1)),
+    ("o1_store", (4,)),
+    ("o1_c", (7, 2)),
+    ("a_prep_copy", (3,)),
+    ("a_prep_copy", (4,)),
+    ("o1_c", (8, 0)),
+    ("o1_t", (8, 2)),
+    ("mxo_mm", (0, 3)),
+    ("o1_t", (9, 2)),
+    ("o1_c", (7, 1)),
+    ("a_prep_quant", (5,)),
+    ("o1_t", (9, 0)),
+    ("o1_c", (8, 2)),
+    ("o1_t", (9, 1)),
+    ("o1_c", (8, 1)),
+    ("o1_store", (5,)),
+    ("o1_t", (10, 1)),
+    ("mxo_c", (0, 3)),
+    ("o1_c", (9, 0)),
+    ("o1_store", (6,)),
+    ("o1_c", (9, 1)),
+    ("o1_store", (7,)),
+    ("o1_t", (10, 0)),
+    ("o1_c", (9, 2)),
+    ("o1_c", (10, 0)),
+    ("mxo_mm", (0, 1)),
+    ("mxo_mm", (0, 2)),
+    ("o1_store", (8,)),
+    ("a_prep_quant", (4,)),
+    ("a_prep_quant", (3,)),
+    ("mxo_c", (0, 1)),
+    ("mxo_c", (0, 2)),
+    ("o1_t", (11, 1)),
+    ("a_prep_copy", (8,)),
+    ("a_prep_copy", (6,)),
+    ("a_prep_copy", (7,)),
+    ("o1_t", (10, 2)),
+    ("o1_t", (11, 0)),
+    ("mxo_mm", (1, 0)),
+    ("mxo_mm", (1, 1)),
+    ("o1_c", (10, 2)),
+    ("mxo_c", (1, 0)),
+    ("mxo_mm", (1, 2)),
+    ("o1_t", (11, 2)),
+    ("o1_c", (10, 1)),
+    ("mxo_c", (1, 1)),
+    ("a_prep_quant", (7,)),
+    ("mxo_mm", (1, 3)),
+    ("o1_store", (9,)),
+    ("a_prep_quant", (6,)),
+    ("o0_store", (0,)),
+    ("a_prep_quant", (8,)),
+    ("o1_store", (10,)),
+    ("mxo_mm", (2, 1)),
+    ("mxo_c", (2, 1)),
+    ("mxo_c", (1, 2)),
+    ("mxo_c", (1, 3)),
+    ("o1_c", (11, 2)),
+    ("mxo_mm", (2, 0)),
+    ("o1_c", (11, 0)),
+    ("o0_store", (1,)),
+    ("mxo_mm", (2, 2)),
+    ("o1_c", (11, 1)),
+    ("mxo_c", (2, 0)),
+    ("o1_store", (11,)),
+    ("mxo_mm", (2, 3)),
+    ("mxo_c", (2, 3)),
+    ("mxo_c", (2, 2)),
+    ("o0_store", (2,))
+]
 
 
 def tile_simplegcn_pa_v_kernel(tc, x, adj, W1, b1, z, rdeg, grad_out, out_0, out_1):
@@ -88,9 +464,6 @@ def tile_simplegcn_pa_v_kernel(tc, x, adj, W1, b1, z, rdeg, grad_out, out_0, out
     W_CUT = (IN, IN // 4)
     NS = G * S
     NF = G * B
-    GADD = NF - 4
-    V0 = 26
-    MX0 = 5
     FREE = 11
 
     with ExitStack() as ctx:
@@ -105,7 +478,6 @@ def tile_simplegcn_pa_v_kernel(tc, x, adj, W1, b1, z, rdeg, grad_out, out_0, out
             return over.tile([P] + cols, dtype, name=name, align_bytes=64, offset=offset)
 
         ident = sb("ident", [P], F32)
-        perm = sb("perm", [2, 2, P], F32)
         d_sb = sb("d_sb", [NS], F32)
         d2_sb = sb("d2_sb", [B * E], F32)
         mh = sb("mh", [NS], F32)
@@ -136,18 +508,18 @@ def tile_simplegcn_pa_v_kernel(tc, x, adj, W1, b1, z, rdeg, grad_out, out_0, out
         aq = [[sb(f"aq{g}{h}", [W], U32, RX + 2048 * (3 * g + h) + (8192 if 3 * g + h >= 6 else 0)) for h in range(G)] for g in range(G)]
         aqs = [[sb(f"aqs{g}{h}", [W], U8, RX + 26624 + 512 * (3 * g + h)) for h in range(G)] for g in range(G)]
         RB = RX + 31232
-        T2A = 9
-        T2N = 12
-        t2 = [sb(f"t2_{i}", [W], F32, RB + 2048 * i) for i in range(T2N)]
+        T2N = 16
+        t2 = [sb(f"t2_{i}", [W], F32, RB + 2048 * i if i < 12 else RX + 2048 * (i - 12)) for i in range(T2N)]
         ot = [sb(f"ot{i}", [N], F32, RB + 6144 * i) for i in range(4)]
-        RC = RB + 2048 * T2N
-        gt = [sb(f"gt{i}", [HID], BF16, RC + 2048 * i) for i in range(NZ)]
-        dz2 = [sb(f"dz2_{i}", [2, HID // 2], BF16, RC + 6144 + 2048 * i) for i in range(2)]
-        d2t = [sb(f"d2t{i}", [HID], BF16, RC + 10240 + 2048 * i) for i in range(2)]
-        d2q = [sb(f"d2q{i}", [2 * P], U32, RC + 14336 + 1024 * i) for i in range(2)]
-        d2s = [sb(f"d2s{i}", [2 * P], U8, RC + 16384 + 256 * i) for i in range(2)]
+        RC = RB + 24576
+        gt = [sb(f"gt{i}", [2, HID], BF16, RC + 4096 * i) for i in range(2)]
+        dz2 = [sb(f"dz2_{i}", [HID], BF16, RC + 8192 + 2048 * i) for i in range(2)]
+        d2t = [sb(f"d2t{i}", [HID], BF16, RC + 12288 + 2048 * i) for i in range(2)]
+        d2q = [sb(f"d2q{i}", [2 * P], U32, RC + 16384 + 1024 * i) for i in range(2)]
+        d2s = [sb(f"d2s{i}", [2 * P], U8, RC + 18432 + 256 * i) for i in range(2)]
         o0 = [sb(f"o0_{i}", [S, IN], F32, RC + 8192 * i) for i in range(2)]
 
+        perm = gt[0][:].rearrange("p a k -> p (a k)").bitcast(F32)[:, :512].rearrange("p (c r k) -> p c r k", c=2, r=2)
         bank = [psum.tile([P, W], F32, name=f"bank{i}") for i in range(8)]
         TPB, DAB, T1B, XB = bank[0], bank[1], bank[4], [bank[5], bank[6], bank[7], bank[2], bank[3]]
         RB4 = [bank[0], bank[1], bank[4], bank[7]]
@@ -159,13 +531,29 @@ def tile_simplegcn_pa_v_kernel(tc, x, adj, W1, b1, z, rdeg, grad_out, out_0, out
         def at_of(i):
             return bank[5 + i % 3] if i < LAST else bank[5 + i % 2]
 
+        def move(name, key, out, in_, scale=None):
+            if key in VEC.get(name, ()):
+                if scale is None:
+                    nc.vector.tensor_copy(out=out, in_=in_)
+                else:
+                    nc.vector.tensor_scalar(out=out, in0=in_, scalar1=scale, scalar2=None, op0=ALU.mult)
+            elif scale is None:
+                nc.scalar.copy(out=out, in_=in_)
+            else:
+                nc.scalar.activation(out=out, in_=in_, func=ACT.Copy, scale=scale)
+
         def load_slot(n):
             nc.sync.dma_start(out=buf4[n % NZ][:], in_=z_v[:, n // S, n % S, :])
-            nc.sync.dma_start(out=gt[n % NZ][:], in_=go_v[:, n // S, n % S, :])
+
+        def load_g(n):
+            nc.sync.dma_start(out=gt[n // 2 % 2][:], in_=go_v[:, n // S, n % S:n % S + 2, :])
+
+        def load_w(c):
+            nc.sync.dma_start(out=wraw[:, c, :, :], in_=w1_v[:, c, :, :])
 
         def load_adj(g):
-            for s in range(S):
-                nc.sync.dma_start(out=adj_sb[:, g, s, :], in_=adj_v[:, g, s, :])
+            for s in (0, 2):
+                nc.sync.dma_start(out=adj_sb[:, g, s:s + 2, :], in_=adj_v[:, g, s:s + 2, :])
 
         def load_x(i):
             nc.sync.dma_start(out=xraw[:, 2 * i:2 * i + 2, :, :], in_=x_v[:, 2 * i:2 * i + 2, :, :])
@@ -189,7 +577,7 @@ def tile_simplegcn_pa_v_kernel(tc, x, adj, W1, b1, z, rdeg, grad_out, out_0, out
         def x_copy(b):
             ps = XB[b % 5][:].rearrange("p (e u t) -> p e u t", e=2, u=2)
             dst = xt[b // 2 % 2][:, (b % 2) * 1024:(b % 2 + 1) * 1024].bitcast(F32).rearrange("p (e t u) -> p e t u", e=2, u=2)
-            nc.scalar.copy(out=dst, in_=ps.rearrange("p e u t -> p e t u"))
+            move("x_copy", (b,), dst, ps.rearrange("p e u t -> p e t u"))
 
         def x_quant(i):
             nc.vector.quantize_mx(out=x_codes[i][:].bitcast(E4M3), scales=x_scales[i][:], in_=xt[i % 2][:])
@@ -197,27 +585,20 @@ def tile_simplegcn_pa_v_kernel(tc, x, adj, W1, b1, z, rdeg, grad_out, out_0, out
         def mask(n):
             if not 0 <= n < NS:
                 return
-            zt, g_, o = buf4[n % NZ], gt[n % NZ], dz2[n % 2]
-            for u in range(2):
-                nc.vector.scalar_tensor_tensor(
-                    out=o[:, u, :].rearrange("p (q e) -> p q e", e=2),
-                    in0=zt[:].rearrange("p (q u e) -> p u q e", u=2, e=2)[:, u, :, :],
-                    scalar=0.0,
-                    in1=g_[:].rearrange("p (q u e) -> p u q e", u=2, e=2)[:, u, :, :],
-                    op0=ALU.is_gt, op1=ALU.mult)
+            nc.vector.scalar_tensor_tensor(out=dz2[n % 2][:], in0=buf4[n % NZ][:], scalar=0.0, in1=gt[n // 2 % 2][:, n % 2, :], op0=ALU.is_gt, op1=ALU.mult)
 
         def tr2(n):
             if not 0 <= n < NS:
                 return
-            words = dz2[n % 2][:].rearrange("p u k -> p (u k)").bitcast(F32)
+            words = dz2[n % 2][:].bitcast(F32)
             ps = TPB[:].rearrange("p (c u t) -> p c u t", c=2, u=2)
             for c in range(2):
                 for u in range(2):
-                    nc.tensor.transpose(ps[:, c, u, :], words[:, u * 256 + c * P:u * 256 + (c + 1) * P], ident[:])
+                    nc.tensor.transpose(ps[:, c, u, :], words[:, c * 256 + u:(c + 1) * 256:2], ident[:])
 
         def cp2(n):
             ps = TPB[:].rearrange("p (c u t) -> p c u t", c=2, u=2)
-            nc.scalar.copy(out=d2t[n % 2][:].bitcast(F32).rearrange("p (c t u) -> p c t u", c=2, u=2), in_=ps.rearrange("p c u t -> p c t u"))
+            move("cp2", (n,), d2t[n % 2][:].bitcast(F32).rearrange("p (c t u) -> p c t u", c=2, u=2), ps.rearrange("p c u t -> p c t u"))
 
         def qz2(n):
             if not 0 <= n < NS:
@@ -233,8 +614,8 @@ def tile_simplegcn_pa_v_kernel(tc, x, adj, W1, b1, z, rdeg, grad_out, out_0, out
                                     start=(c == 0), stop=(c == 1))
 
         def cpd(n):
-            nc.scalar.activation(out=dz1[n // S][:, n % S, :].rearrange("p (u q e) -> p u q e", u=2, e=2),
-                                 in_=DAB[:].rearrange("p (q u e) -> p u q e", u=2, e=2), func=ACT.Copy, scale=d_sb[:, n:n + 1])
+            move("cpd", (n,), dz1[n // S][:, n % S, :].rearrange("p (u q e) -> p u q e", u=2, e=2),
+                 DAB[:].rearrange("p (q u e) -> p u q e", u=2, e=2), scale=d_sb[:, n:n + 1])
 
         def tr1(n):
             if not 0 <= n < NS:
@@ -245,9 +626,9 @@ def tile_simplegcn_pa_v_kernel(tc, x, adj, W1, b1, z, rdeg, grad_out, out_0, out
                 nc.tensor.transpose(ps[:, u, :], words[:, u * P:(u + 1) * P], ident[:])
 
         def cp1(n):
-            ps = T1B[:, (n % 2) * 256:(n % 2 + 1) * 256].rearrange("p (u t) -> p u t", u=2)
-            dst = d1t[:, (n % S) * IN:(n % S + 1) * IN].bitcast(F32).rearrange("p (t u) -> p t u", u=2)
-            nc.scalar.copy(out=dst, in_=ps.rearrange("p u t -> p t u"))
+            ps = T1B[:].rearrange("p (s u t) -> p s u t", s=2, u=2)
+            dst = d1t[:, (n % S - 1) * IN:(n % S + 1) * IN].bitcast(F32).rearrange("p (s t u) -> p s t u", s=2, u=2)
+            move("cp1", (n,), dst, ps.rearrange("p s u t -> p s t u"))
 
         def qz1(g):
             nc.vector.quantize_mx(out=f_codes[g % 2][:].bitcast(E5M2), scales=f_scales[g % 2][:], in_=d1t[:])
@@ -263,8 +644,7 @@ def tile_simplegcn_pa_v_kernel(tc, x, adj, W1, b1, z, rdeg, grad_out, out_0, out
 
         def act(i, e):
             g, b = i // B, i % B
-            if True:
-                nc.scalar.activation(out=st[g][b][:, e, :], in_=pt_of(i)[e][:], func=ACT.Copy, scale=d2_sb[:, b * E + e:b * E + e + 1])
+            move("act", (i, e), st[g][b][:, e, :], pt_of(i)[e][:], scale=d2_sb[:, b * E + e:b * E + e + 1])
 
         def adj_t(i):
             if not 0 <= i < NF:
@@ -276,7 +656,7 @@ def tile_simplegcn_pa_v_kernel(tc, x, adj, W1, b1, z, rdeg, grad_out, out_0, out
 
 
         def t2_of(i, e):
-            return (t2[i % T2A] if e == 0 else t2[T2A + i % (T2N - T2A)])[:]
+            return t2[(2 * i + e) % T2N][:]
 
         def stt(i, e):
             g, b = i // B, i % B
@@ -287,30 +667,27 @@ def tile_simplegcn_pa_v_kernel(tc, x, adj, W1, b1, z, rdeg, grad_out, out_0, out
         def gadd(i):
             nc.gpsimd.tensor_tensor(out=t2_of(i, 0), in0=t2_of(i, 0), in1=t2_of(i, 1), op=ALU.add)
 
-        pend = {i: [t2_of(i, 0)] if i < GADD else [t2_of(i, 0), t2_of(i, 1)] for i in range(NF)}
+        def pend(i):
+            return [t2_of(i, 0)] if i in GADD else [t2_of(i, 0), t2_of(i, 1)]
 
-        def row_half(g, r):
-            bk = bank[4]
-            tiles = [t for i in range(g * B, (g + 1) * B) for t in pend[i]]
-            for s in (2 * r, 2 * r + 1):
-                for j, t in enumerate(tiles):
-                    nc.tensor.matmul(out=bk[:, s * P:(s + 1) * P], lhsT=t[:, s * P:(s + 1) * P], rhs=ident[:], start=(j == 0), stop=(j == len(tiles) - 1), is_transpose=True)
+        def row_q(g, s):
+            tiles = [t for i in range(g * B, (g + 1) * B) for t in pend(i)]
+            for j, t in enumerate(tiles):
+                nc.tensor.matmul(out=TPB[:, s * P:(s + 1) * P], lhsT=t[:, s * P:(s + 1) * P], rhs=ident[:], start=(j == 0), stop=(j == len(tiles) - 1), is_transpose=True)
 
         def row_red(g):
             for s in range(S):
-                nc.scalar.activation(out=junk[:], in_=bank[4][:, s * P:(s + 1) * P], func=ACT.Copy, accum_out=rsum[:, g * S + s:g * S + s + 1])
+                nc.scalar.activation(out=junk[:], in_=TPB[:, s * P:(s + 1) * P], func=ACT.Copy, accum_out=rsum[:, g * S + s:g * S + s + 1])
 
         def row_last(i):
-            for j, t in enumerate(pend[i]):
+            for j, t in enumerate(pend(i)):
                 for s in range(S):
-                    nc.tensor.matmul(out=RB4[s][:, :P], lhsT=t[:, s * P:(s + 1) * P], rhs=ident[:], start=(i % B == 0 and j == 0), stop=(i == NF - 1 and j == len(pend[i]) - 1), is_transpose=True)
+                    nc.tensor.matmul(out=RB4[s][:, :P], lhsT=t[:, s * P:(s + 1) * P], rhs=ident[:], start=(i % B == 0 and j == 0), stop=(i == NF - 1 and j == len(pend(i)) - 1), is_transpose=True)
 
         def n_prep_copy(g):
+            eng = nc.scalar.copy if (g,) in SCA.get("n_prep_copy", ()) else nc.vector.tensor_copy
             o, i = wil[g % 2][:].rearrange("p (f s) -> p f s", s=S), dz1[g][:].rearrange("p s f -> p f s")
-            if g < 2:
-                nc.gpsimd.tensor_scalar(out=o, in0=i, scalar1=1.0, scalar2=1.0, op0=ALU.mult, op1=ALU.mult)
-            else:
-                nc.vector.tensor_copy(out=o, in_=i)
+            eng(out=o, in_=i)
 
         def n_prep_quant(g):
             t = wil[g % 2][:]
@@ -321,148 +698,87 @@ def tile_simplegcn_pa_v_kernel(tc, x, adj, W1, b1, z, rdeg, grad_out, out_0, out
 
         def a_prep_copy(i):
             g, h = i % G, i // G
-            nc.vector.tensor_copy(out=a_buf(i).rearrange("p (a b s) -> p a b s", a=S, s=S), in_=adj_sb[:, g, :, h * W:(h + 1) * W].rearrange("p s (b a) -> p a b s", a=S))
+            o, i_ = a_buf(i).rearrange("p (a b s) -> p a b s", a=S, s=S), adj_sb[:, g, :, h * W:(h + 1) * W].rearrange("p s (b a) -> p a b s", a=S)
+            eng = nc.scalar.copy if (i,) in SCA.get("a_prep_copy", ()) else nc.vector.tensor_copy
+            eng(out=o, in_=i_)
 
         def a_prep_quant(i):
             g, h = i % G, i // G
             nc.vector.quantize_mx(out=aq[g][h][:].bitcast(E4M3), scales=aqs[g][h][:], in_=a_buf(i))
 
-        def mxo(h, s):
-            bk = bank[s % 3]
+        def mxo_mm(h, s):
             for g in range(G):
-                nc.tensor.matmul_mx(out=bk[:], lhsT=aq[g][h][:, s * P:(s + 1) * P].bitcast(E4M3), lhsT_scale=aqs[g][h][:, s * P:(s + 1) * P],
+                nc.tensor.matmul_mx(out=bank[s % 3][:], lhsT=aq[g][h][:, s * P:(s + 1) * P].bitcast(E4M3), lhsT_scale=aqs[g][h][:, s * P:(s + 1) * P],
                                     rhs=nq[g][:].bitcast(E5M2), rhs_scale=nqs[g][:], start=(g == 0), stop=(g == G - 1))
+
+        def mxo_c(h, s):
             o = o0[h % 2][:, s, :].rearrange("p (q u e) -> p q u e", u=2, e=2)
-            i = bk[:].rearrange("p (u q e) -> p q u e", u=2, e=2)
-            sc = d_sb[:, S * h + s:S * h + s + 1]
-            if not (h == 2 and s % 2):
-                nc.scalar.activation(out=o, in_=i, func=ACT.Copy, scale=sc)
-            else:
-                nc.vector.tensor_scalar(out=o, in0=i, scalar1=sc, scalar2=None, op0=ALU.mult)
-            if s == S - 1:
-                nc.sync.dma_start(out=o0_v[:, h, :, :], in_=o0[h % 2][:])
+            i = bank[s % 3][:].rearrange("p (u q e) -> p q u e", u=2, e=2)
+            move("mxo_c", (h, s), o, i, scale=d_sb[:, S * h + s:S * h + s + 1])
 
-        ob = [0]
+        def o0_store(h):
+            nc.sync.dma_start(out=o0_v[:, h, :, :], in_=o0[h % 2][:])
 
-        def o1row(n):
+        def ob(n, h):
+            return bank[3 + (G * n + h) % 5]
+
+        def o1_t(n, h):
             g, s = n // S, n % S
-            t = ot[n % 4]
-            for h in range(G):
-                bk = bank[3 + ob[0] % 5]
-                for k in range(4):
-                    nc.tensor.transpose(bk[:, k * P:(k + 1) * P], st[g][2 * h + k // 2][:, k % 2, s * P:(s + 1) * P], ident[:])
-                o = t[:, h * W:(h + 1) * W].rearrange("p (c b a) -> p c b a", c=2, a=2)
-                i = bk[:].rearrange("p (c a b) -> p c b a", c=2, a=2)
-                if not ((ob[0] >= V0 and ob[0] % 2) or ob[0] == 1):
-                    nc.scalar.activation(out=o, in_=i, func=ACT.Identity, bias=q_sb[:, n:n + 1])
-                else:
-                    nc.vector.tensor_scalar(out=o, in0=i, scalar1=q_sb[:, n:n + 1], scalar2=None, op0=ALU.add)
-                ob[0] += 1
-                if n == 0:
-                    nc.sync.dma_start(out=o1_v[:, g, s, h * W:(h + 1) * W], in_=t[:, h * W:(h + 1) * W])
-            if n:
-                nc.sync.dma_start(out=o1_v[:, g, s, :], in_=t[:])
+            for k in range(4):
+                nc.tensor.transpose(ob(n, h)[:, k * P:(k + 1) * P], st[g][2 * h + k // 2][:, k % 2, s * P:(s + 1) * P], ident[:])
 
-        def mh_step():
-            nc.vector.scalar_tensor_tensor(out=mh[:], in0=d_sb[:], scalar=-0.5, in1=d_sb[:], op0=ALU.mult, op1=ALU.mult)
+        def o1_c(n, h):
+            o = ot[n % 4][:, h * W:(h + 1) * W].rearrange("p (c b a) -> p c b a", c=2, a=2)
+            i = ob(n, h)[:].rearrange("p (c a b) -> p c b a", c=2, a=2)
+            if (n, h) in VEC.get("o1_c", ()):
+                nc.vector.tensor_scalar(out=o, in0=i, scalar1=q_sb[:, n:n + 1], scalar2=None, op0=ALU.add)
+            else:
+                nc.scalar.activation(out=o, in_=i, func=ACT.Identity, bias=q_sb[:, n:n + 1])
 
-        for c in range(2):
-            nc.sync.dma_start(out=wraw[:, c, :, :], in_=w1_v[:, c, :, :])
-        load_slot(0)
-        nc.scalar.dma_start(out=d_sb[:].rearrange("p (g s) -> p g s", g=G), in_=d_v)
-        nc.scalar.dma_start(out=d2_sb[:].rearrange("p (b e) -> p b e", b=B), in_=d2_v)
-        load_slot(1)
-        make_identity(nc, ident[:])
-        nc.gpsimd.memset(perm[:], 0.0)
-        for c in range(2):
+        def o1_store(n, h=None):
+            lo, hi = (0, N) if h is None else (h * W, (h + 1) * W)
+            nc.sync.dma_start(out=o1_v[:, n // S, n % S, lo:hi], in_=ot[n % 4][:, lo:hi])
+
+        def col_red():
+            nc.vector.reduce_sum(out=csum[:].rearrange("p c k -> p (c k)"), in_=cacc[:].rearrange("p c b e g -> p (c b e) g"), axis=AX.X)
+
+        def col_mm():
             for r in range(2):
-                nc.gpsimd.tensor_copy(out=perm[:, c, r, 64 * c:64 * c + 64], in_=ident[:, r::2])
+                for c in range(2):
+                    nc.tensor.matmul(out=bank[2][:, r * 6:(r + 1) * 6], lhsT=perm[:, c, r, :], rhs=csum[:, c, :], start=(c == 0), stop=(c == 1))
 
-        plan = []
-
-        def at(t, fn, *args):
-            plan.append((t, len(plan), fn, args))
-
-        m = PRM["m"]
-        u = []
-        t = PRM["u0"]
-        for h in range(NF):
-            u.append(t)
-            t += PRM["du0"] if h < PRM["hsw"] else PRM["du1"]
-        L = PRM["lag"]
-        at(2.4, w_copy, 0)
-        at(3.5, w_quant, 0)
-        at(3.6, w_copy, 1)
-        at(5.6, w_quant, 1)
-        for i in range(3):
-            at(PRM["x"] + 0.1 * i, load_x, i)
-        for n in range(NS):
-            if n >= 2:
-                at(m[n - NZ] + 0.95 if n >= NZ else 1.0 + n, load_slot, n)
-            at(m[n], mask, n)
-            at(m[n] + L["tr2"], tr2, n)
-            at(m[n] + L["cp2"], cp2, n)
-            at(m[n] + L["qz2"], qz2, n)
-            at(m[n] + L["mxd"], mxd, n)
-            at(m[n] + L["cpd"], cpd, n)
-            at(m[n] + L["tr1"], tr1, n)
-            at(m[n] + L["cp1"], cp1, n)
-        for g in range(G):
-            at(m[S * g + 3] + L["qz1"], qz1, g)
-        for b in range(B):
-            tx = PRM["xt"] + PRM["dx"] * b
-            at(tx, x_half, b)
-            at(tx + 0.5, x_copy, b)
-            if b % 2:
-                at(tx + 1.2, x_quant, b // 2)
-        at(8.5, mh_step)
-        for g in range(G):
-            at(PRM["adj"][g], load_adj, g)
-        for h in range(NF):
-            at(u[h] - L["adj"] if h < LAST else u[h] - 0.4, adj_t, h)
-            at(u[h] - L["mx"], front, h)
-            at(u[h] - L["act"], act, h, 0)
-            at(u[h] - L["act"] + 0.45, act, h, 1)
-            at(u[h], stt, h, 0)
-            at(u[h] + 0.5, stt, h, 1)
-            if h < GADD:
-                at(u[h] + 1.0, gadd, h)
-        for g in range(G - 1):
-            for r in range(2):
-                at(u[(g + 1) * B + 1 + r] + 0.1, row_half, g, r)
-            at(u[(g + 1) * B + 3] + 0.6, row_red, g)
-        for k, h in enumerate(range((G - 1) * B, NF)):
-            at(max(u[h] + 1.2, u[NF - 2] + 0.1 * k), row_last, h)
-        for g in range(2):
-            at(PRM["nc"][g], n_prep_copy, g)
-            at(u[NF - 1] + 0.51 + 0.1 * g, n_prep_quant, g)
-        for t, i, fn, args in sorted(plan, key=lambda step: step[:2]):
-            fn(*args)
-        nc.vector.reduce_sum(out=csum[:].rearrange("p c k -> p (c k)"), in_=cacc[:].rearrange("p c b e g -> p (c b e) g"), axis=AX.X)
-        cps = bank[2]
-        for r in range(2):
-            for c in range(2):
-                nc.tensor.matmul(out=cps[:, r * 6:(r + 1) * 6], lhsT=perm[:, c, r, :], rhs=csum[:, c, :], start=(c == 0), stop=(c == 1))
-        for s in range(S):
+        def last_red(s):
             o = rsum[:, (G - 1) * S + s:(G - 1) * S + s + 1]
             if s % 2:
                 nc.scalar.activation(out=junk[:], in_=RB4[s][:, :P], func=ACT.Copy, accum_out=o)
             else:
                 nc.vector.reduce_sum(out=o, in_=RB4[s][:, :P], axis=AX.X)
-        nc.vector.tensor_tensor(out=q_sb[:].rearrange("p (g r e) -> p g r e", g=G, r=2), in0=cps[:, 0:12].rearrange("p (r g e) -> p g r e", r=2, g=G),
-                                in1=rsum[:].rearrange("p (g r e) -> p g r e", g=G, r=2), op=ALU.add)
-        nc.vector.tensor_tensor(out=q_sb[:], in0=q_sb[:], in1=mh[:], op=ALU.mult)
 
-        copies = [lambda: n_prep_copy(2)] + [lambda i=i: a_prep_copy(i) for i in range(9)]
-        quants = [lambda: n_prep_quant(2)] + [lambda i=i: a_prep_quant(i) for i in range(9)]
-        o1row(0)
-        copies[0]()
-        for k in range(10):
-            if k < 9:
-                copies[k + 1]()
-            quants[k]()
-        for n in range(1, NS):
-            o1row(n)
-            if n >= MX0:
-                for j in range((n - MX0) * 12 // (NS - MX0), (n - MX0 + 1) * 12 // (NS - MX0)):
-                    mxo(j // S, j % S)
+        def q_add():
+            nc.vector.tensor_tensor(out=q_sb[:].rearrange("p (g r e) -> p g r e", g=G, r=2), in0=bank[2][:, 0:12].rearrange("p (r g e) -> p g r e", r=2, g=G),
+                                    in1=rsum[:].rearrange("p (g r e) -> p g r e", g=G, r=2), op=ALU.add)
+
+        def q_mul():
+            nc.vector.tensor_tensor(out=q_sb[:], in0=q_sb[:], in1=mh[:], op=ALU.mult)
+
+        def perm_step():
+            nc.gpsimd.memset(perm, 0.0)
+            for c in range(2):
+                for r in range(2):
+                    nc.gpsimd.tensor_copy(out=perm[:, c, r, 64 * c:64 * c + 64], in_=ident[:, r::2])
+
+        def mh_step():
+            nc.vector.scalar_tensor_tensor(out=mh[:], in0=d_sb[:], scalar=-0.5, in1=d_sb[:], op0=ALU.mult, op1=ALU.mult)
+
+        nc.scalar.dma_start(out=d_sb[:].rearrange("p (g s) -> p g s", g=G), in_=d_v)
+        nc.scalar.dma_start(out=d2_sb[:].rearrange("p (b e) -> p b e", b=B), in_=d2_v)
+        make_identity(nc, ident[:])
+
+        fns = {"load_w": load_w, "w_copy": w_copy, "w_quant": w_quant, "load_x": load_x, "x_quant": x_quant, "x_half": x_half, "x_copy": x_copy,
+               "load_slot": load_slot, "load_g": load_g, "cp1": cp1, "mask": mask, "tr2": tr2, "cp2": cp2, "qz2": qz2, "mxd": mxd, "cpd": cpd, "tr1": tr1,
+               "qz1": qz1, "mh_step": mh_step, "perm_step": perm_step, "load_adj": load_adj, "n_prep_copy": n_prep_copy, "n_prep_quant": n_prep_quant,
+               "adj_t": adj_t, "front": front, "act": act, "stt": stt, "row_q": row_q, "gadd": gadd, "row_red": row_red, "row_last": row_last,
+               "col_red": col_red, "col_mm": col_mm, "last_red": last_red, "q_add": q_add, "q_mul": q_mul, "a_prep_copy": a_prep_copy,
+               "a_prep_quant": a_prep_quant, "o1_t": o1_t, "o1_c": o1_c, "o1_store": o1_store, "mxo_mm": mxo_mm, "mxo_c": mxo_c, "o0_store": o0_store}
+        for name, args in ORDER:
+            fns[name](*args)

@@ -26,425 +26,429 @@ AX = mybir.AxisListType
 
 
 GADD = (6, 7, 8, 9, 10, 11, 12, 13)
-VEC = {"cp2": ((5,),), "cpd": ((4,),), "cp1": ((1,), (3,), (11,),), "x_copy": ((1,),), "act": ((1, 1), (3, 0), (8, 0), (12, 0),), "o1_c": ((1, 0), (1, 1), (2, 1), (4, 0), (6, 0), (6, 2), (7, 0), (7, 2), (10, 2), (10, 1), (11, 1),), "mxo_c": ((0, 0), (0, 3), (0, 1), (2, 1), (2, 0), (2, 3),)}
-SCA = {"n_prep_copy": ((0,), (2,),), "a_prep_copy": ((0,), (5,), (8,),)}
+VEC = {"cp2": ((2,), (5,),), "cpd": ((0,),), "x_copy": ((4,),), "act": ((1, 1), (2, 1), (4, 1),), "o1_c": ((0, 0), (0, 2), (1, 1), (2, 2), (3, 0), (4, 2), (6, 1), (7, 1), (7, 0), (10, 2), (8, 1), (8, 0),), "mxo_c": ((1, 0), (1, 2), (2, 0), (2, 2),)}
+SCA = {"w_copy": ((0,),)}
+GPS = {"n_prep_copy": ((0,), (1,), (2,),), "a_prep_copy": ((0,), (1,), (2,), (4,),)}
 ORDER = [
     ("load_w", (1,)),
-    ("w_copy", (1,)),
     ("load_w", (0,)),
-    ("w_copy", (0,)),
-    ("load_g", (0,)),
     ("load_slot", (0,)),
-    ("load_slot", (1,)),
+    ("identity", ()),
+    ("load_g", (0,)),
+    ("w_copy", (1,)),
+    ("w_quant", (1,)),
     ("mask", (0,)),
-    ("load_g", (2,)),
-    ("load_slot", (2,)),
+    ("w_copy", (0,)),
+    ("tr2", (0,)),
     ("w_quant", (0,)),
+    ("load_slot", (1,)),
+    ("load_g", (2,)),
+    ("cp2", (0,)),
+    ("load_slot", (2,)),
     ("mask", (1,)),
     ("load_slot", (3,)),
-    ("tr2", (0,)),
-    ("load_g", (4,)),
-    ("cp2", (0,)),
     ("tr2", (1,)),
-    ("qz2", (0,)),
-    ("load_slot", (4,)),
-    ("w_quant", (1,)),
-    ("cp2", (1,)),
-    ("mask", (2,)),
-    ("mh_step", ()),
     ("load_x", (0,)),
-    ("load_slot", (5,)),
+    ("load_d", ()),
+    ("qz2", (0,)),
+    ("mask", (2,)),
     ("mxd", (0,)),
     ("tr2", (2,)),
-    ("cpd", (0,)),
-    ("tr1", (0,)),
-    ("cp2", (2,)),
-    ("qz2", (1,)),
     ("mask", (3,)),
-    ("qz2", (2,)),
-    ("load_x", (1,)),
-    ("mxd", (1,)),
-    ("cpd", (1,)),
-    ("mask", (4,)),
-    ("tr2", (3,)),
-    ("mxd", (2,)),
-    ("tr1", (1,)),
-    ("x_half", (1,)),
-    ("cp2", (3,)),
-    ("cpd", (2,)),
     ("x_half", (0,)),
+    ("cp2", (1,)),
     ("x_copy", (0,)),
-    ("tr2", (4,)),
+    ("load_slot", (4,)),
+    ("qz2", (1,)),
+    ("cp2", (2,)),
+    ("tr2", (3,)),
+    ("mxd", (1,)),
+    ("qz2", (2,)),
+    ("mxd", (2,)),
+    ("cp2", (3,)),
+    ("cpd", (0,)),
+    ("cpd", (1,)),
+    ("tr1", (0,)),
     ("qz2", (3,)),
-    ("cp1", (1,)),
-    ("x_copy", (1,)),
-    ("cp2", (4,)),
+    ("cpd", (2,)),
+    ("load_g", (4,)),
+    ("x_half", (1,)),
+    ("tr1", (1,)),
+    ("mask", (4,)),
     ("mxd", (3,)),
-    ("tr1", (2,)),
-    ("load_g", (6,)),
-    ("x_half", (3,)),
+    ("load_slot", (5,)),
+    ("x_copy", (1,)),
+    ("load_d2", ()),
+    ("cp1", (1,)),
     ("mask", (5,)),
-    ("qz2", (4,)),
-    ("load_x", (2,)),
     ("x_quant", (0,)),
-    ("tr2", (5,)),
+    ("tr1", (2,)),
+    ("tr2", (4,)),
     ("cpd", (3,)),
+    ("tr2", (5,)),
+    ("load_x", (1,)),
     ("tr1", (3,)),
-    ("cp2", (5,)),
-    ("mxd", (4,)),
-    ("x_copy", (3,)),
-    ("x_half", (4,)),
-    ("x_half", (2,)),
-    ("cp1", (3,)),
-    ("n_prep_copy", (0,)),
-    ("qz2", (5,)),
-    ("qz1", (0,)),
+    ("load_g", (6,)),
     ("load_slot", (6,)),
     ("load_slot", (7,)),
-    ("x_half", (5,)),
-    ("x_copy", (4,)),
-    ("cpd", (4,)),
-    ("x_copy", (2,)),
-    ("load_slot", (8,)),
-    ("mask", (6,)),
+    ("cp2", (4,)),
+    ("x_half", (3,)),
+    ("x_half", (2,)),
+    ("cp2", (5,)),
+    ("qz2", (4,)),
+    ("cp1", (3,)),
+    ("mh_step", ()),
+    ("mxd", (4,)),
+    ("qz1", (0,)),
+    ("x_copy", (3,)),
+    ("qz2", (5,)),
     ("front", (0,)),
-    ("n_prep_quant", (0,)),
-    ("load_g", (8,)),
-    ("tr2", (6,)),
-    ("act", (0, 0)),
+    ("mask", (6,)),
+    ("x_copy", (2,)),
+    ("mxd", (5,)),
+    ("load_x", (2,)),
+    ("cpd", (4,)),
     ("x_quant", (1,)),
+    ("act", (0, 0)),
+    ("cpd", (5,)),
+    ("load_slot", (8,)),
+    ("tr2", (6,)),
+    ("load_g", (8,)),
     ("load_slot", (9,)),
-    ("act", (0, 1)),
     ("cp2", (6,)),
     ("front", (1,)),
-    ("mask", (7,)),
-    ("x_copy", (5,)),
-    ("mxd", (5,)),
-    ("tr1", (4,)),
-    ("load_adj", (0,)),
     ("act", (1, 0)),
+    ("tr1", (5,)),
+    ("mask", (7,)),
+    ("tr1", (4,)),
+    ("x_half", (4,)),
+    ("act", (0, 1)),
     ("act", (1, 1)),
     ("tr2", (7,)),
-    ("mask", (8,)),
-    ("qz2", (6,)),
-    ("front", (2,)),
-    ("cpd", (5,)),
-    ("tr1", (5,)),
-    ("cp2", (7,)),
-    ("act", (2, 0)),
-    ("tr2", (8,)),
-    ("load_slot", (11,)),
-    ("mask", (9,)),
-    ("act", (2, 1)),
-    ("qz2", (7,)),
-    ("cp2", (8,)),
-    ("mxd", (6,)),
-    ("x_quant", (2,)),
+    ("x_half", (5,)),
     ("front", (3,)),
-    ("tr2", (9,)),
-    ("adj_t", (1,)),
-    ("cpd", (6,)),
-    ("adj_t", (2,)),
-    ("qz2", (8,)),
-    ("act", (3, 1)),
-    ("cp2", (9,)),
-    ("adj_t", (0,)),
+    ("cp2", (7,)),
+    ("x_copy", (5,)),
+    ("qz2", (6,)),
+    ("mxd", (6,)),
+    ("x_copy", (4,)),
     ("act", (3, 0)),
-    ("cp1", (5,)),
-    ("load_slot", (10,)),
-    ("front", (4,)),
-    ("stt", (1, 1)),
-    ("act", (4, 0)),
-    ("load_g", (10,)),
-    ("stt", (0, 0)),
-    ("act", (4, 1)),
+    ("qz2", (7,)),
     ("mxd", (7,)),
-    ("tr1", (6,)),
-    ("stt", (1, 0)),
-    ("front", (5,)),
-    ("stt", (0, 1)),
-    ("stt", (2, 0)),
-    ("adj_t", (4,)),
+    ("cp1", (5,)),
+    ("front", (2,)),
+    ("mask", (8,)),
     ("cpd", (7,)),
-    ("load_adj", (1,)),
-    ("act", (5, 0)),
-    ("mask", (10,)),
+    ("cpd", (6,)),
+    ("mask", (9,)),
+    ("tr2", (8,)),
+    ("tr2", (9,)),
+    ("act", (3, 1)),
+    ("cp2", (8,)),
+    ("tr1", (6,)),
+    ("load_g", (10,)),
+    ("load_slot", (10,)),
+    ("act", (2, 1)),
+    ("load_slot", (11,)),
+    ("act", (2, 0)),
+    ("x_quant", (2,)),
     ("tr1", (7,)),
-    ("mxd", (8,)),
     ("cp1", (7,)),
-    ("cpd", (8,)),
-    ("qz2", (9,)),
-    ("adj_t", (3,)),
-    ("act", (5, 1)),
-    ("tr2", (10,)),
-    ("qz1", (1,)),
-    ("tr1", (8,)),
-    ("front", (6,)),
+    ("cp2", (9,)),
+    ("mask", (10,)),
+    ("front", (4,)),
+    ("qz2", (8,)),
     ("mask", (11,)),
-    ("mxd", (9,)),
-    ("cp2", (10,)),
-    ("act", (6, 0)),
-    ("act", (6, 1)),
-    ("qz2", (10,)),
+    ("front", (5,)),
+    ("qz2", (9,)),
+    ("mxd", (8,)),
+    ("tr2", (10,)),
+    ("act", (4, 0)),
+    ("load_adj", (0,)),
     ("tr2", (11,)),
-    ("stt", (4, 0)),
-    ("stt", (2, 1)),
-    ("front", (7,)),
-    ("cpd", (9,)),
-    ("act", (7, 0)),
-    ("mxd", (10,)),
-    ("tr1", (9,)),
-    ("act", (7, 1)),
-    ("adj_t", (5,)),
-    ("stt", (3, 1)),
-    ("cp2", (11,)),
-    ("front", (8,)),
-    ("stt", (4, 1)),
-    ("stt", (3, 0)),
-    ("stt", (5, 0)),
-    ("adj_t", (7,)),
+    ("act", (4, 1)),
+    ("mxd", (9,)),
+    ("adj_t", (1,)),
+    ("qz1", (1,)),
+    ("act", (5, 0)),
+    ("cp2", (10,)),
+    ("qz2", (10,)),
     ("perm_step", ()),
-    ("stt", (5, 1)),
-    ("adj_t", (6,)),
-    ("stt", (7, 0)),
-    ("row_q", (0, 0)),
-    ("qz2", (11,)),
-    ("row_q", (0, 1)),
-    ("adj_t", (8,)),
-    ("cpd", (10,)),
-    ("act", (8, 1)),
-    ("act", (8, 0)),
-    ("stt", (6, 1)),
-    ("stt", (6, 0)),
-    ("mxd", (11,)),
+    ("cp2", (11,)),
+    ("adj_t", (3,)),
+    ("adj_t", (4,)),
+    ("act", (5, 1)),
     ("a_prep_copy", (0,)),
+    ("cpd", (9,)),
+    ("mxd", (10,)),
+    ("qz2", (11,)),
+    ("cpd", (8,)),
+    ("mxd", (11,)),
+    ("cpd", (10,)),
+    ("stt", (1, 0)),
+    ("stt", (3, 1)),
     ("cpd", (11,)),
-    ("load_adj", (2,)),
-    ("cp1", (9,)),
-    ("front", (9,)),
-    ("stt", (7, 1)),
-    ("row_q", (0, 2)),
-    ("gadd", (6,)),
-    ("row_q", (0, 3)),
-    ("act", (9, 1)),
-    ("adj_t", (9,)),
-    ("stt", (8, 0)),
-    ("adj_t", (10,)),
+    ("stt", (3, 0)),
+    ("front", (7,)),
+    ("stt", (4, 1)),
+    ("adj_t", (0,)),
+    ("adj_t", (5,)),
+    ("act", (7, 1)),
     ("tr1", (10,)),
-    ("stt", (8, 1)),
+    ("tr1", (8,)),
+    ("stt", (4, 0)),
+    ("stt", (0, 0)),
+    ("act", (7, 0)),
+    ("tr1", (9,)),
+    ("cp1", (9,)),
+    ("front", (6,)),
+    ("stt", (0, 1)),
+    ("stt", (1, 1)),
+    ("act", (6, 1)),
+    ("act", (6, 0)),
+    ("load_adj", (1,)),
     ("tr1", (11,)),
-    ("act", (9, 0)),
-    ("gadd", (7,)),
-    ("row_red", (0,)),
-    ("stt", (9, 0)),
+    ("adj_t", (2,)),
+    ("adj_t", (8,)),
+    ("adj_t", (6,)),
     ("front", (10,)),
-    ("act", (10, 1)),
     ("cp1", (11,)),
+    ("stt", (2, 0)),
+    ("front", (8,)),
+    ("stt", (2, 1)),
+    ("n_prep_copy", (1,)),
+    ("stt", (5, 0)),
     ("act", (10, 0)),
-    ("stt", (9, 1)),
-    ("adj_t", (11,)),
-    ("qz1", (2,)),
-    ("gadd", (8,)),
+    ("adj_t", (7,)),
+    ("stt", (5, 1)),
+    ("row_q", (0, 1)),
+    ("row_q", (0, 3)),
+    ("act", (8, 1)),
+    ("n_prep_copy", (0,)),
+    ("stt", (7, 0)),
+    ("act", (10, 1)),
+    ("act", (8, 0)),
     ("front", (11,)),
-    ("stt", (10, 1)),
-    ("act", (11, 0)),
-    ("front", (12,)),
-    ("act", (12, 1)),
-    ("act", (12, 0)),
-    ("adj_t", (12,)),
-    ("front", (14,)),
-    ("stt", (10, 0)),
-    ("adj_t", (13,)),
-    ("gadd", (9,)),
+    ("qz1", (2,)),
+    ("front", (9,)),
+    ("row_q", (0, 0)),
+    ("stt", (6, 0)),
+    ("row_q", (0, 2)),
     ("act", (11, 1)),
-    ("act", (14, 0)),
-    ("act", (14, 1)),
+    ("act", (11, 0)),
+    ("act", (9, 0)),
+    ("stt", (6, 1)),
+    ("stt", (7, 1)),
+    ("load_adj", (2,)),
+    ("stt", (8, 0)),
+    ("act", (9, 1)),
+    ("adj_t", (10,)),
+    ("a_prep_copy", (2,)),
+    ("adj_t", (9,)),
+    ("adj_t", (11,)),
+    ("front", (12,)),
+    ("stt", (8, 1)),
+    ("row_red", (0,)),
+    ("gadd", (7,)),
+    ("stt", (10, 0)),
+    ("stt", (10, 1)),
+    ("gadd", (6,)),
+    ("stt", (9, 1)),
+    ("front", (17,)),
+    ("gadd", (10,)),
+    ("act", (12, 1)),
+    ("adj_t", (12,)),
+    ("act", (12, 0)),
+    ("stt", (9, 0)),
+    ("gadd", (8,)),
     ("front", (13,)),
+    ("act", (17, 0)),
     ("stt", (11, 0)),
+    ("adj_t", (15,)),
+    ("act", (13, 1)),
+    ("gadd", (9,)),
+    ("front", (15,)),
     ("stt", (11, 1)),
+    ("adj_t", (13,)),
+    ("act", (13, 0)),
+    ("front", (14,)),
+    ("act", (15, 1)),
     ("stt", (12, 1)),
     ("stt", (12, 0)),
-    ("act", (13, 0)),
-    ("front", (15,)),
-    ("act", (15, 0)),
-    ("gadd", (10,)),
     ("gadd", (11,)),
     ("adj_t", (14,)),
-    ("act", (15, 1)),
-    ("stt", (14, 1)),
-    ("row_q", (1, 0)),
     ("row_q", (1, 1)),
-    ("front", (16,)),
     ("gadd", (12,)),
-    ("act", (13, 1)),
-    ("row_q", (1, 2)),
-    ("act", (16, 0)),
-    ("row_q", (1, 3)),
-    ("stt", (13, 0)),
-    ("act", (16, 1)),
     ("stt", (13, 1)),
-    ("adj_t", (15,)),
-    ("stt", (14, 0)),
-    ("row_red", (1,)),
-    ("front", (17,)),
-    ("adj_t", (16,)),
     ("stt", (15, 1)),
-    ("stt", (15, 0)),
+    ("act", (14, 1)),
+    ("row_q", (1, 2)),
+    ("stt", (13, 0)),
+    ("row_q", (1, 0)),
+    ("row_q", (1, 3)),
+    ("act", (14, 0)),
     ("gadd", (13,)),
+    ("stt", (14, 1)),
+    ("front", (16,)),
+    ("act", (15, 0)),
     ("act", (17, 1)),
+    ("stt", (15, 0)),
+    ("act", (16, 0)),
+    ("stt", (14, 0)),
     ("adj_t", (17,)),
+    ("adj_t", (16,)),
+    ("act", (16, 1)),
     ("row_last", (12,)),
     ("stt", (16, 0)),
-    ("stt", (16, 1)),
-    ("act", (17, 0)),
-    ("n_prep_copy", (2,)),
-    ("stt", (17, 1)),
-    ("stt", (17, 0)),
     ("row_last", (13,)),
+    ("stt", (17, 0)),
+    ("stt", (16, 1)),
     ("row_last", (14,)),
-    ("row_last", (15,)),
-    ("row_last", (16,)),
+    ("stt", (17, 1)),
     ("col_red", ()),
-    ("n_prep_copy", (1,)),
+    ("row_last", (15,)),
+    ("a_prep_copy", (1,)),
+    ("row_last", (16,)),
     ("row_last", (17,)),
-    ("last_red", (0,)),
-    ("last_red", (1,)),
-    ("o1_t", (0, 2)),
-    ("last_red", (2,)),
     ("col_mm", ()),
-    ("o1_t", (1, 0)),
+    ("n_prep_quant", (0,)),
     ("o1_t", (0, 0)),
+    ("last_red", (2,)),
+    ("row_red", (1,)),
+    ("last_red", (1,)),
     ("last_red", (3,)),
-    ("q_add", ()),
-    ("o1_t", (0, 1)),
-    ("q_mul", ()),
-    ("o1_c", (0, 2)),
-    ("o1_c", (1, 0)),
-    ("o1_c", (0, 0)),
-    ("o1_t", (1, 1)),
-    ("o1_t", (2, 1)),
+    ("o1_t", (1, 0)),
+    ("o1_t", (0, 2)),
     ("o1_t", (1, 2)),
-    ("o1_c", (0, 1)),
-    ("o1_t", (2, 0)),
-    ("n_prep_quant", (1,)),
-    ("o1_c", (1, 2)),
+    ("last_red", (0,)),
+    ("o1_t", (1, 1)),
+    ("q_add", ()),
     ("o1_t", (2, 2)),
-    ("o1_store", (0, 2)),
-    ("a_prep_quant", (0,)),
-    ("o1_c", (1, 1)),
-    ("o1_store", (0, 0)),
-    ("o1_store", (0, 1)),
-    ("o1_t", (3, 0)),
-    ("o1_t", (3, 1)),
-    ("o1_c", (2, 0)),
-    ("o1_store", (1,)),
-    ("o1_c", (2, 2)),
+    ("q_mul", ()),
     ("o1_t", (3, 2)),
-    ("o1_c", (3, 0)),
+    ("o1_c", (1, 0)),
+    ("n_prep_copy", (2,)),
+    ("o1_c", (0, 0)),
+    ("o1_t", (2, 0)),
+    ("o1_t", (2, 1)),
+    ("o1_t", (4, 0)),
+    ("o1_c", (1, 2)),
+    ("o1_t", (5, 0)),
     ("o1_c", (3, 2)),
     ("o1_c", (2, 1)),
-    ("o1_t", (4, 0)),
-    ("a_prep_copy", (1,)),
+    ("o1_c", (0, 2)),
+    ("o1_store", (0, 0)),
+    ("o1_store", (0, 2)),
+    ("o1_t", (3, 1)),
+    ("o1_c", (1, 1)),
+    ("o1_c", (2, 0)),
+    ("o1_store", (1,)),
+    ("o1_t", (3, 0)),
+    ("n_prep_quant", (1,)),
     ("o1_t", (4, 2)),
-    ("o1_c", (3, 1)),
-    ("o1_store", (2,)),
-    ("o1_c", (4, 2)),
-    ("o1_t", (4, 1)),
-    ("o1_c", (4, 1)),
+    ("o1_t", (0, 1)),
     ("o1_c", (4, 0)),
-    ("o1_t", (5, 2)),
-    ("o1_t", (5, 0)),
+    ("o1_c", (2, 2)),
     ("o1_t", (5, 1)),
-    ("a_prep_copy", (2,)),
-    ("o1_t", (6, 1)),
-    ("o1_c", (5, 0)),
-    ("o1_t", (6, 0)),
-    ("n_prep_quant", (2,)),
-    ("a_prep_quant", (1,)),
-    ("o1_t", (6, 2)),
+    ("a_prep_quant", (0,)),
+    ("o1_c", (3, 0)),
+    ("o1_t", (5, 2)),
     ("a_prep_quant", (2,)),
-    ("o1_store", (3,)),
-    ("mxo_mm", (0, 0)),
-    ("o1_c", (6, 0)),
+    ("a_prep_quant", (1,)),
+    ("o1_t", (7, 1)),
+    ("o1_c", (3, 1)),
+    ("n_prep_quant", (2,)),
+    ("o1_t", (7, 2)),
+    ("o1_t", (6, 0)),
+    ("o1_c", (0, 1)),
+    ("mxo_mm", (0, 3)),
+    ("o1_store", (2,)),
     ("o1_c", (5, 1)),
+    ("mxo_mm", (0, 0)),
+    ("o1_c", (5, 2)),
+    ("a_prep_copy", (3,)),
+    ("o1_t", (6, 2)),
+    ("o1_c", (5, 0)),
+    ("o1_store", (3,)),
+    ("mxo_c", (0, 3)),
+    ("o1_t", (6, 1)),
     ("o1_t", (7, 0)),
+    ("o1_c", (4, 2)),
     ("o1_c", (6, 2)),
     ("o1_c", (6, 1)),
-    ("mxo_c", (0, 0)),
-    ("o1_t", (7, 2)),
-    ("o1_c", (5, 2)),
-    ("o1_t", (8, 0)),
-    ("o1_t", (7, 1)),
-    ("o1_c", (7, 0)),
-    ("a_prep_copy", (5,)),
-    ("o1_t", (8, 1)),
-    ("o1_store", (4,)),
-    ("o1_c", (7, 2)),
-    ("a_prep_copy", (3,)),
-    ("a_prep_copy", (4,)),
-    ("o1_c", (8, 0)),
-    ("o1_t", (8, 2)),
-    ("mxo_mm", (0, 3)),
-    ("o1_t", (9, 2)),
+    ("o1_c", (6, 0)),
     ("o1_c", (7, 1)),
-    ("a_prep_quant", (5,)),
+    ("a_prep_copy", (4,)),
+    ("o1_c", (7, 0)),
+    ("mxo_c", (0, 0)),
     ("o1_t", (9, 0)),
-    ("o1_c", (8, 2)),
-    ("o1_t", (9, 1)),
-    ("o1_c", (8, 1)),
-    ("o1_store", (5,)),
-    ("o1_t", (10, 1)),
-    ("mxo_c", (0, 3)),
-    ("o1_c", (9, 0)),
-    ("o1_store", (6,)),
-    ("o1_c", (9, 1)),
-    ("o1_store", (7,)),
+    ("o1_t", (4, 1)),
+    ("o1_store", (0, 1)),
+    ("o1_c", (4, 1)),
     ("o1_t", (10, 0)),
-    ("o1_c", (9, 2)),
-    ("o1_c", (10, 0)),
-    ("mxo_mm", (0, 1)),
-    ("mxo_mm", (0, 2)),
-    ("o1_store", (8,)),
+    ("o1_store", (5,)),
     ("a_prep_quant", (4,)),
+    ("o1_t", (9, 2)),
+    ("o1_t", (9, 1)),
     ("a_prep_quant", (3,)),
-    ("mxo_c", (0, 1)),
-    ("mxo_c", (0, 2)),
-    ("o1_t", (11, 1)),
-    ("a_prep_copy", (8,)),
-    ("a_prep_copy", (6,)),
-    ("a_prep_copy", (7,)),
-    ("o1_t", (10, 2)),
     ("o1_t", (11, 0)),
-    ("mxo_mm", (1, 0)),
-    ("mxo_mm", (1, 1)),
-    ("o1_c", (10, 2)),
-    ("mxo_c", (1, 0)),
-    ("mxo_mm", (1, 2)),
-    ("o1_t", (11, 2)),
+    ("o1_c", (7, 2)),
+    ("o1_c", (9, 2)),
+    ("o1_store", (6,)),
+    ("o1_t", (8, 2)),
+    ("a_prep_copy", (5,)),
+    ("mxo_mm", (0, 2)),
+    ("mxo_mm", (0, 1)),
+    ("a_prep_copy", (7,)),
+    ("mxo_c", (0, 2)),
+    ("o1_t", (8, 1)),
+    ("a_prep_quant", (5,)),
+    ("o1_t", (10, 2)),
+    ("o1_c", (9, 1)),
+    ("o1_t", (10, 1)),
+    ("o1_store", (7,)),
+    ("mxo_c", (0, 1)),
+    ("o1_c", (9, 0)),
+    ("o1_t", (11, 1)),
+    ("o1_store", (4,)),
     ("o1_c", (10, 1)),
-    ("mxo_c", (1, 1)),
-    ("a_prep_quant", (7,)),
-    ("mxo_mm", (1, 3)),
-    ("o1_store", (9,)),
-    ("a_prep_quant", (6,)),
     ("o0_store", (0,)),
+    ("o1_t", (11, 2)),
+    ("o1_c", (11, 1)),
+    ("mxo_mm", (1, 2)),
+    ("o1_c", (11, 0)),
+    ("o1_c", (11, 2)),
+    ("o1_t", (8, 0)),
+    ("mxo_mm", (1, 0)),
+    ("o1_c", (8, 2)),
+    ("mxo_mm", (1, 1)),
+    ("a_prep_copy", (6,)),
+    ("a_prep_copy", (8,)),
+    ("mxo_mm", (1, 3)),
+    ("a_prep_quant", (6,)),
     ("a_prep_quant", (8,)),
-    ("o1_store", (10,)),
+    ("mxo_c", (1, 0)),
+    ("a_prep_quant", (7,)),
+    ("o1_c", (10, 2)),
+    ("mxo_c", (1, 1)),
+    ("o1_store", (11,)),
+    ("o1_store", (9,)),
+    ("mxo_mm", (2, 3)),
+    ("o1_c", (8, 1)),
+    ("o1_c", (10, 0)),
+    ("mxo_c", (1, 2)),
+    ("mxo_mm", (2, 0)),
+    ("mxo_c", (1, 3)),
+    ("mxo_c", (2, 0)),
+    ("mxo_mm", (2, 2)),
+    ("mxo_c", (2, 2)),
+    ("mxo_c", (2, 3)),
     ("mxo_mm", (2, 1)),
     ("mxo_c", (2, 1)),
-    ("mxo_c", (1, 2)),
-    ("mxo_c", (1, 3)),
-    ("o1_c", (11, 2)),
-    ("mxo_mm", (2, 0)),
-    ("o1_c", (11, 0)),
+    ("o1_store", (10,)),
     ("o0_store", (1,)),
-    ("mxo_mm", (2, 2)),
-    ("o1_c", (11, 1)),
-    ("mxo_c", (2, 0)),
-    ("o1_store", (11,)),
-    ("mxo_mm", (2, 3)),
-    ("mxo_c", (2, 3)),
-    ("mxo_c", (2, 2)),
+    ("o1_c", (8, 0)),
+    ("o1_store", (8,)),
     ("o0_store", (2,))
 ]
 
@@ -461,10 +465,8 @@ def tile_simplegcn_pa_v_kernel(tc, x, adj, W1, b1, z, rdeg, grad_out, out_0, out
     o0_v = out_0.rearrange("(g p s) f -> p g s f", g=G, s=S)
     o1_v = out_1.rearrange("(g p s) w -> p g s w", g=G, s=S)
     NZ = 3
-    W_CUT = (IN, IN // 4)
     NS = G * S
     NF = G * B
-    FREE = 11
 
     with ExitStack() as ctx:
         keep = ctx.enter_context(tc.tile_pool(name="keep", bufs=1))
@@ -521,15 +523,23 @@ def tile_simplegcn_pa_v_kernel(tc, x, adj, W1, b1, z, rdeg, grad_out, out_0, out
 
         perm = gt[0][:].rearrange("p a k -> p (a k)").bitcast(F32)[:, :512].rearrange("p (c r k) -> p c r k", c=2, r=2)
         bank = [psum.tile([P, W], F32, name=f"bank{i}") for i in range(8)]
-        TPB, DAB, T1B, XB = bank[0], bank[1], bank[4], [bank[5], bank[6], bank[7], bank[2], bank[3]]
-        RB4 = [bank[0], bank[1], bank[4], bank[7]]
-        LAST = NF - 3
+        free = list(bank)
+        held = {}
+        reads = {}
 
-        def pt_of(i):
-            return bank[0:2] if (i % 2 and FREE <= i < LAST) else bank[2:4]
+        def take(key, readers):
+            if key not in held:
+                held[key] = free[0]
+                reads[key] = readers
+                free.remove(held[key])
+            return held[key]
 
-        def at_of(i):
-            return bank[5 + i % 3] if i < LAST else bank[5 + i % 2]
+        def last(key):
+            b = held[key]
+            reads[key] -= 1
+            if reads[key] == 0:
+                free.append(b)
+            return b
 
         def move(name, key, out, in_, scale=None):
             if key in VEC.get(name, ()):
@@ -541,6 +551,23 @@ def tile_simplegcn_pa_v_kernel(tc, x, adj, W1, b1, z, rdeg, grad_out, out_0, out
                 nc.scalar.copy(out=out, in_=in_)
             else:
                 nc.scalar.activation(out=out, in_=in_, func=ACT.Copy, scale=scale)
+
+        def weave(name, key, out, in_):
+            if (key,) in GPS.get(name, ()):
+                nc.gpsimd.tensor_scalar(out=out, in0=in_, scalar1=1.0, scalar2=1.0, op0=ALU.mult, op1=ALU.mult)
+            elif (key,) in SCA.get(name, ()):
+                nc.scalar.copy(out=out, in_=in_)
+            else:
+                nc.vector.tensor_copy(out=out, in_=in_)
+
+        def load_d():
+            nc.sync.dma_start(out=d_sb[:].rearrange("p (g s) -> p g s", g=G), in_=d_v)
+
+        def load_d2():
+            nc.sync.dma_start(out=d2_sb[:].rearrange("p (b e) -> p b e", b=B), in_=d2_v)
+
+        def identity():
+            make_identity(nc, ident[:])
 
         def load_slot(n):
             nc.sync.dma_start(out=buf4[n % NZ][:], in_=z_v[:, n // S, n % S, :])
@@ -559,15 +586,13 @@ def tile_simplegcn_pa_v_kernel(tc, x, adj, W1, b1, z, rdeg, grad_out, out_0, out
             nc.sync.dma_start(out=xraw[:, 2 * i:2 * i + 2, :, :], in_=x_v[:, 2 * i:2 * i + 2, :, :])
 
         def w_copy(c):
-            for lo, hi, eng in ((0, W_CUT[c], nc.vector.tensor_copy), (W_CUT[c], IN, nc.scalar.copy)):
-                if lo < hi:
-                    eng(out=wil[c][:, 4 * lo:4 * hi].rearrange("p (f j) -> p f j", j=4), in_=wraw[:, c, :, lo:hi].rearrange("p j f -> p f j"))
+            weave("w_copy", c, wil[c][:].rearrange("p (f j) -> p f j", j=4), wraw[:, c, :, :].rearrange("p j f -> p f j"))
 
         def w_quant(c):
             nc.vector.quantize_mx(out=w_codes[:, c * IN:(c + 1) * IN].bitcast(E4M3), scales=w_scales[:, c * IN:(c + 1) * IN], in_=wil[c][:])
 
         def x_half(b):
-            bk = XB[b % 5]
+            bk = take(("x", b), 1)
             ps = bk[:].rearrange("p (e u t) -> p e u t", e=2, u=2)
             for e in range(2):
                 words = xraw[:, b, e, :].bitcast(F32)
@@ -575,7 +600,7 @@ def tile_simplegcn_pa_v_kernel(tc, x, adj, W1, b1, z, rdeg, grad_out, out_0, out
                     nc.tensor.transpose(ps[:, e, u, :], words[:, u::2], ident[:])
 
         def x_copy(b):
-            ps = XB[b % 5][:].rearrange("p (e u t) -> p e u t", e=2, u=2)
+            ps = last(("x", b))[:].rearrange("p (e u t) -> p e u t", e=2, u=2)
             dst = xt[b // 2 % 2][:, (b % 2) * 1024:(b % 2 + 1) * 1024].bitcast(F32).rearrange("p (e t u) -> p e t u", e=2, u=2)
             move("x_copy", (b,), dst, ps.rearrange("p e u t -> p e t u"))
 
@@ -585,19 +610,23 @@ def tile_simplegcn_pa_v_kernel(tc, x, adj, W1, b1, z, rdeg, grad_out, out_0, out
         def mask(n):
             if not 0 <= n < NS:
                 return
-            nc.vector.scalar_tensor_tensor(out=dz2[n % 2][:], in0=buf4[n % NZ][:], scalar=0.0, in1=gt[n // 2 % 2][:, n % 2, :], op0=ALU.is_gt, op1=ALU.mult)
+            zt, g_, o = buf4[n % NZ][:], gt[n // 2 % 2][:, n % 2, :], dz2[n % 2][:].rearrange("p (u q e) -> p u q e", u=2, e=2)
+            for u in range(2):
+                nc.vector.scalar_tensor_tensor(
+                    out=o[:, u, :, :], in0=zt.rearrange("p (q u e) -> p u q e", u=2, e=2)[:, u, :, :], scalar=0.0,
+                    in1=g_.rearrange("p (q u e) -> p u q e", u=2, e=2)[:, u, :, :], op0=ALU.is_gt, op1=ALU.mult)
 
         def tr2(n):
             if not 0 <= n < NS:
                 return
             words = dz2[n % 2][:].bitcast(F32)
-            ps = TPB[:].rearrange("p (c u t) -> p c u t", c=2, u=2)
+            ps = take(("t2", n), 1)[:].rearrange("p (c u t) -> p c u t", c=2, u=2)
             for c in range(2):
                 for u in range(2):
-                    nc.tensor.transpose(ps[:, c, u, :], words[:, c * 256 + u:(c + 1) * 256:2], ident[:])
+                    nc.tensor.transpose(ps[:, c, u, :], words[:, u * 256 + c * P:u * 256 + (c + 1) * P], ident[:])
 
         def cp2(n):
-            ps = TPB[:].rearrange("p (c u t) -> p c u t", c=2, u=2)
+            ps = last(("t2", n))[:].rearrange("p (c u t) -> p c u t", c=2, u=2)
             move("cp2", (n,), d2t[n % 2][:].bitcast(F32).rearrange("p (c t u) -> p c t u", c=2, u=2), ps.rearrange("p c u t -> p c t u"))
 
         def qz2(n):
@@ -608,25 +637,26 @@ def tile_simplegcn_pa_v_kernel(tc, x, adj, W1, b1, z, rdeg, grad_out, out_0, out
         def mxd(n):
             if not 0 <= n < NS:
                 return
+            bk = take(("da", n), 1)
             for c in range(2):
-                nc.tensor.matmul_mx(out=DAB[:], lhsT=d2q[n % 2][:, c * P:(c + 1) * P].bitcast(E5M2), lhsT_scale=d2s[n % 2][:, c * P:(c + 1) * P],
+                nc.tensor.matmul_mx(out=bk[:], lhsT=d2q[n % 2][:, c * P:(c + 1) * P].bitcast(E5M2), lhsT_scale=d2s[n % 2][:, c * P:(c + 1) * P],
                                     rhs=w_codes[:, c * IN:(c + 1) * IN].bitcast(E4M3), rhs_scale=w_scales[:, c * IN:(c + 1) * IN],
                                     start=(c == 0), stop=(c == 1))
 
         def cpd(n):
             move("cpd", (n,), dz1[n // S][:, n % S, :].rearrange("p (u q e) -> p u q e", u=2, e=2),
-                 DAB[:].rearrange("p (q u e) -> p u q e", u=2, e=2), scale=d_sb[:, n:n + 1])
+                 last(("da", n))[:].rearrange("p (q u e) -> p u q e", u=2, e=2), scale=d_sb[:, n:n + 1])
 
         def tr1(n):
             if not 0 <= n < NS:
                 return
             words = dz1[n // S][:, n % S, :].bitcast(F32)
-            ps = T1B[:, (n % 2) * 256:(n % 2 + 1) * 256].rearrange("p (u t) -> p u t", u=2)
+            ps = take(("t1", n // 2), 1)[:, (n % 2) * 256:(n % 2 + 1) * 256].rearrange("p (u t) -> p u t", u=2)
             for u in range(2):
                 nc.tensor.transpose(ps[:, u, :], words[:, u * P:(u + 1) * P], ident[:])
 
         def cp1(n):
-            ps = T1B[:].rearrange("p (s u t) -> p s u t", s=2, u=2)
+            ps = last(("t1", n // 2))[:].rearrange("p (s u t) -> p s u t", s=2, u=2)
             dst = d1t[:, (n % S - 1) * IN:(n % S + 1) * IN].bitcast(F32).rearrange("p (s t u) -> p s t u", s=2, u=2)
             move("cp1", (n,), dst, ps.rearrange("p s u t -> p s t u"))
 
@@ -639,12 +669,12 @@ def tile_simplegcn_pa_v_kernel(tc, x, adj, W1, b1, z, rdeg, grad_out, out_0, out
             g, b = i // B, i % B
             for e in range(E):
                 c0 = ((b % 2) * E + e) * P
-                nc.tensor.matmul_mx(out=pt_of(i)[e][:], lhsT=x_codes[b // 2][:, c0:c0 + P].bitcast(E4M3), lhsT_scale=x_scales[b // 2][:, c0:c0 + P],
+                nc.tensor.matmul_mx(out=take(("pt", i, e), 1)[:], lhsT=x_codes[b // 2][:, c0:c0 + P].bitcast(E4M3), lhsT_scale=x_scales[b // 2][:, c0:c0 + P],
                                     rhs=f_codes[g % 2][:].bitcast(E5M2), rhs_scale=f_scales[g % 2][:], start=True, stop=True)
 
         def act(i, e):
             g, b = i // B, i % B
-            move("act", (i, e), st[g][b][:, e, :], pt_of(i)[e][:], scale=d2_sb[:, b * E + e:b * E + e + 1])
+            move("act", (i, e), st[g][b][:, e, :], last(("pt", i, e))[:], scale=d2_sb[:, b * E + e:b * E + e + 1])
 
         def adj_t(i):
             if not 0 <= i < NF:
@@ -652,7 +682,7 @@ def tile_simplegcn_pa_v_kernel(tc, x, adj, W1, b1, z, rdeg, grad_out, out_0, out
             g, b = i // B, i % B
             for s in range(S):
                 words = adj_sb[:, g, s, b * 256:(b + 1) * 256].bitcast(F32)
-                nc.tensor.transpose(at_of(i)[:, s * P:(s + 1) * P], words, ident[:])
+                nc.tensor.transpose(take(("at", i), 2)[:, s * P:(s + 1) * P], words, ident[:])
 
 
         def t2_of(i, e):
@@ -660,7 +690,7 @@ def tile_simplegcn_pa_v_kernel(tc, x, adj, W1, b1, z, rdeg, grad_out, out_0, out
 
         def stt(i, e):
             g, b = i // B, i % B
-            at = at_of(i)[:].bitcast(BF16).rearrange("p (t e) -> p e t", e=E)
+            at = last(("at", i))[:].bitcast(BF16).rearrange("p (t e) -> p e t", e=E)
             nc.vector.scalar_tensor_tensor(out=t2_of(i, e), in0=at[:, e, :], scalar=1.0, in1=st[g][b][:, e, :],
                                            op0=ALU.mult, op1=ALU.mult, accum_out=cacc[:, b % 2, b // 2, e, g:g + 1])
 
@@ -673,21 +703,20 @@ def tile_simplegcn_pa_v_kernel(tc, x, adj, W1, b1, z, rdeg, grad_out, out_0, out
         def row_q(g, s):
             tiles = [t for i in range(g * B, (g + 1) * B) for t in pend(i)]
             for j, t in enumerate(tiles):
-                nc.tensor.matmul(out=TPB[:, s * P:(s + 1) * P], lhsT=t[:, s * P:(s + 1) * P], rhs=ident[:], start=(j == 0), stop=(j == len(tiles) - 1), is_transpose=True)
+                nc.tensor.matmul(out=take(("row", g), S)[:, s * P:(s + 1) * P], lhsT=t[:, s * P:(s + 1) * P], rhs=ident[:], start=(j == 0), stop=(j == len(tiles) - 1), is_transpose=True)
 
         def row_red(g):
             for s in range(S):
-                nc.scalar.activation(out=junk[:], in_=TPB[:, s * P:(s + 1) * P], func=ACT.Copy, accum_out=rsum[:, g * S + s:g * S + s + 1])
+                nc.scalar.activation(out=junk[:], in_=last(("row", g))[:, s * P:(s + 1) * P], func=ACT.Copy, accum_out=rsum[:, g * S + s:g * S + s + 1])
 
         def row_last(i):
             for j, t in enumerate(pend(i)):
                 for s in range(S):
-                    nc.tensor.matmul(out=RB4[s][:, :P], lhsT=t[:, s * P:(s + 1) * P], rhs=ident[:], start=(i % B == 0 and j == 0), stop=(i == NF - 1 and j == len(pend(i)) - 1), is_transpose=True)
+                    nc.tensor.matmul(out=take(("last", s), 1)[:, :P], lhsT=t[:, s * P:(s + 1) * P], rhs=ident[:], start=(i % B == 0 and j == 0), stop=(i == NF - 1 and j == len(pend(i)) - 1), is_transpose=True)
 
         def n_prep_copy(g):
-            eng = nc.scalar.copy if (g,) in SCA.get("n_prep_copy", ()) else nc.vector.tensor_copy
             o, i = wil[g % 2][:].rearrange("p (f s) -> p f s", s=S), dz1[g][:].rearrange("p s f -> p f s")
-            eng(out=o, in_=i)
+            weave("n_prep_copy", g, o, i)
 
         def n_prep_quant(g):
             t = wil[g % 2][:]
@@ -699,37 +728,34 @@ def tile_simplegcn_pa_v_kernel(tc, x, adj, W1, b1, z, rdeg, grad_out, out_0, out
         def a_prep_copy(i):
             g, h = i % G, i // G
             o, i_ = a_buf(i).rearrange("p (a b s) -> p a b s", a=S, s=S), adj_sb[:, g, :, h * W:(h + 1) * W].rearrange("p s (b a) -> p a b s", a=S)
-            eng = nc.scalar.copy if (i,) in SCA.get("a_prep_copy", ()) else nc.vector.tensor_copy
-            eng(out=o, in_=i_)
+            weave("a_prep_copy", i, o, i_)
 
         def a_prep_quant(i):
             g, h = i % G, i // G
             nc.vector.quantize_mx(out=aq[g][h][:].bitcast(E4M3), scales=aqs[g][h][:], in_=a_buf(i))
 
         def mxo_mm(h, s):
+            bk = take(("o0", h, s), 1)
             for g in range(G):
-                nc.tensor.matmul_mx(out=bank[s % 3][:], lhsT=aq[g][h][:, s * P:(s + 1) * P].bitcast(E4M3), lhsT_scale=aqs[g][h][:, s * P:(s + 1) * P],
+                nc.tensor.matmul_mx(out=bk[:], lhsT=aq[g][h][:, s * P:(s + 1) * P].bitcast(E4M3), lhsT_scale=aqs[g][h][:, s * P:(s + 1) * P],
                                     rhs=nq[g][:].bitcast(E5M2), rhs_scale=nqs[g][:], start=(g == 0), stop=(g == G - 1))
 
         def mxo_c(h, s):
             o = o0[h % 2][:, s, :].rearrange("p (q u e) -> p q u e", u=2, e=2)
-            i = bank[s % 3][:].rearrange("p (u q e) -> p q u e", u=2, e=2)
+            i = last(("o0", h, s))[:].rearrange("p (u q e) -> p q u e", u=2, e=2)
             move("mxo_c", (h, s), o, i, scale=d_sb[:, S * h + s:S * h + s + 1])
 
         def o0_store(h):
             nc.sync.dma_start(out=o0_v[:, h, :, :], in_=o0[h % 2][:])
 
-        def ob(n, h):
-            return bank[3 + (G * n + h) % 5]
-
         def o1_t(n, h):
             g, s = n // S, n % S
             for k in range(4):
-                nc.tensor.transpose(ob(n, h)[:, k * P:(k + 1) * P], st[g][2 * h + k // 2][:, k % 2, s * P:(s + 1) * P], ident[:])
+                nc.tensor.transpose(take(("o1", n, h), 1)[:, k * P:(k + 1) * P], st[g][2 * h + k // 2][:, k % 2, s * P:(s + 1) * P], ident[:])
 
         def o1_c(n, h):
             o = ot[n % 4][:, h * W:(h + 1) * W].rearrange("p (c b a) -> p c b a", c=2, a=2)
-            i = ob(n, h)[:].rearrange("p (c a b) -> p c b a", c=2, a=2)
+            i = last(("o1", n, h))[:].rearrange("p (c a b) -> p c b a", c=2, a=2)
             if (n, h) in VEC.get("o1_c", ()):
                 nc.vector.tensor_scalar(out=o, in0=i, scalar1=q_sb[:, n:n + 1], scalar2=None, op0=ALU.add)
             else:
@@ -743,19 +769,21 @@ def tile_simplegcn_pa_v_kernel(tc, x, adj, W1, b1, z, rdeg, grad_out, out_0, out
             nc.vector.reduce_sum(out=csum[:].rearrange("p c k -> p (c k)"), in_=cacc[:].rearrange("p c b e g -> p (c b e) g"), axis=AX.X)
 
         def col_mm():
+            bk = take(("col",), 1)
             for r in range(2):
                 for c in range(2):
-                    nc.tensor.matmul(out=bank[2][:, r * 6:(r + 1) * 6], lhsT=perm[:, c, r, :], rhs=csum[:, c, :], start=(c == 0), stop=(c == 1))
+                    nc.tensor.matmul(out=bk[:, r * 6:(r + 1) * 6], lhsT=perm[:, c, r, :], rhs=csum[:, c, :], start=(c == 0), stop=(c == 1))
 
         def last_red(s):
             o = rsum[:, (G - 1) * S + s:(G - 1) * S + s + 1]
+            bk = last(("last", s))
             if s % 2:
-                nc.scalar.activation(out=junk[:], in_=RB4[s][:, :P], func=ACT.Copy, accum_out=o)
+                nc.scalar.activation(out=junk[:], in_=bk[:, :P], func=ACT.Copy, accum_out=o)
             else:
-                nc.vector.reduce_sum(out=o, in_=RB4[s][:, :P], axis=AX.X)
+                nc.vector.reduce_sum(out=o, in_=bk[:, :P], axis=AX.X)
 
         def q_add():
-            nc.vector.tensor_tensor(out=q_sb[:].rearrange("p (g r e) -> p g r e", g=G, r=2), in0=bank[2][:, 0:12].rearrange("p (r g e) -> p g r e", r=2, g=G),
+            nc.vector.tensor_tensor(out=q_sb[:].rearrange("p (g r e) -> p g r e", g=G, r=2), in0=last(("col",))[:, 0:12].rearrange("p (r g e) -> p g r e", r=2, g=G),
                                     in1=rsum[:].rearrange("p (g r e) -> p g r e", g=G, r=2), op=ALU.add)
 
         def q_mul():
@@ -770,11 +798,8 @@ def tile_simplegcn_pa_v_kernel(tc, x, adj, W1, b1, z, rdeg, grad_out, out_0, out
         def mh_step():
             nc.vector.scalar_tensor_tensor(out=mh[:], in0=d_sb[:], scalar=-0.5, in1=d_sb[:], op0=ALU.mult, op1=ALU.mult)
 
-        nc.scalar.dma_start(out=d_sb[:].rearrange("p (g s) -> p g s", g=G), in_=d_v)
-        nc.scalar.dma_start(out=d2_sb[:].rearrange("p (b e) -> p b e", b=B), in_=d2_v)
-        make_identity(nc, ident[:])
 
-        fns = {"load_w": load_w, "w_copy": w_copy, "w_quant": w_quant, "load_x": load_x, "x_quant": x_quant, "x_half": x_half, "x_copy": x_copy,
+        fns = {"load_d": load_d, "load_d2": load_d2, "identity": identity, "load_w": load_w, "w_copy": w_copy, "w_quant": w_quant, "load_x": load_x, "x_quant": x_quant, "x_half": x_half, "x_copy": x_copy,
                "load_slot": load_slot, "load_g": load_g, "cp1": cp1, "mask": mask, "tr2": tr2, "cp2": cp2, "qz2": qz2, "mxd": mxd, "cpd": cpd, "tr1": tr1,
                "qz1": qz1, "mh_step": mh_step, "perm_step": perm_step, "load_adj": load_adj, "n_prep_copy": n_prep_copy, "n_prep_quant": n_prep_quant,
                "adj_t": adj_t, "front": front, "act": act, "stt": stt, "row_q": row_q, "gadd": gadd, "row_red": row_red, "row_last": row_last,

@@ -26,429 +26,429 @@ AX = mybir.AxisListType
 
 
 GADD = (6, 7, 8, 9, 10, 11, 12, 13)
-VEC = {"cp2": ((2,), (5,),), "cpd": ((0,),), "x_copy": ((4,),), "act": ((1, 1), (2, 1), (4, 1),), "o1_c": ((0, 0), (0, 2), (1, 1), (2, 2), (3, 0), (4, 2), (6, 1), (7, 1), (7, 0), (10, 2), (8, 1), (8, 0),), "mxo_c": ((1, 0), (1, 2), (2, 0), (2, 2),)}
-SCA = {"w_copy": ((0,),)}
-GPS = {"n_prep_copy": ((0,), (1,), (2,),), "a_prep_copy": ((0,), (1,), (2,), (4,),)}
+VEC = {"o1_c": ((0, 1), (0, 0), (1, 2), (2, 1), (3, 1), (8, 2), (9, 1), (9, 2),), "mxo_c": ((0, 3), (1, 2), (1, 3), (2, 3),)}
+SCA = {"a_prep_copy": ((1,), (8,),)}
+GPS = {}
 ORDER = [
-    ("load_w", (1,)),
+    ("load_slot", (1,)),
+    ("load_g", (0,)),
     ("load_w", (0,)),
     ("load_slot", (0,)),
-    ("identity", ()),
-    ("load_g", (0,)),
-    ("w_copy", (1,)),
-    ("w_quant", (1,)),
-    ("mask", (0,)),
-    ("w_copy", (0,)),
-    ("tr2", (0,)),
-    ("w_quant", (0,)),
-    ("load_slot", (1,)),
-    ("load_g", (2,)),
-    ("cp2", (0,)),
-    ("load_slot", (2,)),
     ("mask", (1,)),
-    ("load_slot", (3,)),
+    ("load_w", (1,)),
+    ("identity", ()),
     ("tr2", (1,)),
     ("load_x", (0,)),
+    ("load_g", (2,)),
+    ("w_copy", (0,)),
+    ("cp2", (1,)),
+    ("mask", (0,)),
+    ("tr2", (0,)),
+    ("w_quant", (0,)),
+    ("w_copy", (1,)),
+    ("x_half", (0,)),
+    ("load_slot", (2,)),
+    ("cp2", (0,)),
+    ("load_slot", (3,)),
     ("load_d", ()),
+    ("qz2", (1,)),
     ("qz2", (0,)),
+    ("load_x", (1,)),
+    ("w_quant", (1,)),
     ("mask", (2,)),
+    ("mask", (3,)),
+    ("x_half", (1,)),
+    ("mxd", (1,)),
+    ("x_copy", (1,)),
+    ("load_g", (4,)),
+    ("x_copy", (0,)),
+    ("cpd", (1,)),
     ("mxd", (0,)),
     ("tr2", (2,)),
-    ("mask", (3,)),
-    ("x_half", (0,)),
-    ("cp2", (1,)),
-    ("x_copy", (0,)),
-    ("load_slot", (4,)),
-    ("qz2", (1,)),
+    ("load_slot", (5,)),
+    ("cpd", (0,)),
+    ("tr1", (1,)),
     ("cp2", (2,)),
     ("tr2", (3,)),
-    ("mxd", (1,)),
-    ("qz2", (2,)),
-    ("mxd", (2,)),
+    ("load_slot", (4,)),
     ("cp2", (3,)),
-    ("cpd", (0,)),
-    ("cpd", (1,)),
-    ("tr1", (0,)),
-    ("qz2", (3,)),
-    ("cpd", (2,)),
-    ("load_g", (4,)),
-    ("x_half", (1,)),
-    ("tr1", (1,)),
-    ("mask", (4,)),
-    ("mxd", (3,)),
-    ("load_slot", (5,)),
-    ("x_copy", (1,)),
-    ("load_d2", ()),
-    ("cp1", (1,)),
-    ("mask", (5,)),
+    ("x_half", (2,)),
     ("x_quant", (0,)),
-    ("tr1", (2,)),
-    ("tr2", (4,)),
-    ("cpd", (3,)),
-    ("tr2", (5,)),
-    ("load_x", (1,)),
-    ("tr1", (3,)),
+    ("qz2", (2,)),
+    ("load_x", (2,)),
+    ("x_half", (3,)),
+    ("x_copy", (2,)),
+    ("qz2", (3,)),
+    ("mask", (5,)),
+    ("mxd", (2,)),
+    ("x_copy", (3,)),
+    ("mh_step", ()),
     ("load_g", (6,)),
+    ("mxd", (3,)),
+    ("cpd", (2,)),
+    ("tr1", (0,)),
+    ("tr1", (2,)),
+    ("cpd", (3,)),
+    ("cp1", (1,)),
+    ("tr1", (3,)),
+    ("mask", (4,)),
+    ("tr2", (5,)),
+    ("x_half", (5,)),
+    ("tr2", (4,)),
+    ("x_quant", (1,)),
+    ("cp1", (3,)),
+    ("x_half", (4,)),
+    ("cp2", (5,)),
+    ("x_copy", (5,)),
+    ("cp2", (4,)),
+    ("load_d2", ()),
+    ("qz1", (0,)),
+    ("n_prep_copy", (0,)),
+    ("qz2", (4,)),
+    ("front", (1,)),
     ("load_slot", (6,)),
     ("load_slot", (7,)),
-    ("cp2", (4,)),
-    ("x_half", (3,)),
-    ("x_half", (2,)),
-    ("cp2", (5,)),
-    ("qz2", (4,)),
-    ("cp1", (3,)),
-    ("mh_step", ()),
-    ("mxd", (4,)),
-    ("qz1", (0,)),
-    ("x_copy", (3,)),
-    ("qz2", (5,)),
+    ("front", (3,)),
     ("front", (0,)),
     ("mask", (6,)),
-    ("x_copy", (2,)),
-    ("mxd", (5,)),
-    ("load_x", (2,)),
-    ("cpd", (4,)),
-    ("x_quant", (1,)),
-    ("act", (0, 0)),
-    ("cpd", (5,)),
-    ("load_slot", (8,)),
-    ("tr2", (6,)),
-    ("load_g", (8,)),
-    ("load_slot", (9,)),
-    ("cp2", (6,)),
-    ("front", (1,)),
-    ("act", (1, 0)),
-    ("tr1", (5,)),
-    ("mask", (7,)),
-    ("tr1", (4,)),
-    ("x_half", (4,)),
-    ("act", (0, 1)),
-    ("act", (1, 1)),
-    ("tr2", (7,)),
-    ("x_half", (5,)),
-    ("front", (3,)),
-    ("cp2", (7,)),
-    ("x_copy", (5,)),
-    ("qz2", (6,)),
-    ("mxd", (6,)),
     ("x_copy", (4,)),
-    ("act", (3, 0)),
-    ("qz2", (7,)),
-    ("mxd", (7,)),
-    ("cp1", (5,)),
+    ("act", (1, 1)),
+    ("mask", (7,)),
+    ("qz2", (5,)),
+    ("load_slot", (8,)),
+    ("load_g", (8,)),
+    ("act", (3, 1)),
+    ("load_slot", (9,)),
+    ("x_quant", (2,)),
+    ("act", (0, 1)),
     ("front", (2,)),
+    ("tr2", (6,)),
+    ("act", (1, 0)),
+    ("load_adj", (0,)),
+    ("mxd", (4,)),
+    ("tr2", (7,)),
+    ("cp2", (6,)),
+    ("act", (2, 0)),
+    ("cpd", (4,)),
+    ("mxd", (5,)),
+    ("qz2", (6,)),
+    ("front", (5,)),
+    ("load_g", (10,)),
+    ("act", (2, 1)),
+    ("cp2", (7,)),
+    ("mxd", (6,)),
     ("mask", (8,)),
-    ("cpd", (7,)),
-    ("cpd", (6,)),
     ("mask", (9,)),
     ("tr2", (8,)),
     ("tr2", (9,)),
-    ("act", (3, 1)),
-    ("cp2", (8,)),
-    ("tr1", (6,)),
-    ("load_g", (10,)),
+    ("qz2", (7,)),
+    ("cpd", (6,)),
+    ("n_prep_quant", (0,)),
+    ("cpd", (5,)),
     ("load_slot", (10,)),
-    ("act", (2, 1)),
-    ("load_slot", (11,)),
-    ("act", (2, 0)),
-    ("x_quant", (2,)),
-    ("tr1", (7,)),
-    ("cp1", (7,)),
+    ("tr1", (6,)),
+    ("cp2", (8,)),
     ("cp2", (9,)),
-    ("mask", (10,)),
-    ("front", (4,)),
+    ("act", (3, 0)),
     ("qz2", (8,)),
-    ("mask", (11,)),
-    ("front", (5,)),
-    ("qz2", (9,)),
-    ("mxd", (8,)),
-    ("tr2", (10,)),
-    ("act", (4, 0)),
-    ("load_adj", (0,)),
-    ("tr2", (11,)),
-    ("act", (4, 1)),
-    ("mxd", (9,)),
+    ("mxd", (7,)),
     ("adj_t", (1,)),
-    ("qz1", (1,)),
+    ("mxd", (8,)),
     ("act", (5, 0)),
-    ("cp2", (10,)),
-    ("qz2", (10,)),
-    ("perm_step", ()),
-    ("cp2", (11,)),
-    ("adj_t", (3,)),
-    ("adj_t", (4,)),
-    ("act", (5, 1)),
-    ("a_prep_copy", (0,)),
-    ("cpd", (9,)),
-    ("mxd", (10,)),
-    ("qz2", (11,)),
-    ("cpd", (8,)),
-    ("mxd", (11,)),
-    ("cpd", (10,)),
-    ("stt", (1, 0)),
-    ("stt", (3, 1)),
-    ("cpd", (11,)),
-    ("stt", (3, 0)),
-    ("front", (7,)),
-    ("stt", (4, 1)),
+    ("act", (0, 0)),
     ("adj_t", (0,)),
-    ("adj_t", (5,)),
-    ("act", (7, 1)),
-    ("tr1", (10,)),
-    ("tr1", (8,)),
-    ("stt", (4, 0)),
-    ("stt", (0, 0)),
-    ("act", (7, 0)),
-    ("tr1", (9,)),
-    ("cp1", (9,)),
-    ("front", (6,)),
-    ("stt", (0, 1)),
+    ("qz2", (9,)),
     ("stt", (1, 1)),
-    ("act", (6, 1)),
-    ("act", (6, 0)),
+    ("stt", (1, 0)),
+    ("cpd", (7,)),
+    ("load_slot", (11,)),
+    ("cpd", (8,)),
+    ("tr1", (4,)),
     ("load_adj", (1,)),
-    ("tr1", (11,)),
+    ("front", (4,)),
+    ("stt", (0, 1)),
+    ("tr1", (7,)),
+    ("act", (4, 0)),
+    ("tr1", (5,)),
+    ("mask", (10,)),
+    ("adj_t", (4,)),
+    ("cp1", (5,)),
     ("adj_t", (2,)),
-    ("adj_t", (8,)),
-    ("adj_t", (6,)),
-    ("front", (10,)),
-    ("cp1", (11,)),
-    ("stt", (2, 0)),
-    ("front", (8,)),
-    ("stt", (2, 1)),
-    ("n_prep_copy", (1,)),
-    ("stt", (5, 0)),
-    ("act", (10, 0)),
-    ("adj_t", (7,)),
-    ("stt", (5, 1)),
-    ("row_q", (0, 1)),
-    ("row_q", (0, 3)),
-    ("act", (8, 1)),
-    ("n_prep_copy", (0,)),
-    ("stt", (7, 0)),
-    ("act", (10, 1)),
-    ("act", (8, 0)),
+    ("mxd", (9,)),
+    ("cp1", (7,)),
+    ("stt", (0, 0)),
+    ("act", (5, 1)),
+    ("mask", (11,)),
+    ("tr2", (10,)),
+    ("cp2", (10,)),
+    ("adj_t", (3,)),
+    ("tr2", (11,)),
+    ("qz1", (1,)),
     ("front", (11,)),
-    ("qz1", (2,)),
-    ("front", (9,)),
-    ("row_q", (0, 0)),
-    ("stt", (6, 0)),
-    ("row_q", (0, 2)),
-    ("act", (11, 1)),
+    ("qz2", (10,)),
+    ("cpd", (9,)),
+    ("stt", (4, 0)),
+    ("act", (4, 1)),
+    ("stt", (3, 0)),
+    ("cp2", (11,)),
+    ("tr1", (8,)),
     ("act", (11, 0)),
-    ("act", (9, 0)),
-    ("stt", (6, 1)),
-    ("stt", (7, 1)),
-    ("load_adj", (2,)),
-    ("stt", (8, 0)),
+    ("tr1", (9,)),
+    ("stt", (3, 1)),
+    ("stt", (4, 1)),
+    ("mxd", (10,)),
+    ("cpd", (10,)),
+    ("cp1", (9,)),
+    ("adj_t", (5,)),
+    ("qz2", (11,)),
+    ("front", (7,)),
+    ("stt", (2, 1)),
+    ("act", (7, 1)),
+    ("stt", (2, 0)),
+    ("front", (6,)),
+    ("act", (7, 0)),
+    ("mxd", (11,)),
+    ("perm_step", ()),
+    ("act", (11, 1)),
+    ("front", (9,)),
+    ("stt", (5, 0)),
+    ("cpd", (11,)),
+    ("act", (6, 1)),
+    ("stt", (5, 1)),
+    ("adj_t", (6,)),
+    ("row_q", (0, 0)),
+    ("act", (6, 0)),
+    ("adj_t", (7,)),
+    ("tr1", (11,)),
+    ("row_q", (0, 2)),
+    ("tr1", (10,)),
     ("act", (9, 1)),
-    ("adj_t", (10,)),
-    ("a_prep_copy", (2,)),
+    ("front", (10,)),
+    ("n_prep_copy", (1,)),
+    ("stt", (6, 0)),
+    ("act", (9, 0)),
+    ("cp1", (11,)),
+    ("stt", (7, 0)),
+    ("front", (8,)),
+    ("row_q", (0, 3)),
+    ("act", (10, 0)),
+    ("row_q", (0, 1)),
     ("adj_t", (9,)),
-    ("adj_t", (11,)),
-    ("front", (12,)),
-    ("stt", (8, 1)),
+    ("stt", (7, 1)),
+    ("n_prep_quant", (1,)),
+    ("act", (8, 0)),
+    ("act", (8, 1)),
+    ("adj_t", (8,)),
+    ("load_adj", (2,)),
+    ("act", (10, 1)),
+    ("stt", (6, 1)),
+    ("qz1", (2,)),
     ("row_red", (0,)),
-    ("gadd", (7,)),
-    ("stt", (10, 0)),
-    ("stt", (10, 1)),
-    ("gadd", (6,)),
-    ("stt", (9, 1)),
-    ("front", (17,)),
-    ("gadd", (10,)),
-    ("act", (12, 1)),
-    ("adj_t", (12,)),
-    ("act", (12, 0)),
     ("stt", (9, 0)),
-    ("gadd", (8,)),
-    ("front", (13,)),
-    ("act", (17, 0)),
-    ("stt", (11, 0)),
-    ("adj_t", (15,)),
-    ("act", (13, 1)),
-    ("gadd", (9,)),
-    ("front", (15,)),
-    ("stt", (11, 1)),
-    ("adj_t", (13,)),
-    ("act", (13, 0)),
     ("front", (14,)),
-    ("act", (15, 1)),
-    ("stt", (12, 1)),
-    ("stt", (12, 0)),
-    ("gadd", (11,)),
-    ("adj_t", (14,)),
-    ("row_q", (1, 1)),
-    ("gadd", (12,)),
-    ("stt", (13, 1)),
-    ("stt", (15, 1)),
+    ("adj_t", (10,)),
     ("act", (14, 1)),
-    ("row_q", (1, 2)),
-    ("stt", (13, 0)),
-    ("row_q", (1, 0)),
-    ("row_q", (1, 3)),
+    ("stt", (8, 0)),
+    ("gadd", (6,)),
+    ("adj_t", (11,)),
+    ("gadd", (7,)),
+    ("front", (13,)),
+    ("adj_t", (12,)),
+    ("stt", (8, 1)),
+    ("act", (13, 1)),
     ("act", (14, 0)),
-    ("gadd", (13,)),
-    ("stt", (14, 1)),
+    ("stt", (9, 1)),
+    ("stt", (10, 1)),
+    ("act", (13, 0)),
+    ("front", (12,)),
+    ("front", (17,)),
+    ("gadd", (8,)),
+    ("stt", (10, 0)),
+    ("adj_t", (13,)),
+    ("act", (12, 1)),
+    ("gadd", (9,)),
     ("front", (16,)),
-    ("act", (15, 0)),
+    ("stt", (11, 0)),
+    ("act", (12, 0)),
+    ("stt", (11, 1)),
+    ("gadd", (10,)),
+    ("stt", (12, 1)),
+    ("act", (17, 0)),
+    ("front", (15,)),
+    ("adj_t", (15,)),
+    ("stt", (12, 0)),
     ("act", (17, 1)),
-    ("stt", (15, 0)),
-    ("act", (16, 0)),
-    ("stt", (14, 0)),
-    ("adj_t", (17,)),
-    ("adj_t", (16,)),
+    ("act", (15, 1)),
     ("act", (16, 1)),
+    ("act", (16, 0)),
+    ("adj_t", (14,)),
+    ("gadd", (11,)),
+    ("gadd", (12,)),
+    ("stt", (13, 0)),
+    ("row_q", (1, 3)),
+    ("row_q", (1, 0)),
+    ("stt", (13, 1)),
+    ("row_q", (1, 2)),
+    ("stt", (15, 1)),
+    ("row_q", (1, 1)),
+    ("adj_t", (16,)),
+    ("adj_t", (17,)),
+    ("act", (15, 0)),
+    ("stt", (14, 1)),
+    ("gadd", (13,)),
+    ("stt", (14, 0)),
+    ("stt", (15, 0)),
     ("row_last", (12,)),
-    ("stt", (16, 0)),
+    ("row_red", (1,)),
     ("row_last", (13,)),
-    ("stt", (17, 0)),
     ("stt", (16, 1)),
-    ("row_last", (14,)),
-    ("stt", (17, 1)),
-    ("col_red", ()),
-    ("row_last", (15,)),
     ("a_prep_copy", (1,)),
+    ("row_last", (14,)),
+    ("stt", (16, 0)),
+    ("stt", (17, 0)),
+    ("stt", (17, 1)),
+    ("row_last", (15,)),
+    ("col_red", ()),
+    ("o1_t", (1, 2)),
+    ("o1_t", (0, 1)),
     ("row_last", (16,)),
     ("row_last", (17,)),
-    ("col_mm", ()),
-    ("n_prep_quant", (0,)),
-    ("o1_t", (0, 0)),
-    ("last_red", (2,)),
-    ("row_red", (1,)),
     ("last_red", (1,)),
+    ("col_mm", ()),
     ("last_red", (3,)),
-    ("o1_t", (1, 0)),
-    ("o1_t", (0, 2)),
-    ("o1_t", (1, 2)),
-    ("last_red", (0,)),
-    ("o1_t", (1, 1)),
-    ("q_add", ()),
-    ("o1_t", (2, 2)),
-    ("q_mul", ()),
-    ("o1_t", (3, 2)),
-    ("o1_c", (1, 0)),
-    ("n_prep_copy", (2,)),
-    ("o1_c", (0, 0)),
     ("o1_t", (2, 0)),
-    ("o1_t", (2, 1)),
-    ("o1_t", (4, 0)),
-    ("o1_c", (1, 2)),
-    ("o1_t", (5, 0)),
-    ("o1_c", (3, 2)),
-    ("o1_c", (2, 1)),
-    ("o1_c", (0, 2)),
-    ("o1_store", (0, 0)),
-    ("o1_store", (0, 2)),
-    ("o1_t", (3, 1)),
-    ("o1_c", (1, 1)),
-    ("o1_c", (2, 0)),
-    ("o1_store", (1,)),
-    ("o1_t", (3, 0)),
-    ("n_prep_quant", (1,)),
-    ("o1_t", (4, 2)),
-    ("o1_t", (0, 1)),
-    ("o1_c", (4, 0)),
-    ("o1_c", (2, 2)),
-    ("o1_t", (5, 1)),
-    ("a_prep_quant", (0,)),
-    ("o1_c", (3, 0)),
-    ("o1_t", (5, 2)),
-    ("a_prep_quant", (2,)),
+    ("last_red", (0,)),
+    ("last_red", (2,)),
     ("a_prep_quant", (1,)),
-    ("o1_t", (7, 1)),
-    ("o1_c", (3, 1)),
-    ("n_prep_quant", (2,)),
-    ("o1_t", (7, 2)),
-    ("o1_t", (6, 0)),
+    ("q_add", ()),
+    ("o1_t", (2, 1)),
+    ("q_mul", ()),
     ("o1_c", (0, 1)),
-    ("mxo_mm", (0, 3)),
-    ("o1_store", (2,)),
-    ("o1_c", (5, 1)),
-    ("mxo_mm", (0, 0)),
-    ("o1_c", (5, 2)),
-    ("a_prep_copy", (3,)),
-    ("o1_t", (6, 2)),
-    ("o1_c", (5, 0)),
-    ("o1_store", (3,)),
-    ("mxo_c", (0, 3)),
-    ("o1_t", (6, 1)),
-    ("o1_t", (7, 0)),
-    ("o1_c", (4, 2)),
-    ("o1_c", (6, 2)),
-    ("o1_c", (6, 1)),
-    ("o1_c", (6, 0)),
-    ("o1_c", (7, 1)),
-    ("a_prep_copy", (4,)),
-    ("o1_c", (7, 0)),
-    ("mxo_c", (0, 0)),
-    ("o1_t", (9, 0)),
-    ("o1_t", (4, 1)),
     ("o1_store", (0, 1)),
-    ("o1_c", (4, 1)),
-    ("o1_t", (10, 0)),
-    ("o1_store", (5,)),
-    ("a_prep_quant", (4,)),
-    ("o1_t", (9, 2)),
-    ("o1_t", (9, 1)),
-    ("a_prep_quant", (3,)),
-    ("o1_t", (11, 0)),
-    ("o1_c", (7, 2)),
-    ("o1_c", (9, 2)),
-    ("o1_store", (6,)),
-    ("o1_t", (8, 2)),
-    ("a_prep_copy", (5,)),
-    ("mxo_mm", (0, 2)),
-    ("mxo_mm", (0, 1)),
-    ("a_prep_copy", (7,)),
-    ("mxo_c", (0, 2)),
-    ("o1_t", (8, 1)),
-    ("a_prep_quant", (5,)),
-    ("o1_t", (10, 2)),
-    ("o1_c", (9, 1)),
+    ("o1_t", (0, 0)),
+    ("o1_t", (0, 2)),
+    ("o1_t", (3, 2)),
+    ("o1_c", (2, 0)),
+    ("o1_t", (2, 2)),
+    ("o1_c", (0, 0)),
+    ("o1_t", (1, 1)),
+    ("o1_t", (3, 1)),
+    ("o1_t", (3, 0)),
+    ("o1_c", (0, 2)),
+    ("o1_t", (7, 2)),
+    ("o1_c", (1, 2)),
+    ("o1_c", (2, 2)),
+    ("o1_c", (2, 1)),
+    ("o1_t", (1, 0)),
+    ("o1_store", (0, 0)),
     ("o1_t", (10, 1)),
-    ("o1_store", (7,)),
-    ("mxo_c", (0, 1)),
-    ("o1_c", (9, 0)),
-    ("o1_t", (11, 1)),
+    ("o1_c", (3, 1)),
+    ("o1_c", (1, 1)),
+    ("o1_t", (6, 0)),
+    ("o1_store", (0, 2)),
+    ("o1_c", (3, 2)),
+    ("o1_t", (4, 2)),
+    ("a_prep_copy", (0,)),
+    ("n_prep_copy", (2,)),
+    ("o1_c", (3, 0)),
+    ("a_prep_copy", (4,)),
+    ("o1_store", (2,)),
+    ("a_prep_copy", (2,)),
+    ("o1_t", (4, 1)),
+    ("a_prep_quant", (0,)),
+    ("o1_c", (1, 0)),
+    ("o1_t", (4, 0)),
+    ("a_prep_quant", (2,)),
+    ("o1_t", (7, 0)),
+    ("o1_t", (6, 1)),
+    ("o1_c", (4, 0)),
+    ("o1_t", (7, 1)),
+    ("o1_store", (3,)),
+    ("o1_c", (4, 1)),
+    ("o1_c", (4, 2)),
+    ("o1_c", (6, 1)),
+    ("o1_store", (1,)),
+    ("o1_t", (6, 2)),
+    ("o1_c", (6, 0)),
+    ("o1_c", (6, 2)),
     ("o1_store", (4,)),
-    ("o1_c", (10, 1)),
-    ("o0_store", (0,)),
-    ("o1_t", (11, 2)),
-    ("o1_c", (11, 1)),
-    ("mxo_mm", (1, 2)),
-    ("o1_c", (11, 0)),
-    ("o1_c", (11, 2)),
+    ("o1_c", (7, 0)),
+    ("o1_t", (8, 1)),
+    ("o1_t", (9, 2)),
+    ("o1_t", (5, 2)),
+    ("o1_c", (7, 1)),
+    ("o1_t", (5, 1)),
+    ("o1_store", (6,)),
+    ("o1_c", (7, 2)),
+    ("a_prep_quant", (4,)),
+    ("o1_t", (10, 2)),
+    ("o1_t", (5, 0)),
+    ("o1_store", (7,)),
+    ("n_prep_quant", (2,)),
+    ("o1_c", (5, 2)),
     ("o1_t", (8, 0)),
-    ("mxo_mm", (1, 0)),
-    ("o1_c", (8, 2)),
-    ("mxo_mm", (1, 1)),
-    ("a_prep_copy", (6,)),
-    ("a_prep_copy", (8,)),
-    ("mxo_mm", (1, 3)),
-    ("a_prep_quant", (6,)),
-    ("a_prep_quant", (8,)),
-    ("mxo_c", (1, 0)),
-    ("a_prep_quant", (7,)),
-    ("o1_c", (10, 2)),
-    ("mxo_c", (1, 1)),
-    ("o1_store", (11,)),
-    ("o1_store", (9,)),
-    ("mxo_mm", (2, 3)),
+    ("o1_c", (5, 0)),
+    ("o1_c", (5, 1)),
     ("o1_c", (8, 1)),
+    ("o1_t", (8, 2)),
+    ("a_prep_copy", (3,)),
+    ("o1_c", (8, 0)),
+    ("o1_c", (8, 2)),
+    ("mxo_mm", (0, 1)),
+    ("mxo_mm", (0, 0)),
+    ("mxo_c", (0, 1)),
+    ("a_prep_quant", (3,)),
+    ("mxo_mm", (0, 3)),
+    ("mxo_mm", (0, 2)),
+    ("mxo_c", (0, 0)),
+    ("o1_c", (10, 2)),
+    ("o1_t", (11, 1)),
+    ("o1_store", (5,)),
+    ("o1_t", (9, 1)),
+    ("o1_t", (10, 0)),
+    ("o1_t", (9, 0)),
+    ("o1_c", (10, 1)),
+    ("a_prep_copy", (5,)),
+    ("mxo_c", (0, 2)),
+    ("o1_store", (8,)),
+    ("mxo_c", (0, 3)),
+    ("a_prep_copy", (6,)),
+    ("o1_t", (11, 0)),
+    ("o1_t", (11, 2)),
+    ("a_prep_quant", (5,)),
     ("o1_c", (10, 0)),
+    ("mxo_mm", (1, 2)),
+    ("o1_c", (9, 1)),
+    ("o0_store", (0,)),
+    ("o1_c", (11, 0)),
+    ("o1_c", (9, 0)),
+    ("a_prep_copy", (8,)),
+    ("mxo_mm", (1, 0)),
+    ("mxo_mm", (1, 1)),
+    ("mxo_c", (1, 1)),
+    ("mxo_mm", (1, 3)),
+    ("o1_store", (10,)),
+    ("o1_c", (11, 1)),
+    ("o1_c", (9, 2)),
+    ("a_prep_quant", (6,)),
+    ("o1_c", (11, 2)),
+    ("a_prep_copy", (7,)),
+    ("a_prep_quant", (7,)),
+    ("mxo_c", (1, 0)),
+    ("a_prep_quant", (8,)),
+    ("mxo_mm", (2, 1)),
+    ("mxo_mm", (2, 3)),
+    ("o1_store", (9,)),
+    ("o1_store", (11,)),
     ("mxo_c", (1, 2)),
-    ("mxo_mm", (2, 0)),
+    ("mxo_c", (2, 1)),
     ("mxo_c", (1, 3)),
-    ("mxo_c", (2, 0)),
     ("mxo_mm", (2, 2)),
+    ("mxo_mm", (2, 0)),
+    ("o0_store", (1,)),
     ("mxo_c", (2, 2)),
     ("mxo_c", (2, 3)),
-    ("mxo_mm", (2, 1)),
-    ("mxo_c", (2, 1)),
-    ("o1_store", (10,)),
-    ("o0_store", (1,)),
-    ("o1_c", (8, 0)),
-    ("o1_store", (8,)),
+    ("mxo_c", (2, 0)),
     ("o0_store", (2,))
 ]
 
@@ -462,7 +462,7 @@ def tile_simplegcn_pa_v_kernel(tc, x, adj, W1, b1, z, rdeg, grad_out, out_0, out
     go_v = grad_out.rearrange("(g p s) k -> p g s k", g=G, s=S)
     d_v = rdeg.rearrange("(g p s) -> p g s", g=G, s=S)
     d2_v = rdeg.rearrange("(b p e) -> p b e", b=B, e=E)
-    o0_v = out_0.rearrange("(g p s) f -> p g s f", g=G, s=S)
+    o0_v = out_0.rearrange("(b p e) f -> p b e f", b=B, e=E)
     o1_v = out_1.rearrange("(g p s) w -> p g s w", g=G, s=S)
     NZ = 3
     NS = G * S
@@ -610,11 +610,7 @@ def tile_simplegcn_pa_v_kernel(tc, x, adj, W1, b1, z, rdeg, grad_out, out_0, out
         def mask(n):
             if not 0 <= n < NS:
                 return
-            zt, g_, o = buf4[n % NZ][:], gt[n // 2 % 2][:, n % 2, :], dz2[n % 2][:].rearrange("p (u q e) -> p u q e", u=2, e=2)
-            for u in range(2):
-                nc.vector.scalar_tensor_tensor(
-                    out=o[:, u, :, :], in0=zt.rearrange("p (q u e) -> p u q e", u=2, e=2)[:, u, :, :], scalar=0.0,
-                    in1=g_.rearrange("p (q u e) -> p u q e", u=2, e=2)[:, u, :, :], op0=ALU.is_gt, op1=ALU.mult)
+            nc.vector.scalar_tensor_tensor(out=dz2[n % 2][:], in0=buf4[n % NZ][:], scalar=0.0, in1=gt[n // 2 % 2][:, n % 2, :], op0=ALU.is_gt, op1=ALU.mult)
 
         def tr2(n):
             if not 0 <= n < NS:
@@ -623,7 +619,7 @@ def tile_simplegcn_pa_v_kernel(tc, x, adj, W1, b1, z, rdeg, grad_out, out_0, out
             ps = take(("t2", n), 1)[:].rearrange("p (c u t) -> p c u t", c=2, u=2)
             for c in range(2):
                 for u in range(2):
-                    nc.tensor.transpose(ps[:, c, u, :], words[:, u * 256 + c * P:u * 256 + (c + 1) * P], ident[:])
+                    nc.tensor.transpose(ps[:, c, u, :], words[:, c * 256 + u:(c + 1) * 256:2], ident[:])
 
         def cp2(n):
             ps = last(("t2", n))[:].rearrange("p (c u t) -> p c u t", c=2, u=2)
@@ -727,7 +723,7 @@ def tile_simplegcn_pa_v_kernel(tc, x, adj, W1, b1, z, rdeg, grad_out, out_0, out
 
         def a_prep_copy(i):
             g, h = i % G, i // G
-            o, i_ = a_buf(i).rearrange("p (a b s) -> p a b s", a=S, s=S), adj_sb[:, g, :, h * W:(h + 1) * W].rearrange("p s (b a) -> p a b s", a=S)
+            o, i_ = a_buf(i).rearrange("p (e k s) -> p e k s", e=E, s=S), adj_sb[:, g, :, h * W:(h + 1) * W].rearrange("p s (k e) -> p e k s", e=E)
             weave("a_prep_copy", i, o, i_)
 
         def a_prep_quant(i):
@@ -741,12 +737,13 @@ def tile_simplegcn_pa_v_kernel(tc, x, adj, W1, b1, z, rdeg, grad_out, out_0, out
                                     rhs=nq[g][:].bitcast(E5M2), rhs_scale=nqs[g][:], start=(g == 0), stop=(g == G - 1))
 
         def mxo_c(h, s):
-            o = o0[h % 2][:, s, :].rearrange("p (q u e) -> p q u e", u=2, e=2)
+            o = o0[h % 2][:, E * (s % 2) + s // 2, :].rearrange("p (q u e) -> p q u e", u=2, e=2)
             i = last(("o0", h, s))[:].rearrange("p (u q e) -> p q u e", u=2, e=2)
-            move("mxo_c", (h, s), o, i, scale=d_sb[:, S * h + s:S * h + s + 1])
+            b, e = 2 * h + s % 2, s // 2
+            move("mxo_c", (h, s), o, i, scale=d2_sb[:, b * E + e:b * E + e + 1])
 
         def o0_store(h):
-            nc.sync.dma_start(out=o0_v[:, h, :, :], in_=o0[h % 2][:])
+            nc.sync.dma_start(out=o0_v[:, 2 * h:2 * h + 2, :, :], in_=o0[h % 2][:].rearrange("p (b e) f -> p b e f", b=2))
 
         def o1_t(n, h):
             g, s = n // S, n % S

@@ -25,430 +25,438 @@ ACT = mybir.ActivationFunctionType
 AX = mybir.AxisListType
 
 
-GADD = (6, 7, 8, 9, 10, 11, 12, 13)
-VEC = {"o1_c": ((0, 1), (0, 0), (1, 2), (2, 1), (3, 1), (8, 2), (9, 1), (9, 2),), "mxo_c": ((0, 3), (1, 2), (1, 3), (2, 3),)}
-SCA = {"a_prep_copy": ((1,), (8,),)}
+GADD = (0, 1, 2, 3, 4, 5, 6, 7, 8, 9, 10, 11, 12, 13, 14, 15)
+VEC = {"cp2": ((1,), (8,),), "cpd": ((0,), (6,),), "act": ((5, 0), (6, 1),), "o1_c": ((0, 2), (1, 2), (2, 2), (4, 0), (7, 0), (7, 1), (6, 1), (9, 0), (11, 0), (11, 2), (10, 2),), "mxo_c": ((1, 3), (1, 0), (2, 3), (2, 2), (2, 0),)}
+SCA = {"a_prep_copy": ((2,), (5,), (6,),), "w_copy": ((1,),)}
 GPS = {}
 ORDER = [
     ("load_slot", (1,)),
+    ("identity", ()),
     ("load_g", (0,)),
-    ("load_w", (0,)),
     ("load_slot", (0,)),
     ("mask", (1,)),
-    ("load_w", (1,)),
-    ("identity", ()),
     ("tr2", (1,)),
-    ("load_x", (0,)),
-    ("load_g", (2,)),
-    ("w_copy", (0,)),
-    ("cp2", (1,)),
-    ("mask", (0,)),
-    ("tr2", (0,)),
-    ("w_quant", (0,)),
+    ("load_w", (1,)),
     ("w_copy", (1,)),
-    ("x_half", (0,)),
-    ("load_slot", (2,)),
-    ("cp2", (0,)),
-    ("load_slot", (3,)),
+    ("mask", (0,)),
+    ("load_w", (0,)),
+    ("cp2", (1,)),
+    ("load_x", (0,)),
     ("load_d", ()),
+    ("load_g", (2,)),
+    ("tr2", (0,)),
+    ("load_slot", (2,)),
     ("qz2", (1,)),
-    ("qz2", (0,)),
-    ("load_x", (1,)),
+    ("w_copy", (0,)),
+    ("x_half", (0,)),
+    ("x_half", (1,)),
+    ("load_slot", (3,)),
     ("w_quant", (1,)),
+    ("w_quant", (0,)),
+    ("cp2", (0,)),
+    ("qz2", (0,)),
+    ("mxd", (0,)),
+    ("mxd", (1,)),
+    ("load_g", (4,)),
     ("mask", (2,)),
     ("mask", (3,)),
-    ("x_half", (1,)),
-    ("mxd", (1,)),
     ("x_copy", (1,)),
-    ("load_g", (4,)),
-    ("x_copy", (0,)),
-    ("cpd", (1,)),
-    ("mxd", (0,)),
-    ("tr2", (2,)),
-    ("load_slot", (5,)),
-    ("cpd", (0,)),
-    ("tr1", (1,)),
-    ("cp2", (2,)),
-    ("tr2", (3,)),
     ("load_slot", (4,)),
-    ("cp2", (3,)),
-    ("x_half", (2,)),
-    ("x_quant", (0,)),
-    ("qz2", (2,)),
-    ("load_x", (2,)),
-    ("x_half", (3,)),
-    ("x_copy", (2,)),
-    ("qz2", (3,)),
-    ("mask", (5,)),
-    ("mxd", (2,)),
-    ("x_copy", (3,)),
-    ("mh_step", ()),
-    ("load_g", (6,)),
-    ("mxd", (3,)),
-    ("cpd", (2,)),
+    ("cpd", (0,)),
+    ("load_slot", (5,)),
+    ("tr2", (2,)),
+    ("tr2", (3,)),
     ("tr1", (0,)),
-    ("tr1", (2,)),
-    ("cpd", (3,)),
-    ("cp1", (1,)),
-    ("tr1", (3,)),
+    ("cpd", (1,)),
+    ("cp2", (2,)),
+    ("tr1", (1,)),
+    ("qz2", (2,)),
+    ("x_copy", (0,)),
+    ("load_x", (2,)),
+    ("mxd", (2,)),
     ("mask", (4,)),
+    ("cp2", (3,)),
+    ("tr2", (4,)),
+    ("qz2", (3,)),
+    ("cp1", (1,)),
+    ("mh_step", ()),
+    ("mask", (5,)),
+    ("mxd", (3,)),
+    ("load_slot", (6,)),
+    ("x_quant", (0,)),
+    ("load_g", (6,)),
+    ("cpd", (2,)),
+    ("tr1", (2,)),
+    ("cp2", (4,)),
+    ("qz2", (4,)),
+    ("load_x", (1,)),
     ("tr2", (5,)),
     ("x_half", (5,)),
-    ("tr2", (4,)),
-    ("x_quant", (1,)),
-    ("cp1", (3,)),
+    ("cpd", (3,)),
+    ("tr1", (3,)),
     ("x_half", (4,)),
-    ("cp2", (5,)),
-    ("x_copy", (5,)),
-    ("cp2", (4,)),
-    ("load_d2", ()),
-    ("qz1", (0,)),
     ("n_prep_copy", (0,)),
-    ("qz2", (4,)),
-    ("front", (1,)),
-    ("load_slot", (6,)),
+    ("load_d2", ()),
     ("load_slot", (7,)),
-    ("front", (3,)),
-    ("front", (0,)),
-    ("mask", (6,)),
-    ("x_copy", (4,)),
-    ("act", (1, 1)),
-    ("mask", (7,)),
-    ("qz2", (5,)),
-    ("load_slot", (8,)),
-    ("load_g", (8,)),
-    ("act", (3, 1)),
-    ("load_slot", (9,)),
-    ("x_quant", (2,)),
-    ("act", (0, 1)),
-    ("front", (2,)),
-    ("tr2", (6,)),
-    ("act", (1, 0)),
-    ("load_adj", (0,)),
+    ("cp2", (5,)),
     ("mxd", (4,)),
-    ("tr2", (7,)),
-    ("cp2", (6,)),
-    ("act", (2, 0)),
+    ("x_half", (2,)),
+    ("qz2", (5,)),
+    ("cp1", (3,)),
+    ("x_copy", (4,)),
+    ("mask", (6,)),
+    ("x_copy", (5,)),
+    ("qz1", (0,)),
+    ("x_quant", (2,)),
     ("cpd", (4,)),
+    ("tr2", (6,)),
+    ("x_half", (3,)),
+    ("load_g", (8,)),
+    ("front", (1,)),
+    ("mask", (7,)),
+    ("x_copy", (2,)),
     ("mxd", (5,)),
+    ("front", (0,)),
+    ("cp2", (6,)),
+    ("x_copy", (3,)),
+    ("act", (1, 1)),
+    ("load_slot", (8,)),
+    ("x_quant", (1,)),
+    ("act", (1, 0)),
     ("qz2", (6,)),
     ("front", (5,)),
-    ("load_g", (10,)),
-    ("act", (2, 1)),
-    ("cp2", (7,)),
-    ("mxd", (6,)),
+    ("tr2", (7,)),
     ("mask", (8,)),
-    ("mask", (9,)),
-    ("tr2", (8,)),
-    ("tr2", (9,)),
-    ("qz2", (7,)),
-    ("cpd", (6,)),
-    ("n_prep_quant", (0,)),
     ("cpd", (5,)),
-    ("load_slot", (10,)),
-    ("tr1", (6,)),
-    ("cp2", (8,)),
-    ("cp2", (9,)),
-    ("act", (3, 0)),
-    ("qz2", (8,)),
-    ("mxd", (7,)),
-    ("adj_t", (1,)),
-    ("mxd", (8,)),
-    ("act", (5, 0)),
-    ("act", (0, 0)),
-    ("adj_t", (0,)),
-    ("qz2", (9,)),
-    ("stt", (1, 1)),
-    ("stt", (1, 0)),
-    ("cpd", (7,)),
-    ("load_slot", (11,)),
-    ("cpd", (8,)),
-    ("tr1", (4,)),
-    ("load_adj", (1,)),
     ("front", (4,)),
-    ("stt", (0, 1)),
-    ("tr1", (7,)),
-    ("act", (4, 0)),
-    ("tr1", (5,)),
-    ("mask", (10,)),
-    ("adj_t", (4,)),
-    ("cp1", (5,)),
-    ("adj_t", (2,)),
-    ("mxd", (9,)),
-    ("cp1", (7,)),
-    ("stt", (0, 0)),
-    ("act", (5, 1)),
-    ("mask", (11,)),
-    ("tr2", (10,)),
-    ("cp2", (10,)),
-    ("adj_t", (3,)),
-    ("tr2", (11,)),
-    ("qz1", (1,)),
-    ("front", (11,)),
-    ("qz2", (10,)),
-    ("cpd", (9,)),
-    ("stt", (4, 0)),
-    ("act", (4, 1)),
-    ("stt", (3, 0)),
-    ("cp2", (11,)),
-    ("tr1", (8,)),
-    ("act", (11, 0)),
-    ("tr1", (9,)),
-    ("stt", (3, 1)),
-    ("stt", (4, 1)),
-    ("mxd", (10,)),
-    ("cpd", (10,)),
-    ("cp1", (9,)),
-    ("adj_t", (5,)),
-    ("qz2", (11,)),
-    ("front", (7,)),
-    ("stt", (2, 1)),
-    ("act", (7, 1)),
-    ("stt", (2, 0)),
-    ("front", (6,)),
-    ("act", (7, 0)),
-    ("mxd", (11,)),
     ("perm_step", ()),
-    ("act", (11, 1)),
-    ("front", (9,)),
-    ("stt", (5, 0)),
-    ("cpd", (11,)),
-    ("act", (6, 1)),
+    ("act", (5, 1)),
+    ("cp2", (7,)),
+    ("load_slot", (9,)),
+    ("tr2", (8,)),
+    ("act", (4, 0)),
+    ("mxd", (6,)),
+    ("mask", (9,)),
+    ("load_adj", (0,)),
+    ("tr1", (5,)),
+    ("act", (0, 0)),
+    ("cp2", (8,)),
+    ("tr2", (9,)),
+    ("act", (0, 1)),
+    ("load_slot", (11,)),
+    ("load_slot", (10,)),
+    ("qz2", (7,)),
+    ("cp2", (9,)),
+    ("tr1", (4,)),
+    ("cpd", (6,)),
+    ("qz2", (8,)),
+    ("act", (5, 0)),
+    ("mxd", (7,)),
+    ("act", (4, 1)),
+    ("adj_t", (5,)),
+    ("tr1", (6,)),
+    ("front", (3,)),
+    ("cpd", (7,)),
+    ("adj_t", (1,)),
+    ("tr1", (7,)),
+    ("cp1", (5,)),
+    ("front", (2,)),
+    ("act", (3, 0)),
+    ("qz2", (9,)),
     ("stt", (5, 1)),
-    ("adj_t", (6,)),
-    ("row_q", (0, 0)),
+    ("stt", (5, 0)),
+    ("cp1", (7,)),
+    ("load_g", (10,)),
+    ("mxd", (8,)),
+    ("stt", (1, 0)),
+    ("act", (2, 0)),
+    ("adj_t", (2,)),
+    ("act", (2, 1)),
+    ("stt", (1, 1)),
+    ("qz1", (1,)),
+    ("mxd", (9,)),
+    ("load_adj", (1,)),
+    ("cpd", (8,)),
+    ("act", (3, 1)),
+    ("mask", (11,)),
+    ("front", (6,)),
+    ("mask", (10,)),
     ("act", (6, 0)),
-    ("adj_t", (7,)),
-    ("tr1", (11,)),
-    ("row_q", (0, 2)),
-    ("tr1", (10,)),
-    ("act", (9, 1)),
-    ("front", (10,)),
-    ("n_prep_copy", (1,)),
-    ("stt", (6, 0)),
-    ("act", (9, 0)),
-    ("cp1", (11,)),
-    ("stt", (7, 0)),
-    ("front", (8,)),
-    ("row_q", (0, 3)),
-    ("act", (10, 0)),
-    ("row_q", (0, 1)),
-    ("adj_t", (9,)),
-    ("stt", (7, 1)),
-    ("n_prep_quant", (1,)),
-    ("act", (8, 0)),
-    ("act", (8, 1)),
-    ("adj_t", (8,)),
+    ("cpd", (9,)),
+    ("tr1", (8,)),
+    ("front", (11,)),
+    ("tr2", (11,)),
+    ("adj_t", (4,)),
+    ("stt", (2, 0)),
+    ("gadd", (5,)),
+    ("tr1", (9,)),
+    ("act", (11, 1)),
+    ("tr2", (10,)),
+    ("adj_t", (0,)),
+    ("act", (6, 1)),
+    ("cp2", (11,)),
+    ("act", (11, 0)),
+    ("front", (7,)),
     ("load_adj", (2,)),
-    ("act", (10, 1)),
+    ("stt", (2, 1)),
+    ("cp2", (10,)),
+    ("qz2", (11,)),
+    ("stt", (0, 1)),
+    ("adj_t", (3,)),
+    ("stt", (0, 0)),
+    ("front", (9,)),
+    ("act", (7, 0)),
+    ("act", (7, 1)),
+    ("adj_t", (7,)),
+    ("stt", (4, 0)),
+    ("stt", (4, 1)),
+    ("gadd", (1,)),
+    ("cp1", (9,)),
+    ("gadd", (2,)),
+    ("qz2", (10,)),
+    ("stt", (3, 0)),
+    ("front", (8,)),
+    ("mxd", (11,)),
+    ("act", (9, 0)),
+    ("act", (9, 1)),
+    ("mxd", (10,)),
+    ("stt", (3, 1)),
+    ("adj_t", (6,)),
+    ("stt", (7, 1)),
+    ("front", (10,)),
+    ("cpd", (11,)),
+    ("tr1", (11,)),
+    ("cpd", (10,)),
+    ("act", (8, 0)),
+    ("gadd", (0,)),
+    ("gadd", (4,)),
+    ("stt", (7, 0)),
+    ("stt", (6, 0)),
+    ("adj_t", (8,)),
+    ("gadd", (3,)),
     ("stt", (6, 1)),
+    ("act", (8, 1)),
+    ("tr1", (10,)),
+    ("cp1", (11,)),
+    ("row_q", (0, 1)),
+    ("row_q", (0, 0)),
+    ("act", (10, 1)),
+    ("gadd", (7,)),
+    ("row_q", (0, 3)),
+    ("row_q", (0, 2)),
+    ("stt", (8, 1)),
+    ("adj_t", (11,)),
     ("qz1", (2,)),
+    ("act", (10, 0)),
+    ("adj_t", (14,)),
+    ("stt", (8, 0)),
+    ("adj_t", (9,)),
+    ("adj_t", (12,)),
+    ("front", (12,)),
+    ("stt", (11, 1)),
     ("row_red", (0,)),
+    ("stt", (11, 0)),
+    ("act", (12, 1)),
+    ("adj_t", (10,)),
+    ("act", (12, 0)),
+    ("front", (13,)),
     ("stt", (9, 0)),
     ("front", (14,)),
-    ("adj_t", (10,)),
-    ("act", (14, 1)),
-    ("stt", (8, 0)),
-    ("gadd", (6,)),
-    ("adj_t", (11,)),
-    ("gadd", (7,)),
-    ("front", (13,)),
-    ("adj_t", (12,)),
-    ("stt", (8, 1)),
-    ("act", (13, 1)),
-    ("act", (14, 0)),
-    ("stt", (9, 1)),
-    ("stt", (10, 1)),
-    ("act", (13, 0)),
-    ("front", (12,)),
-    ("front", (17,)),
-    ("gadd", (8,)),
     ("stt", (10, 0)),
-    ("adj_t", (13,)),
-    ("act", (12, 1)),
-    ("gadd", (9,)),
-    ("front", (16,)),
-    ("stt", (11, 0)),
-    ("act", (12, 0)),
-    ("stt", (11, 1)),
-    ("gadd", (10,)),
+    ("act", (13, 0)),
+    ("act", (13, 1)),
+    ("gadd", (8,)),
+    ("gadd", (6,)),
+    ("stt", (10, 1)),
+    ("stt", (9, 1)),
+    ("gadd", (11,)),
+    ("front", (17,)),
     ("stt", (12, 1)),
+    ("gadd", (10,)),
+    ("front", (16,)),
+    ("act", (14, 0)),
+    ("act", (14, 1)),
+    ("stt", (12, 0)),
+    ("gadd", (9,)),
+    ("stt", (14, 1)),
+    ("gadd", (12,)),
+    ("adj_t", (13,)),
+    ("act", (17, 1)),
+    ("stt", (13, 1)),
     ("act", (17, 0)),
     ("front", (15,)),
-    ("adj_t", (15,)),
-    ("stt", (12, 0)),
-    ("act", (17, 1)),
+    ("row_q", (1, 1)),
     ("act", (15, 1)),
-    ("act", (16, 1)),
-    ("act", (16, 0)),
-    ("adj_t", (14,)),
-    ("gadd", (11,)),
-    ("gadd", (12,)),
-    ("stt", (13, 0)),
+    ("row_q", (1, 2)),
     ("row_q", (1, 3)),
     ("row_q", (1, 0)),
-    ("stt", (13, 1)),
-    ("row_q", (1, 2)),
-    ("stt", (15, 1)),
-    ("row_q", (1, 1)),
-    ("adj_t", (16,)),
-    ("adj_t", (17,)),
+    ("adj_t", (15,)),
+    ("stt", (13, 0)),
     ("act", (15, 0)),
-    ("stt", (14, 1)),
+    ("act", (16, 1)),
+    ("act", (16, 0)),
+    ("row_last", (12,)),
     ("gadd", (13,)),
     ("stt", (14, 0)),
+    ("gadd", (14,)),
+    ("adj_t", (16,)),
+    ("stt", (15, 1)),
     ("stt", (15, 0)),
-    ("row_last", (12,)),
     ("row_red", (1,)),
-    ("row_last", (13,)),
     ("stt", (16, 1)),
-    ("a_prep_copy", (1,)),
-    ("row_last", (14,)),
+    ("adj_t", (17,)),
     ("stt", (16, 0)),
     ("stt", (17, 0)),
+    ("row_last", (13,)),
+    ("row_last", (14,)),
+    ("o1_t", (0, 2)),
+    ("gadd", (15,)),
+    ("o1_t", (0, 0)),
     ("stt", (17, 1)),
     ("row_last", (15,)),
-    ("col_red", ()),
-    ("o1_t", (1, 2)),
-    ("o1_t", (0, 1)),
+    ("n_prep_quant", (0,)),
     ("row_last", (16,)),
+    ("col_red", ()),
     ("row_last", (17,)),
-    ("last_red", (1,)),
-    ("col_mm", ()),
-    ("last_red", (3,)),
-    ("o1_t", (2, 0)),
+    ("a_prep_copy", (2,)),
     ("last_red", (0,)),
-    ("last_red", (2,)),
-    ("a_prep_quant", (1,)),
-    ("q_add", ()),
+    ("last_red", (1,)),
+    ("last_red", (3,)),
     ("o1_t", (2, 1)),
+    ("last_red", (2,)),
+    ("a_prep_quant", (2,)),
+    ("col_mm", ()),
+    ("o1_t", (1, 0)),
+    ("q_add", ()),
+    ("o1_t", (3, 0)),
+    ("o1_t", (0, 1)),
     ("q_mul", ()),
-    ("o1_c", (0, 1)),
-    ("o1_store", (0, 1)),
-    ("o1_t", (0, 0)),
-    ("o1_t", (0, 2)),
-    ("o1_t", (3, 2)),
-    ("o1_c", (2, 0)),
-    ("o1_t", (2, 2)),
     ("o1_c", (0, 0)),
     ("o1_t", (1, 1)),
-    ("o1_t", (3, 1)),
-    ("o1_t", (3, 0)),
-    ("o1_c", (0, 2)),
-    ("o1_t", (7, 2)),
-    ("o1_c", (1, 2)),
-    ("o1_c", (2, 2)),
-    ("o1_c", (2, 1)),
-    ("o1_t", (1, 0)),
     ("o1_store", (0, 0)),
-    ("o1_t", (10, 1)),
-    ("o1_c", (3, 1)),
-    ("o1_c", (1, 1)),
-    ("o1_t", (6, 0)),
-    ("o1_store", (0, 2)),
-    ("o1_c", (3, 2)),
-    ("o1_t", (4, 2)),
-    ("a_prep_copy", (0,)),
-    ("n_prep_copy", (2,)),
-    ("o1_c", (3, 0)),
-    ("a_prep_copy", (4,)),
-    ("o1_store", (2,)),
-    ("a_prep_copy", (2,)),
+    ("a_prep_copy", (1,)),
+    ("o1_c", (0, 1)),
+    ("o1_c", (0, 2)),
     ("o1_t", (4, 1)),
-    ("a_prep_quant", (0,)),
     ("o1_c", (1, 0)),
+    ("o1_c", (1, 1)),
+    ("o1_t", (1, 2)),
+    ("o1_t", (2, 2)),
+    ("o1_c", (3, 0)),
+    ("o1_t", (3, 2)),
+    ("o1_c", (1, 2)),
+    ("o1_c", (3, 2)),
+    ("o1_t", (3, 1)),
+    ("o1_t", (5, 1)),
+    ("o1_store", (0, 1)),
+    ("o1_t", (4, 2)),
+    ("o1_c", (3, 1)),
     ("o1_t", (4, 0)),
-    ("a_prep_quant", (2,)),
-    ("o1_t", (7, 0)),
-    ("o1_t", (6, 1)),
-    ("o1_c", (4, 0)),
-    ("o1_t", (7, 1)),
-    ("o1_store", (3,)),
-    ("o1_c", (4, 1)),
-    ("o1_c", (4, 2)),
-    ("o1_c", (6, 1)),
+    ("o1_t", (2, 0)),
+    ("n_prep_copy", (1,)),
+    ("o1_t", (8, 0)),
+    ("o1_store", (0, 2)),
+    ("o1_c", (2, 1)),
+    ("o1_c", (2, 2)),
     ("o1_store", (1,)),
+    ("o1_c", (4, 2)),
+    ("o1_store", (3,)),
+    ("o1_t", (5, 2)),
+    ("o1_t", (6, 1)),
+    ("o1_c", (2, 0)),
+    ("o1_t", (8, 1)),
+    ("o1_c", (4, 1)),
+    ("n_prep_copy", (2,)),
+    ("o1_t", (5, 0)),
+    ("o1_t", (7, 0)),
+    ("o1_c", (4, 0)),
+    ("a_prep_copy", (0,)),
+    ("o1_t", (7, 2)),
+    ("n_prep_quant", (1,)),
+    ("o1_store", (2,)),
+    ("a_prep_quant", (1,)),
+    ("o1_c", (5, 1)),
+    ("a_prep_quant", (0,)),
+    ("o1_t", (6, 0)),
+    ("o1_c", (5, 2)),
+    ("o1_t", (7, 1)),
+    ("o1_c", (5, 0)),
+    ("o1_c", (7, 2)),
+    ("o1_c", (7, 0)),
+    ("n_prep_quant", (2,)),
+    ("a_prep_copy", (5,)),
     ("o1_t", (6, 2)),
+    ("o1_c", (7, 1)),
+    ("o1_c", (6, 1)),
     ("o1_c", (6, 0)),
+    ("mxo_mm", (0, 0)),
     ("o1_c", (6, 2)),
     ("o1_store", (4,)),
-    ("o1_c", (7, 0)),
-    ("o1_t", (8, 1)),
-    ("o1_t", (9, 2)),
-    ("o1_t", (5, 2)),
-    ("o1_c", (7, 1)),
-    ("o1_t", (5, 1)),
-    ("o1_store", (6,)),
-    ("o1_c", (7, 2)),
-    ("a_prep_quant", (4,)),
-    ("o1_t", (10, 2)),
-    ("o1_t", (5, 0)),
-    ("o1_store", (7,)),
-    ("n_prep_quant", (2,)),
-    ("o1_c", (5, 2)),
-    ("o1_t", (8, 0)),
-    ("o1_c", (5, 0)),
-    ("o1_c", (5, 1)),
-    ("o1_c", (8, 1)),
     ("o1_t", (8, 2)),
-    ("a_prep_copy", (3,)),
+    ("o1_t", (9, 1)),
+    ("o1_t", (9, 0)),
+    ("a_prep_copy", (4,)),
+    ("o1_c", (8, 1)),
     ("o1_c", (8, 0)),
-    ("o1_c", (8, 2)),
+    ("o1_t", (11, 0)),
     ("mxo_mm", (0, 1)),
-    ("mxo_mm", (0, 0)),
-    ("mxo_c", (0, 1)),
-    ("a_prep_quant", (3,)),
-    ("mxo_mm", (0, 3)),
-    ("mxo_mm", (0, 2)),
-    ("mxo_c", (0, 0)),
-    ("o1_c", (10, 2)),
+    ("o1_c", (8, 2)),
+    ("o1_t", (9, 2)),
     ("o1_t", (11, 1)),
     ("o1_store", (5,)),
-    ("o1_t", (9, 1)),
-    ("o1_t", (10, 0)),
-    ("o1_t", (9, 0)),
-    ("o1_c", (10, 1)),
-    ("a_prep_copy", (5,)),
-    ("mxo_c", (0, 2)),
-    ("o1_store", (8,)),
-    ("mxo_c", (0, 3)),
-    ("a_prep_copy", (6,)),
-    ("o1_t", (11, 0)),
-    ("o1_t", (11, 2)),
     ("a_prep_quant", (5,)),
+    ("o1_t", (11, 2)),
+    ("o1_c", (9, 1)),
+    ("a_prep_copy", (3,)),
+    ("o1_t", (10, 1)),
+    ("o1_c", (9, 0)),
+    ("mxo_mm", (0, 3)),
+    ("o1_store", (7,)),
+    ("o1_c", (11, 0)),
+    ("o1_c", (11, 2)),
+    ("o1_c", (9, 2)),
+    ("o1_store", (6,)),
+    ("mxo_mm", (0, 2)),
+    ("a_prep_quant", (4,)),
+    ("o1_c", (11, 1)),
+    ("mxo_c", (0, 1)),
+    ("mxo_c", (0, 0)),
+    ("mxo_c", (0, 3)),
+    ("o1_t", (10, 2)),
+    ("a_prep_quant", (3,)),
+    ("a_prep_copy", (8,)),
+    ("mxo_c", (0, 2)),
+    ("a_prep_copy", (6,)),
+    ("a_prep_copy", (7,)),
+    ("o1_t", (10, 0)),
+    ("mxo_mm", (1, 3)),
+    ("o1_store", (8,)),
+    ("mxo_mm", (1, 0)),
+    ("o1_store", (11,)),
     ("o1_c", (10, 0)),
     ("mxo_mm", (1, 2)),
-    ("o1_c", (9, 1)),
-    ("o0_store", (0,)),
-    ("o1_c", (11, 0)),
-    ("o1_c", (9, 0)),
-    ("a_prep_copy", (8,)),
-    ("mxo_mm", (1, 0)),
-    ("mxo_mm", (1, 1)),
-    ("mxo_c", (1, 1)),
-    ("mxo_mm", (1, 3)),
-    ("o1_store", (10,)),
-    ("o1_c", (11, 1)),
-    ("o1_c", (9, 2)),
-    ("a_prep_quant", (6,)),
-    ("o1_c", (11, 2)),
-    ("a_prep_copy", (7,)),
+    ("o1_c", (10, 2)),
+    ("o1_c", (10, 1)),
     ("a_prep_quant", (7,)),
-    ("mxo_c", (1, 0)),
+    ("a_prep_quant", (6,)),
+    ("o1_store", (9,)),
+    ("mxo_c", (1, 2)),
+    ("o0_store", (0,)),
+    ("mxo_mm", (1, 1)),
     ("a_prep_quant", (8,)),
     ("mxo_mm", (2, 1)),
-    ("mxo_mm", (2, 3)),
-    ("o1_store", (9,)),
-    ("o1_store", (11,)),
-    ("mxo_c", (1, 2)),
-    ("mxo_c", (2, 1)),
     ("mxo_c", (1, 3)),
+    ("mxo_c", (1, 1)),
+    ("mxo_mm", (2, 3)),
     ("mxo_mm", (2, 2)),
-    ("mxo_mm", (2, 0)),
-    ("o0_store", (1,)),
-    ("mxo_c", (2, 2)),
+    ("mxo_c", (1, 0)),
+    ("mxo_c", (2, 1)),
     ("mxo_c", (2, 3)),
+    ("mxo_c", (2, 2)),
+    ("mxo_mm", (2, 0)),
+    ("o1_store", (10,)),
     ("mxo_c", (2, 0)),
+    ("o0_store", (1,)),
     ("o0_store", (2,))
 ]
 

from contextlib import ExitStack

import concourse.mybir as mybir
from concourse.masks import make_identity

N, IN, HID = 1536, 512, 1024
P = 128
G = 3
S = 4
B = 6
E = 2
W = 512

FLOPS = 2 * N * HID * IN + 2 * 2 * N * N * IN
BYTES = 2 * (N * IN + N * N + HID * IN + N * HID) + 4 * (N * HID + N) + 4 * (N * IN + N * N)

F32 = mybir.dt.float32
BF16 = mybir.dt.bfloat16
U32 = mybir.dt.uint32
U8 = mybir.dt.uint8
E4M3 = mybir.dt.float8_e4m3fn_x4
E5M2 = mybir.dt.float8_e5m2_x4
ALU = mybir.AluOpType
ACT = mybir.ActivationFunctionType
AX = mybir.AxisListType


GADD = (0, 1, 2, 3, 4, 5, 6, 7, 8, 9, 10, 11, 12, 13, 14, 15)
VEC = {"cp2": ((1,), (8,),), "cpd": ((0,), (6,),), "act": ((5, 0), (6, 1),), "o1_c": ((0, 2), (1, 2), (2, 2), (4, 0), (7, 0), (7, 1), (6, 1), (9, 0), (11, 0), (11, 2), (10, 2),), "mxo_c": ((1, 3), (1, 0), (2, 3), (2, 2), (2, 0),)}
SCA = {"a_prep_copy": ((2,), (5,), (6,),), "w_copy": ((1,),)}
GPS = {}
ORDER = [
    ("load_slot", (1,)),
    ("identity", ()),
    ("load_g", (0,)),
    ("load_slot", (0,)),
    ("mask", (1,)),
    ("tr2", (1,)),
    ("load_w", (1,)),
    ("w_copy", (1,)),
    ("mask", (0,)),
    ("load_w", (0,)),
    ("cp2", (1,)),
    ("load_x", (0,)),
    ("load_d", ()),
    ("load_g", (2,)),
    ("tr2", (0,)),
    ("load_slot", (2,)),
    ("qz2", (1,)),
    ("w_copy", (0,)),
    ("x_half", (0,)),
    ("x_half", (1,)),
    ("load_slot", (3,)),
    ("w_quant", (1,)),
    ("w_quant", (0,)),
    ("cp2", (0,)),
    ("qz2", (0,)),
    ("mxd", (0,)),
    ("mxd", (1,)),
    ("load_g", (4,)),
    ("mask", (2,)),
    ("mask", (3,)),
    ("x_copy", (1,)),
    ("load_slot", (4,)),
    ("cpd", (0,)),
    ("load_slot", (5,)),
    ("tr2", (2,)),
    ("tr2", (3,)),
    ("tr1", (0,)),
    ("cpd", (1,)),
    ("cp2", (2,)),
    ("tr1", (1,)),
    ("qz2", (2,)),
    ("x_copy", (0,)),
    ("load_x", (2,)),
    ("mxd", (2,)),
    ("mask", (4,)),
    ("cp2", (3,)),
    ("tr2", (4,)),
    ("qz2", (3,)),
    ("cp1", (1,)),
    ("mh_step", ()),
    ("mask", (5,)),
    ("mxd", (3,)),
    ("load_slot", (6,)),
    ("x_quant", (0,)),
    ("load_g", (6,)),
    ("cpd", (2,)),
    ("tr1", (2,)),
    ("cp2", (4,)),
    ("qz2", (4,)),
    ("load_x", (1,)),
    ("tr2", (5,)),
    ("x_half", (5,)),
    ("cpd", (3,)),
    ("tr1", (3,)),
    ("x_half", (4,)),
    ("n_prep_copy", (0,)),
    ("load_d2", ()),
    ("load_slot", (7,)),
    ("cp2", (5,)),
    ("mxd", (4,)),
    ("x_half", (2,)),
    ("qz2", (5,)),
    ("cp1", (3,)),
    ("x_copy", (4,)),
    ("mask", (6,)),
    ("x_copy", (5,)),
    ("qz1", (0,)),
    ("x_quant", (2,)),
    ("cpd", (4,)),
    ("tr2", (6,)),
    ("x_half", (3,)),
    ("load_g", (8,)),
    ("front", (1,)),
    ("mask", (7,)),
    ("x_copy", (2,)),
    ("mxd", (5,)),
    ("front", (0,)),
    ("cp2", (6,)),
    ("x_copy", (3,)),
    ("act", (1, 1)),
    ("load_slot", (8,)),
    ("x_quant", (1,)),
    ("act", (1, 0)),
    ("qz2", (6,)),
    ("front", (5,)),
    ("tr2", (7,)),
    ("mask", (8,)),
    ("cpd", (5,)),
    ("front", (4,)),
    ("perm_step", ()),
    ("act", (5, 1)),
    ("cp2", (7,)),
    ("load_slot", (9,)),
    ("tr2", (8,)),
    ("act", (4, 0)),
    ("mxd", (6,)),
    ("mask", (9,)),
    ("load_adj", (0,)),
    ("tr1", (5,)),
    ("act", (0, 0)),
    ("cp2", (8,)),
    ("tr2", (9,)),
    ("act", (0, 1)),
    ("load_slot", (11,)),
    ("load_slot", (10,)),
    ("qz2", (7,)),
    ("cp2", (9,)),
    ("tr1", (4,)),
    ("cpd", (6,)),
    ("qz2", (8,)),
    ("act", (5, 0)),
    ("mxd", (7,)),
    ("act", (4, 1)),
    ("adj_t", (5,)),
    ("tr1", (6,)),
    ("front", (3,)),
    ("cpd", (7,)),
    ("adj_t", (1,)),
    ("tr1", (7,)),
    ("cp1", (5,)),
    ("front", (2,)),
    ("act", (3, 0)),
    ("qz2", (9,)),
    ("stt", (5, 1)),
    ("stt", (5, 0)),
    ("cp1", (7,)),
    ("load_g", (10,)),
    ("mxd", (8,)),
    ("stt", (1, 0)),
    ("act", (2, 0)),
    ("adj_t", (2,)),
    ("act", (2, 1)),
    ("stt", (1, 1)),
    ("qz1", (1,)),
    ("mxd", (9,)),
    ("load_adj", (1,)),
    ("cpd", (8,)),
    ("act", (3, 1)),
    ("mask", (11,)),
    ("front", (6,)),
    ("mask", (10,)),
    ("act", (6, 0)),
    ("cpd", (9,)),
    ("tr1", (8,)),
    ("front", (11,)),
    ("tr2", (11,)),
    ("adj_t", (4,)),
    ("stt", (2, 0)),
    ("gadd", (5,)),
    ("tr1", (9,)),
    ("act", (11, 1)),
    ("tr2", (10,)),
    ("adj_t", (0,)),
    ("act", (6, 1)),
    ("cp2", (11,)),
    ("act", (11, 0)),
    ("front", (7,)),
    ("load_adj", (2,)),
    ("stt", (2, 1)),
    ("cp2", (10,)),
    ("qz2", (11,)),
    ("stt", (0, 1)),
    ("adj_t", (3,)),
    ("stt", (0, 0)),
    ("front", (9,)),
    ("act", (7, 0)),
    ("act", (7, 1)),
    ("adj_t", (7,)),
    ("stt", (4, 0)),
    ("stt", (4, 1)),
    ("gadd", (1,)),
    ("cp1", (9,)),
    ("gadd", (2,)),
    ("qz2", (10,)),
    ("stt", (3, 0)),
    ("front", (8,)),
    ("mxd", (11,)),
    ("act", (9, 0)),
    ("act", (9, 1)),
    ("mxd", (10,)),
    ("stt", (3, 1)),
    ("adj_t", (6,)),
    ("stt", (7, 1)),
    ("front", (10,)),
    ("cpd", (11,)),
    ("tr1", (11,)),
    ("cpd", (10,)),
    ("act", (8, 0)),
    ("gadd", (0,)),
    ("gadd", (4,)),
    ("stt", (7, 0)),
    ("stt", (6, 0)),
    ("adj_t", (8,)),
    ("gadd", (3,)),
    ("stt", (6, 1)),
    ("act", (8, 1)),
    ("tr1", (10,)),
    ("cp1", (11,)),
    ("row_q", (0, 1)),
    ("row_q", (0, 0)),
    ("act", (10, 1)),
    ("gadd", (7,)),
    ("row_q", (0, 3)),
    ("row_q", (0, 2)),
    ("stt", (8, 1)),
    ("adj_t", (11,)),
    ("qz1", (2,)),
    ("act", (10, 0)),
    ("adj_t", (14,)),
    ("stt", (8, 0)),
    ("adj_t", (9,)),
    ("adj_t", (12,)),
    ("front", (12,)),
    ("stt", (11, 1)),
    ("row_red", (0,)),
    ("stt", (11, 0)),
    ("act", (12, 1)),
    ("adj_t", (10,)),
    ("act", (12, 0)),
    ("front", (13,)),
    ("stt", (9, 0)),
    ("front", (14,)),
    ("stt", (10, 0)),
    ("act", (13, 0)),
    ("act", (13, 1)),
    ("gadd", (8,)),
    ("gadd", (6,)),
    ("stt", (10, 1)),
    ("stt", (9, 1)),
    ("gadd", (11,)),
    ("front", (17,)),
    ("stt", (12, 1)),
    ("gadd", (10,)),
    ("front", (16,)),
    ("act", (14, 0)),
    ("act", (14, 1)),
    ("stt", (12, 0)),
    ("gadd", (9,)),
    ("stt", (14, 1)),
    ("gadd", (12,)),
    ("adj_t", (13,)),
    ("act", (17, 1)),
    ("stt", (13, 1)),
    ("act", (17, 0)),
    ("front", (15,)),
    ("row_q", (1, 1)),
    ("act", (15, 1)),
    ("row_q", (1, 2)),
    ("row_q", (1, 3)),
    ("row_q", (1, 0)),
    ("adj_t", (15,)),
    ("stt", (13, 0)),
    ("act", (15, 0)),
    ("act", (16, 1)),
    ("act", (16, 0)),
    ("row_last", (12,)),
    ("gadd", (13,)),
    ("stt", (14, 0)),
    ("gadd", (14,)),
    ("adj_t", (16,)),
    ("stt", (15, 1)),
    ("stt", (15, 0)),
    ("row_red", (1,)),
    ("stt", (16, 1)),
    ("adj_t", (17,)),
    ("stt", (16, 0)),
    ("stt", (17, 0)),
    ("row_last", (13,)),
    ("row_last", (14,)),
    ("o1_t", (0, 2)),
    ("gadd", (15,)),
    ("o1_t", (0, 0)),
    ("stt", (17, 1)),
    ("row_last", (15,)),
    ("n_prep_quant", (0,)),
    ("row_last", (16,)),
    ("col_red", ()),
    ("row_last", (17,)),
    ("a_prep_copy", (2,)),
    ("last_red", (0,)),
    ("last_red", (1,)),
    ("last_red", (3,)),
    ("o1_t", (2, 1)),
    ("last_red", (2,)),
    ("a_prep_quant", (2,)),
    ("col_mm", ()),
    ("o1_t", (1, 0)),
    ("q_add", ()),
    ("o1_t", (3, 0)),
    ("o1_t", (0, 1)),
    ("q_mul", ()),
    ("o1_c", (0, 0)),
    ("o1_t", (1, 1)),
    ("o1_store", (0, 0)),
    ("a_prep_copy", (1,)),
    ("o1_c", (0, 1)),
    ("o1_c", (0, 2)),
    ("o1_t", (4, 1)),
    ("o1_c", (1, 0)),
    ("o1_c", (1, 1)),
    ("o1_t", (1, 2)),
    ("o1_t", (2, 2)),
    ("o1_c", (3, 0)),
    ("o1_t", (3, 2)),
    ("o1_c", (1, 2)),
    ("o1_c", (3, 2)),
    ("o1_t", (3, 1)),
    ("o1_t", (5, 1)),
    ("o1_store", (0, 1)),
    ("o1_t", (4, 2)),
    ("o1_c", (3, 1)),
    ("o1_t", (4, 0)),
    ("o1_t", (2, 0)),
    ("n_prep_copy", (1,)),
    ("o1_t", (8, 0)),
    ("o1_store", (0, 2)),
    ("o1_c", (2, 1)),
    ("o1_c", (2, 2)),
    ("o1_store", (1,)),
    ("o1_c", (4, 2)),
    ("o1_store", (3,)),
    ("o1_t", (5, 2)),
    ("o1_t", (6, 1)),
    ("o1_c", (2, 0)),
    ("o1_t", (8, 1)),
    ("o1_c", (4, 1)),
    ("n_prep_copy", (2,)),
    ("o1_t", (5, 0)),
    ("o1_t", (7, 0)),
    ("o1_c", (4, 0)),
    ("a_prep_copy", (0,)),
    ("o1_t", (7, 2)),
    ("n_prep_quant", (1,)),
    ("o1_store", (2,)),
    ("a_prep_quant", (1,)),
    ("o1_c", (5, 1)),
    ("a_prep_quant", (0,)),
    ("o1_t", (6, 0)),
    ("o1_c", (5, 2)),
    ("o1_t", (7, 1)),
    ("o1_c", (5, 0)),
    ("o1_c", (7, 2)),
    ("o1_c", (7, 0)),
    ("n_prep_quant", (2,)),
    ("a_prep_copy", (5,)),
    ("o1_t", (6, 2)),
    ("o1_c", (7, 1)),
    ("o1_c", (6, 1)),
    ("o1_c", (6, 0)),
    ("mxo_mm", (0, 0)),
    ("o1_c", (6, 2)),
    ("o1_store", (4,)),
    ("o1_t", (8, 2)),
    ("o1_t", (9, 1)),
    ("o1_t", (9, 0)),
    ("a_prep_copy", (4,)),
    ("o1_c", (8, 1)),
    ("o1_c", (8, 0)),
    ("o1_t", (11, 0)),
    ("mxo_mm", (0, 1)),
    ("o1_c", (8, 2)),
    ("o1_t", (9, 2)),
    ("o1_t", (11, 1)),
    ("o1_store", (5,)),
    ("a_prep_quant", (5,)),
    ("o1_t", (11, 2)),
    ("o1_c", (9, 1)),
    ("a_prep_copy", (3,)),
    ("o1_t", (10, 1)),
    ("o1_c", (9, 0)),
    ("mxo_mm", (0, 3)),
    ("o1_store", (7,)),
    ("o1_c", (11, 0)),
    ("o1_c", (11, 2)),
    ("o1_c", (9, 2)),
    ("o1_store", (6,)),
    ("mxo_mm", (0, 2)),
    ("a_prep_quant", (4,)),
    ("o1_c", (11, 1)),
    ("mxo_c", (0, 1)),
    ("mxo_c", (0, 0)),
    ("mxo_c", (0, 3)),
    ("o1_t", (10, 2)),
    ("a_prep_quant", (3,)),
    ("a_prep_copy", (8,)),
    ("mxo_c", (0, 2)),
    ("a_prep_copy", (6,)),
    ("a_prep_copy", (7,)),
    ("o1_t", (10, 0)),
    ("mxo_mm", (1, 3)),
    ("o1_store", (8,)),
    ("mxo_mm", (1, 0)),
    ("o1_store", (11,)),
    ("o1_c", (10, 0)),
    ("mxo_mm", (1, 2)),
    ("o1_c", (10, 2)),
    ("o1_c", (10, 1)),
    ("a_prep_quant", (7,)),
    ("a_prep_quant", (6,)),
    ("o1_store", (9,)),
    ("mxo_c", (1, 2)),
    ("o0_store", (0,)),
    ("mxo_mm", (1, 1)),
    ("a_prep_quant", (8,)),
    ("mxo_mm", (2, 1)),
    ("mxo_c", (1, 3)),
    ("mxo_c", (1, 1)),
    ("mxo_mm", (2, 3)),
    ("mxo_mm", (2, 2)),
    ("mxo_c", (1, 0)),
    ("mxo_c", (2, 1)),
    ("mxo_c", (2, 3)),
    ("mxo_c", (2, 2)),
    ("mxo_mm", (2, 0)),
    ("o1_store", (10,)),
    ("mxo_c", (2, 0)),
    ("o0_store", (1,)),
    ("o0_store", (2,))
]


def tile_simplegcn_pa_v_kernel(tc, x, adj, W1, b1, z, rdeg, grad_out, out_0, out_1):
    nc = tc.nc
    x_v = x.rearrange("(b p e) f -> p b e f", b=B, e=E)
    adj_v = adj.rearrange("(g p s) w -> p g s w", g=G, s=S)
    w1_v = W1.rearrange("(c p j) f -> p c j f", c=2, j=4)
    z_v = z.rearrange("(g p s) k -> p g s k", g=G, s=S)
    go_v = grad_out.rearrange("(g p s) k -> p g s k", g=G, s=S)
    d_v = rdeg.rearrange("(g p s) -> p g s", g=G, s=S)
    d2_v = rdeg.rearrange("(b p e) -> p b e", b=B, e=E)
    o0_v = out_0.rearrange("(b p e) f -> p b e f", b=B, e=E)
    o1_v = out_1.rearrange("(g p s) w -> p g s w", g=G, s=S)
    NZ = 3
    NS = G * S
    NF = G * B

    with ExitStack() as ctx:
        keep = ctx.enter_context(tc.tile_pool(name="keep", bufs=1))
        over = ctx.enter_context(tc.tile_pool(name="over", bufs=1))
        psum = ctx.enter_context(tc.psum_pool(name="psum", bufs=1))
        ctx.enter_context(tc.manual_schedule())

        def sb(name, cols, dtype, offset=None):
            if offset is None:
                return keep.tile([P] + cols, dtype, name=name, align_bytes=64)
            return over.tile([P] + cols, dtype, name=name, align_bytes=64, offset=offset)

        ident = sb("ident", [P], F32)
        d_sb = sb("d_sb", [NS], F32)
        d2_sb = sb("d2_sb", [B * E], F32)
        mh = sb("mh", [NS], F32)
        csum = sb("csum", [2, G * E], F32)
        cacc = sb("cacc", [2, G, E, G], F32)
        rsum = sb("rsum", [NS], F32)
        junk = sb("junk", [P], F32)
        q_sb = sb("q_sb", [NS], F32)
        adj_sb = sb("adj_sb", [G, S, N], BF16)
        st = [[sb(f"st{g}{b}", [E, W], F32) for b in range(B)] for g in range(G)]
        dz1 = [sb(f"dz1_{g}", [S, IN], BF16) for g in range(G)]
        w_codes = sb("w_codes", [2 * IN], U32)
        w_scales = sb("w_scales", [2 * IN], U8)
        x_codes = [sb(f"x_codes{i}", [W], U32) for i in range(3)]
        x_scales = [sb(f"x_scales{i}", [W], U8) for i in range(3)]
        f_codes = [sb(f"f_codes{i}", [W], U32) for i in range(2)]
        f_scales = [sb(f"f_scales{i}", [W], U8) for i in range(2)]
        buf4 = [sb(f"buf4_{i}", [HID], F32) for i in range(NZ)]
        d1t = sb("d1t", [S * IN], BF16)

        wil = [sb(f"wil{i}", [4 * IN], BF16, 4096 * i) for i in range(2)]
        RX = 8192
        xraw = sb("xraw", [B, E, IN], BF16, RX)
        wraw = sb("wraw", [2, 4, IN], BF16, RX + 12288)
        xt = [sb(f"xt{i}", [4 * IN], BF16, RX + 20480 + 4096 * i) for i in range(2)]
        nq = [sb(f"nq{g}", [W], U32, RX + 12288 + 2048 * g) for g in range(G)]
        nqs = [sb(f"nqs{g}", [W], U8, RX + 18432 + 512 * g) for g in range(G)]
        aq = [[sb(f"aq{g}{h}", [W], U32, RX + 2048 * (3 * g + h) + (8192 if 3 * g + h >= 6 else 0)) for h in range(G)] for g in range(G)]
        aqs = [[sb(f"aqs{g}{h}", [W], U8, RX + 26624 + 512 * (3 * g + h)) for h in range(G)] for g in range(G)]
        RB = RX + 31232
        T2N = 16
        t2 = [sb(f"t2_{i}", [W], F32, RB + 2048 * i if i < 12 else RX + 2048 * (i - 12)) for i in range(T2N)]
        ot = [sb(f"ot{i}", [N], F32, RB + 6144 * i) for i in range(4)]
        RC = RB + 24576
        gt = [sb(f"gt{i}", [2, HID], BF16, RC + 4096 * i) for i in range(2)]
        dz2 = [sb(f"dz2_{i}", [HID], BF16, RC + 8192 + 2048 * i) for i in range(2)]
        d2t = [sb(f"d2t{i}", [HID], BF16, RC + 12288 + 2048 * i) for i in range(2)]
        d2q = [sb(f"d2q{i}", [2 * P], U32, RC + 16384 + 1024 * i) for i in range(2)]
        d2s = [sb(f"d2s{i}", [2 * P], U8, RC + 18432 + 256 * i) for i in range(2)]
        o0 = [sb(f"o0_{i}", [S, IN], F32, RC + 8192 * i) for i in range(2)]

        perm = gt[0][:].rearrange("p a k -> p (a k)").bitcast(F32)[:, :512].rearrange("p (c r k) -> p c r k", c=2, r=2)
        bank = [psum.tile([P, W], F32, name=f"bank{i}") for i in range(8)]
        free = list(bank)
        held = {}
        reads = {}

        def take(key, readers):
            if key not in held:
                held[key] = free[0]
                reads[key] = readers
                free.remove(held[key])
            return held[key]

        def last(key):
            b = held[key]
            reads[key] -= 1
            if reads[key] == 0:
                free.append(b)
            return b

        def move(name, key, out, in_, scale=None):
            if key in VEC.get(name, ()):
                if scale is None:
                    nc.vector.tensor_copy(out=out, in_=in_)
                else:
                    nc.vector.tensor_scalar(out=out, in0=in_, scalar1=scale, scalar2=None, op0=ALU.mult)
            elif scale is None:
                nc.scalar.copy(out=out, in_=in_)
            else:
                nc.scalar.activation(out=out, in_=in_, func=ACT.Copy, scale=scale)

        def weave(name, key, out, in_):
            if (key,) in GPS.get(name, ()):
                nc.gpsimd.tensor_scalar(out=out, in0=in_, scalar1=1.0, scalar2=1.0, op0=ALU.mult, op1=ALU.mult)
            elif (key,) in SCA.get(name, ()):
                nc.scalar.copy(out=out, in_=in_)
            else:
                nc.vector.tensor_copy(out=out, in_=in_)

        def load_d():
            nc.sync.dma_start(out=d_sb[:].rearrange("p (g s) -> p g s", g=G), in_=d_v)

        def load_d2():
            nc.sync.dma_start(out=d2_sb[:].rearrange("p (b e) -> p b e", b=B), in_=d2_v)

        def identity():
            make_identity(nc, ident[:])

        def load_slot(n):
            nc.sync.dma_start(out=buf4[n % NZ][:], in_=z_v[:, n // S, n % S, :])

        def load_g(n):
            nc.sync.dma_start(out=gt[n // 2 % 2][:], in_=go_v[:, n // S, n % S:n % S + 2, :])

        def load_w(c):
            nc.sync.dma_start(out=wraw[:, c, :, :], in_=w1_v[:, c, :, :])

        def load_adj(g):
            for s in (0, 2):
                nc.sync.dma_start(out=adj_sb[:, g, s:s + 2, :], in_=adj_v[:, g, s:s + 2, :])

        def load_x(i):
            nc.sync.dma_start(out=xraw[:, 2 * i:2 * i + 2, :, :], in_=x_v[:, 2 * i:2 * i + 2, :, :])

        def w_copy(c):
            weave("w_copy", c, wil[c][:].rearrange("p (f j) -> p f j", j=4), wraw[:, c, :, :].rearrange("p j f -> p f j"))

        def w_quant(c):
            nc.vector.quantize_mx(out=w_codes[:, c * IN:(c + 1) * IN].bitcast(E4M3), scales=w_scales[:, c * IN:(c + 1) * IN], in_=wil[c][:])

        def x_half(b):
            bk = take(("x", b), 1)
            ps = bk[:].rearrange("p (e u t) -> p e u t", e=2, u=2)
            for e in range(2):
                words = xraw[:, b, e, :].bitcast(F32)
                for u in range(2):
                    nc.tensor.transpose(ps[:, e, u, :], words[:, u::2], ident[:])

        def x_copy(b):
            ps = last(("x", b))[:].rearrange("p (e u t) -> p e u t", e=2, u=2)
            dst = xt[b // 2 % 2][:, (b % 2) * 1024:(b % 2 + 1) * 1024].bitcast(F32).rearrange("p (e t u) -> p e t u", e=2, u=2)
            move("x_copy", (b,), dst, ps.rearrange("p e u t -> p e t u"))

        def x_quant(i):
            nc.vector.quantize_mx(out=x_codes[i][:].bitcast(E4M3), scales=x_scales[i][:], in_=xt[i % 2][:])

        def mask(n):
            if not 0 <= n < NS:
                return
            nc.vector.scalar_tensor_tensor(out=dz2[n % 2][:], in0=buf4[n % NZ][:], scalar=0.0, in1=gt[n // 2 % 2][:, n % 2, :], op0=ALU.is_gt, op1=ALU.mult)

        def tr2(n):
            if not 0 <= n < NS:
                return
            words = dz2[n % 2][:].bitcast(F32)
            ps = take(("t2", n), 1)[:].rearrange("p (c u t) -> p c u t", c=2, u=2)
            for c in range(2):
                for u in range(2):
                    nc.tensor.transpose(ps[:, c, u, :], words[:, c * 256 + u:(c + 1) * 256:2], ident[:])

        def cp2(n):
            ps = last(("t2", n))[:].rearrange("p (c u t) -> p c u t", c=2, u=2)
            move("cp2", (n,), d2t[n % 2][:].bitcast(F32).rearrange("p (c t u) -> p c t u", c=2, u=2), ps.rearrange("p c u t -> p c t u"))

        def qz2(n):
            if not 0 <= n < NS:
                return
            nc.vector.quantize_mx(out=d2q[n % 2][:].bitcast(E5M2), scales=d2s[n % 2][:], in_=d2t[n % 2][:])

        def mxd(n):
            if not 0 <= n < NS:
                return
            bk = take(("da", n), 1)
            for c in range(2):
                nc.tensor.matmul_mx(out=bk[:], lhsT=d2q[n % 2][:, c * P:(c + 1) * P].bitcast(E5M2), lhsT_scale=d2s[n % 2][:, c * P:(c + 1) * P],
                                    rhs=w_codes[:, c * IN:(c + 1) * IN].bitcast(E4M3), rhs_scale=w_scales[:, c * IN:(c + 1) * IN],
                                    start=(c == 0), stop=(c == 1))

        def cpd(n):
            move("cpd", (n,), dz1[n // S][:, n % S, :].rearrange("p (u q e) -> p u q e", u=2, e=2),
                 last(("da", n))[:].rearrange("p (q u e) -> p u q e", u=2, e=2), scale=d_sb[:, n:n + 1])

        def tr1(n):
            if not 0 <= n < NS:
                return
            words = dz1[n // S][:, n % S, :].bitcast(F32)
            ps = take(("t1", n // 2), 1)[:, (n % 2) * 256:(n % 2 + 1) * 256].rearrange("p (u t) -> p u t", u=2)
            for u in range(2):
                nc.tensor.transpose(ps[:, u, :], words[:, u * P:(u + 1) * P], ident[:])

        def cp1(n):
            ps = last(("t1", n // 2))[:].rearrange("p (s u t) -> p s u t", s=2, u=2)
            dst = d1t[:, (n % S - 1) * IN:(n % S + 1) * IN].bitcast(F32).rearrange("p (s t u) -> p s t u", s=2, u=2)
            move("cp1", (n,), dst, ps.rearrange("p s u t -> p s t u"))

        def qz1(g):
            nc.vector.quantize_mx(out=f_codes[g % 2][:].bitcast(E5M2), scales=f_scales[g % 2][:], in_=d1t[:])

        def front(i):
            if not 0 <= i < NF:
                return
            g, b = i // B, i % B
            for e in range(E):
                c0 = ((b % 2) * E + e) * P
                nc.tensor.matmul_mx(out=take(("pt", i, e), 1)[:], lhsT=x_codes[b // 2][:, c0:c0 + P].bitcast(E4M3), lhsT_scale=x_scales[b // 2][:, c0:c0 + P],
                                    rhs=f_codes[g % 2][:].bitcast(E5M2), rhs_scale=f_scales[g % 2][:], start=True, stop=True)

        def act(i, e):
            g, b = i // B, i % B
            move("act", (i, e), st[g][b][:, e, :], last(("pt", i, e))[:], scale=d2_sb[:, b * E + e:b * E + e + 1])

        def adj_t(i):
            if not 0 <= i < NF:
                return
            g, b = i // B, i % B
            for s in range(S):
                words = adj_sb[:, g, s, b * 256:(b + 1) * 256].bitcast(F32)
                nc.tensor.transpose(take(("at", i), 2)[:, s * P:(s + 1) * P], words, ident[:])


        def t2_of(i, e):
            return t2[(2 * i + e) % T2N][:]

        def stt(i, e):
            g, b = i // B, i % B
            at = last(("at", i))[:].bitcast(BF16).rearrange("p (t e) -> p e t", e=E)
            nc.vector.scalar_tensor_tensor(out=t2_of(i, e), in0=at[:, e, :], scalar=1.0, in1=st[g][b][:, e, :],
                                           op0=ALU.mult, op1=ALU.mult, accum_out=cacc[:, b % 2, b // 2, e, g:g + 1])

        def gadd(i):
            nc.gpsimd.tensor_tensor(out=t2_of(i, 0), in0=t2_of(i, 0), in1=t2_of(i, 1), op=ALU.add)

        def pend(i):
            return [t2_of(i, 0)] if i in GADD else [t2_of(i, 0), t2_of(i, 1)]

        def row_q(g, s):
            tiles = [t for i in range(g * B, (g + 1) * B) for t in pend(i)]
            for j, t in enumerate(tiles):
                nc.tensor.matmul(out=take(("row", g), S)[:, s * P:(s + 1) * P], lhsT=t[:, s * P:(s + 1) * P], rhs=ident[:], start=(j == 0), stop=(j == len(tiles) - 1), is_transpose=True)

        def row_red(g):
            for s in range(S):
                nc.scalar.activation(out=junk[:], in_=last(("row", g))[:, s * P:(s + 1) * P], func=ACT.Copy, accum_out=rsum[:, g * S + s:g * S + s + 1])

        def row_last(i):
            for j, t in enumerate(pend(i)):
                for s in range(S):
                    nc.tensor.matmul(out=take(("last", s), 1)[:, :P], lhsT=t[:, s * P:(s + 1) * P], rhs=ident[:], start=(i % B == 0 and j == 0), stop=(i == NF - 1 and j == len(pend(i)) - 1), is_transpose=True)

        def n_prep_copy(g):
            o, i = wil[g % 2][:].rearrange("p (f s) -> p f s", s=S), dz1[g][:].rearrange("p s f -> p f s")
            weave("n_prep_copy", g, o, i)

        def n_prep_quant(g):
            t = wil[g % 2][:]
            nc.vector.quantize_mx(out=nq[g][:].bitcast(E5M2), scales=nqs[g][:], in_=t)

        def a_buf(i):
            return buf4[i % NZ][:].bitcast(BF16)

        def a_prep_copy(i):
            g, h = i % G, i // G
            o, i_ = a_buf(i).rearrange("p (e k s) -> p e k s", e=E, s=S), adj_sb[:, g, :, h * W:(h + 1) * W].rearrange("p s (k e) -> p e k s", e=E)
            weave("a_prep_copy", i, o, i_)

        def a_prep_quant(i):
            g, h = i % G, i // G
            nc.vector.quantize_mx(out=aq[g][h][:].bitcast(E4M3), scales=aqs[g][h][:], in_=a_buf(i))

        def mxo_mm(h, s):
            bk = take(("o0", h, s), 1)
            for g in range(G):
                nc.tensor.matmul_mx(out=bk[:], lhsT=aq[g][h][:, s * P:(s + 1) * P].bitcast(E4M3), lhsT_scale=aqs[g][h][:, s * P:(s + 1) * P],
                                    rhs=nq[g][:].bitcast(E5M2), rhs_scale=nqs[g][:], start=(g == 0), stop=(g == G - 1))

        def mxo_c(h, s):
            o = o0[h % 2][:, E * (s % 2) + s // 2, :].rearrange("p (q u e) -> p q u e", u=2, e=2)
            i = last(("o0", h, s))[:].rearrange("p (u q e) -> p q u e", u=2, e=2)
            b, e = 2 * h + s % 2, s // 2
            move("mxo_c", (h, s), o, i, scale=d2_sb[:, b * E + e:b * E + e + 1])

        def o0_store(h):
            nc.sync.dma_start(out=o0_v[:, 2 * h:2 * h + 2, :, :], in_=o0[h % 2][:].rearrange("p (b e) f -> p b e f", b=2))

        def o1_t(n, h):
            g, s = n // S, n % S
            for k in range(4):
                nc.tensor.transpose(take(("o1", n, h), 1)[:, k * P:(k + 1) * P], st[g][2 * h + k // 2][:, k % 2, s * P:(s + 1) * P], ident[:])

        def o1_c(n, h):
            o = ot[n % 4][:, h * W:(h + 1) * W].rearrange("p (c b a) -> p c b a", c=2, a=2)
            i = last(("o1", n, h))[:].rearrange("p (c a b) -> p c b a", c=2, a=2)
            if (n, h) in VEC.get("o1_c", ()):
                nc.vector.tensor_scalar(out=o, in0=i, scalar1=q_sb[:, n:n + 1], scalar2=None, op0=ALU.add)
            else:
                nc.scalar.activation(out=o, in_=i, func=ACT.Identity, bias=q_sb[:, n:n + 1])

        def o1_store(n, h=None):
            lo, hi = (0, N) if h is None else (h * W, (h + 1) * W)
            nc.sync.dma_start(out=o1_v[:, n // S, n % S, lo:hi], in_=ot[n % 4][:, lo:hi])

        def col_red():
            nc.vector.reduce_sum(out=csum[:].rearrange("p c k -> p (c k)"), in_=cacc[:].rearrange("p c b e g -> p (c b e) g"), axis=AX.X)

        def col_mm():
            bk = take(("col",), 1)
            for r in range(2):
                for c in range(2):
                    nc.tensor.matmul(out=bk[:, r * 6:(r + 1) * 6], lhsT=perm[:, c, r, :], rhs=csum[:, c, :], start=(c == 0), stop=(c == 1))

        def last_red(s):
            o = rsum[:, (G - 1) * S + s:(G - 1) * S + s + 1]
            bk = last(("last", s))
            if s % 2:
                nc.scalar.activation(out=junk[:], in_=bk[:, :P], func=ACT.Copy, accum_out=o)
            else:
                nc.vector.reduce_sum(out=o, in_=bk[:, :P], axis=AX.X)

        def q_add():
            nc.vector.tensor_tensor(out=q_sb[:].rearrange("p (g r e) -> p g r e", g=G, r=2), in0=last(("col",))[:, 0:12].rearrange("p (r g e) -> p g r e", r=2, g=G),
                                    in1=rsum[:].rearrange("p (g r e) -> p g r e", g=G, r=2), op=ALU.add)

        def q_mul():
            nc.vector.tensor_tensor(out=q_sb[:], in0=q_sb[:], in1=mh[:], op=ALU.mult)

        def perm_step():
            nc.gpsimd.memset(perm, 0.0)
            for c in range(2):
                for r in range(2):
                    nc.gpsimd.tensor_copy(out=perm[:, c, r, 64 * c:64 * c + 64], in_=ident[:, r::2])

        def mh_step():
            nc.vector.scalar_tensor_tensor(out=mh[:], in0=d_sb[:], scalar=-0.5, in1=d_sb[:], op0=ALU.mult, op1=ALU.mult)


        fns = {"load_d": load_d, "load_d2": load_d2, "identity": identity, "load_w": load_w, "w_copy": w_copy, "w_quant": w_quant, "load_x": load_x, "x_quant": x_quant, "x_half": x_half, "x_copy": x_copy,
               "load_slot": load_slot, "load_g": load_g, "cp1": cp1, "mask": mask, "tr2": tr2, "cp2": cp2, "qz2": qz2, "mxd": mxd, "cpd": cpd, "tr1": tr1,
               "qz1": qz1, "mh_step": mh_step, "perm_step": perm_step, "load_adj": load_adj, "n_prep_copy": n_prep_copy, "n_prep_quant": n_prep_quant,
               "adj_t": adj_t, "front": front, "act": act, "stt": stt, "row_q": row_q, "gadd": gadd, "row_red": row_red, "row_last": row_last,
               "col_red": col_red, "col_mm": col_mm, "last_red": last_red, "q_add": q_add, "q_mul": q_mul, "a_prep_copy": a_prep_copy,
               "a_prep_quant": a_prep_quant, "o1_t": o1_t, "o1_c": o1_c, "o1_store": o1_store, "mxo_mm": mxo_mm, "mxo_c": mxo_c, "o0_store": o0_store}
        for name, args in ORDER:
            fns[name](*args)
